import numpy as np
import ml_dtypes


def mxq(x, axis, fmt="e4m3"):
    dtype, down = {"e4m3": (ml_dtypes.float8_e4m3fn, 7), "e5m2": (ml_dtypes.float8_e5m2, 14)}[fmt]
    v = np.moveaxis(np.asarray(x, np.float32).astype(ml_dtypes.bfloat16).astype(np.float64), axis, -1)
    blocks = v.reshape(v.shape[:-1] + (-1, 32))
    amax = np.abs(blocks).max(-1, keepdims=True)
    byte = np.maximum(np.where(amax > 0, np.frexp(amax)[1] - 1 + 127, 0) - down, 1)
    scale = np.exp2(byte - 127.0)
    codes = (blocks / scale).astype(np.float32).astype(dtype).astype(np.float64)
    return np.moveaxis((codes * scale).reshape(v.shape), -1, axis)


WIDE = False


def mx_kscale(k):
    if not WIDE:
        return np.ones(k)
    levels = np.array([10, -10, 5, -5, 0])
    if k % 512:
        return np.exp2(np.random.permutation(np.resize(levels, k // 32))).repeat(32)
    a = np.empty((k // 512, 16))
    for p in range(k // 512):
        a[p, :8] = np.random.permutation(np.resize(levels, 8))
        for g in range(8):
            far = levels[np.abs(levels - a[p, g]) >= 10]
            a[p, g + 8] = far[np.random.randint(len(far))]
    return np.exp2(a.ravel()).repeat(32)


BF16 = ml_dtypes.bfloat16


def bf(x):
    return np.asarray(x, np.float32).astype(BF16)


def f64(x):
    return np.asarray(x).astype(np.float64)


E2M1 = np.array([0.0, 0.5, 1.0, 1.5, 2.0, 3.0, 4.0, 6.0, -0.0, -0.5, -1.0, -1.5, -2.0, -3.0, -4.0, -6.0])


def pack_weight(w, fmt):
    k, n = w.shape
    w = f64(bf(w)).reshape(k // 32, 32, n)
    amax = np.abs(w).max(1)
    if fmt == "e4m3":
        byte = np.frexp(amax)[1] - 1 + 127 - 7
    else:
        mant, ex = np.frexp(amax / 6.0)
        byte = np.where(mant > 0.5, ex, ex - 1) + 127
    byte = np.clip(np.where(amax > 0, byte, 1), 1, 254)
    scaled = (w * np.exp2(127.0 - byte)[:, None, :]).reshape(k, n).astype(np.float32)
    by_word = np.ascontiguousarray(scaled.reshape(k // 512, 128, 4, n).transpose(0, 1, 3, 2))
    if fmt == "e4m3":
        words = by_word.astype(ml_dtypes.float8_e4m3fn).view(np.uint8)
    else:
        c = by_word.astype(ml_dtypes.float4_e2m1fn).view(np.uint8) & 0xF
        words = c[..., 0::2] | (c[..., 1::2] << 4)
    return np.ascontiguousarray(words), np.ascontiguousarray(byte.astype(np.uint8).reshape(k // 512, 16, n))


def unpack_weight(words, scales, fmt):
    g, p, n, _ = words.shape
    if fmt == "e4m3":
        vals = np.ascontiguousarray(words).view(ml_dtypes.float8_e4m3fn).astype(np.float64)
    else:
        nib = np.empty((g, p, n, 4), np.uint8)
        nib[..., 0::2] = words & 0xF
        nib[..., 1::2] = words >> 4
        vals = E2M1[nib]
    vals = vals * np.repeat(np.exp2(scales.astype(np.float64) - 127.0), 8, axis=1)[..., None]
    return vals.transpose(0, 1, 3, 2).reshape(g * 512, n)


B, I, H, ORDER = 8192, 512, 256, 2
OH = ORDER * H


def sigmoid(v):
    return 1.0 / (1.0 + np.exp(-v))


def draw0():
    s, t = mx_kscale(I), mx_kscale(OH)
    x = bf(np.random.standard_normal((B, I)) * s)
    me_output = bf(np.random.standard_normal((B, OH)) * t)
    W_memi_words, W_memi_scales = pack_weight(np.random.standard_normal((I, OH)) * 0.7 / np.sqrt(I) / s[:, None], "e4m3")
    W_memh_words, W_memh_scales = pack_weight(np.random.standard_normal((OH, OH)) * 0.7 / np.sqrt(OH) / t[:, None], "e4m3")
    W_memt_words, W_memt_scales = pack_weight(np.random.standard_normal((OH, H)) * 1.0 / np.sqrt(OH) / t[:, None], "e4m3")
    return {"x": x,
            "me_output": me_output,
            "W_memi_words": W_memi_words,
            "W_memi_scales": W_memi_scales,
            "W_memh_words": W_memh_words,
            "W_memh_scales": W_memh_scales,
            "W_memt_words": W_memt_words,
            "W_memt_scales": W_memt_scales,
            "mem_bias": bf(np.random.standard_normal(OH) * 0.3)}


def core(x, me_output, W_memi_words, W_memi_scales, W_memh_words, W_memh_scales, W_memt_words, W_memt_scales, mem_bias):
    me = f64(me_output)
    mg = ((mxq(f64(x), 1, "e4m3") @ unpack_weight(W_memi_words, W_memi_scales, "e4m3"))
          + (mxq(me, 1, "e4m3") @ unpack_weight(W_memh_words, W_memh_scales, "e4m3"))
          + f64(mem_bias))
    gated = sigmoid(mg) * me
    return mxq(gated, 1, "e4m3") @ unpack_weight(W_memt_words, W_memt_scales, "e4m3")


def e4m3fn_bytes(y):
    return np.clip(np.asarray(y, np.float64), -448.0, 448.0).astype(np.float32).astype(ml_dtypes.float8_e4m3fn).view(np.uint8)


def e4m3fn_values(b):
    return np.asarray(b, np.uint8).view(ml_dtypes.float8_e4m3fn).astype(np.float64)


def setup_inputs():
    d = draw0()
    x0 = np.asarray(d['x']).astype(np.float64)
    s = (np.max(np.abs(x0), axis=(0,), keepdims=True) / 448.0).astype(np.float32)
    out = {}
    for k, v in d.items():
        if k == 'x':
            out['x_bytes'] = e4m3fn_bytes(x0 / s.astype(np.float64))
            out['x_scale'] = s
        else:
            out[k] = v
    return out


def reference(x_bytes, x_scale, me_output, W_memi_words, W_memi_scales, W_memh_words, W_memh_scales, W_memt_words, W_memt_scales, mem_bias):
    return core(e4m3fn_values(x_bytes) * x_scale.astype(np.float64), me_output, W_memi_words, W_memi_scales, W_memh_words, W_memh_scales, W_memt_words, W_memt_scales, mem_bias)

@@ -1,0 +1,261 @@
+from contextlib import ExitStack
+
+import concourse.mybir as mybir
+from concourse.masks import make_identity
+
+TOKENS, K, CH, N_OUT = 8192, 512, 512, 256
+FLOPS = 2 * TOKENS * (K * CH + CH * CH + CH * N_OUT)
+
+F32 = mybir.dt.float32
+BF16 = mybir.dt.bfloat16
+I32 = mybir.dt.int32
+U32 = mybir.dt.uint32
+U8 = mybir.dt.uint8
+FP8 = mybir.dt.float8_e4m3fn
+FP8X4 = mybir.dt.float8_e4m3fn_x4
+MULT = mybir.AluOpType.mult
+ACT = mybir.ActivationFunctionType
+
+P = 128
+PACK = 4
+TILES = TOKENS // P
+G = 4
+GROUPS = TILES // G
+GT = G * P
+AHEAD = 4
+
+
+def tile_lstmcell_pa_t_w8_kernel(
+    tc, x_bytes, x_scale, me_output, wi_words, wi_scales, wh_words, wh_scales, wt_words, wt_scales, mem_bias, out
+):
+    nc = tc.nc
+    x_hbm = x_bytes.rearrange("(p i) k -> p i k", i=TILES)
+    me_hbm = me_output.rearrange("(p i) k -> p i k", i=TILES)
+    out_hbm = out.rearrange("(p i) n -> p i n", i=TILES)
+
+    with ExitStack() as ctx:
+        keep = ctx.enter_context(tc.tile_pool(name="keep", bufs=1))
+        xin = ctx.enter_context(tc.tile_pool(name="xin", bufs=6))
+        mein = ctx.enter_context(tc.tile_pool(name="mein", bufs=7))
+        work = ctx.enter_context(tc.tile_pool(name="work", bufs=3))
+        turnp = ctx.enter_context(tc.tile_pool(name="turnp", bufs=5))
+        outp = ctx.enter_context(tc.tile_pool(name="outp", bufs=3))
+        ptp = ctx.enter_context(tc.psum_pool(name="ptp", bufs=3))
+        pmg = ctx.enter_context(tc.psum_pool(name="pmg", bufs=3))
+        pout = ctx.enter_context(tc.psum_pool(name="pout", bufs=2))
+        ctx.enter_context(tc.manual_schedule())
+
+        ident = keep.tile([P, P], F32, name="ident")
+        s_col = keep.tile([P, PACK], F32, name="s_col")
+        scale = keep.tile([P, G * K], F32, name="scale")
+        bias_bf = keep.tile([P, PACK], BF16, name="bias_bf")
+        bias = keep.tile([P, PACK], F32, name="bias")
+        warm = keep.tile([P, 1], F32, name="warm")
+        wi_raw = keep.tile([P, CH], U32, name="wi_raw", align_bytes=64)
+        wh_raw = keep.tile([P, CH], U32, name="wh_raw", align_bytes=64)
+        wi = keep.tile([P, CH], U32, name="wi", align_bytes=64)
+        wh = keep.tile([P, CH], U32, name="wh", align_bytes=64)
+        wt = keep.tile([P, N_OUT], U32, name="wt", align_bytes=64)
+        ws_raw = keep.tile([P, CH], U8, name="ws_raw", align_bytes=64)
+        ws = keep.tile([P, CH], U8, name="ws", align_bytes=64)
+        wts = keep.tile([P, N_OUT], U8, name="wts", align_bytes=64)
+
+        xb, me, xw, turned, q = {}, {}, {}, {}, {}
+        sig, gated, gq = {}, {}, {}
+
+        def load_x(g):
+            t = xin.tile([P, G, K], U8, name="xb")
+            nc.sync.dma_start(out=t[:], in_=x_hbm[:, g * G : (g + 1) * G, :])
+            xb[g] = t
+
+        def load_me(g):
+            t = mein.tile([P, G, K], BF16, name="me")
+            nc.sync.dma_start(out=t[:], in_=me_hbm[:, g * G : (g + 1) * G, :])
+            me[g] = t
+
+        def load(g):
+            load_x(g)
+            load_me(g)
+
+        def widen(g):
+            t = work.tile([P, G * K], BF16, name="xw")
+            src = xb[g][:].rearrange("p i k -> p (i k)")
+            pieces = G if g == 0 else 1
+            w = G * K // pieces
+            for j in range(pieces):
+                nc.vector.tensor_tensor(
+                    out=t[:, j * w : (j + 1) * w],
+                    in0=src[:, j * w : (j + 1) * w].bitcast(FP8),
+                    in1=scale[:, 0:w],
+                    op=MULT,
+                )
+            xw[g] = t
+
+        def turn(src, dst):
+            words = src.bitcast(F32)
+            dst_w = dst.bitcast(F32).rearrange("p (i r u) -> p i r u", i=G, u=2)
+            for b in range(G // 2):
+                pt = ptp.tile([P, 2, 2, P], F32, name="pt")
+                for i in range(2):
+                    for u in range(2):
+                        base = (2 * b + i) * (K // 2)
+                        nc.tensor.transpose(pt[:, i, u, :], words[:, base + u : base + K // 2 : 2], ident[:])
+                nc.scalar.copy(out=dst_w[:, 2 * b : 2 * b + 2], in_=pt[:].rearrange("p i u r -> p i r u"))
+
+        def turn_me(g):
+            t = turnp.tile([P, 2 * GT * PACK], BF16, name="turned", align_bytes=64)
+            turned[g] = t
+            turn(me[g][:].rearrange("p i k -> p (i k)"), t[:, 0 : GT * PACK])
+
+        def turn_x(g):
+            turn(xw[g][:], turned[g][:, GT * PACK : 2 * GT * PACK])
+
+        def quant_in(g):
+            codes = work.tile([P, 2 * GT], U32, name="qc", align_bytes=64)
+            scales = work.tile([P, 2 * GT], U8, name="qs", align_bytes=64)
+            nc.vector.quantize_mx(out=codes[:].bitcast(FP8X4), scales=scales[:], in_=turned[g][:])
+            q[g] = (codes, scales)
+
+        def gates(g, ts):
+            if g not in sig:
+                s = work.tile([P, PACK, GT], F32, name="sig")
+                sig[g] = s
+            s = sig[g]
+            for t in ts:
+                cols = slice(t * P, (t + 1) * P)
+                pm = pmg.tile([P, GT], F32, name="pm")
+                nc.tensor.matmul_mx(
+                    out=pm[:], lhsT=wi[:, cols].bitcast(FP8X4), lhsT_scale=ws[:, cols],
+                    rhs=q[g][0][:, GT:].bitcast(FP8X4), rhs_scale=q[g][1][:, GT:], start=True, stop=False,
+                )
+                nc.tensor.matmul_mx(
+                    out=pm[:], lhsT=wh[:, cols].bitcast(FP8X4), lhsT_scale=ws[4:, cols],
+                    rhs=q[g][0][:, 0:GT].bitcast(FP8X4), rhs_scale=q[g][1][:, 0:GT], start=False, stop=True,
+                )
+                nc.scalar.activation(out=s[:, t, :], in_=pm[:], func=ACT.Sigmoid, bias=bias[:, t : t + 1])
+
+        def pieces_of(g):
+            return ((0, 2), (2, 3), (3, 4)) if g == GROUPS - 1 else ((0, G),)
+
+        def gate(g, pieces):
+            if g not in gated:
+                fresh = work.tile([P, GT * PACK], BF16, name="gated", align_bytes=64)
+                gated[g] = fresh
+            t = gated[g]
+            for i0, i1 in pieces:
+                rows = slice(i0 * P, i1 * P)
+                cols = slice(i0 * P * PACK, i1 * P * PACK)
+                nc.vector.tensor_tensor(
+                    out=t[:, cols].rearrange("p (c i t) -> p c t i", i=4, t=PACK),
+                    in0=sig[g][:, :, rows].rearrange("p t (c i) -> p c t i", i=4),
+                    in1=turned[g][:, cols].rearrange("p (c i t) -> p c t i", i=4, t=PACK),
+                    op=MULT,
+                )
+
+        def quant_gated(g, pieces):
+            if g not in gq:
+                codes = work.tile([P, GT], U32, name="gc", align_bytes=64)
+                scales = work.tile([P, GT], U8, name="gs", align_bytes=64)
+                gq[g] = (codes, scales)
+            codes, scales = gq[g]
+            for i0, i1 in pieces:
+                rows = slice(i0 * P, i1 * P)
+                nc.vector.quantize_mx(
+                    out=codes[:, rows].bitcast(FP8X4),
+                    scales=scales[:, rows],
+                    in_=gated[g][:, i0 * P * PACK : i1 * P * PACK],
+                )
+
+        def read_out(g):
+            o = outp.tile([P, G, N_OUT], F32, name="res")
+            for i0, i1 in pieces_of(g):
+                for b in range(i0, i1, 2):
+                    e = min(b + 2, i1)
+                    po = pout.tile([P, 2, N_OUT], F32, name="po")
+                    for i in range(b, e):
+                        cols = slice(i * P, (i + 1) * P)
+                        nc.tensor.matmul_mx(
+                            out=po[:, i - b, :], lhsT=gq[g][0][:, cols].bitcast(FP8X4), lhsT_scale=gq[g][1][:, cols],
+                            rhs=wt[:].bitcast(FP8X4), rhs_scale=wts[:], start=True, stop=True,
+                        )
+                    nc.scalar.copy(out=o[:, b:e, :], in_=po[:, 0 : e - b, :])
+                nc.sync.dma_start(out=out_hbm[:, g * G + i0 : g * G + i1, :], in_=o[:, i0:i1, :])
+
+        make_identity(nc, ident[:])
+        nc.gpsimd.memset(ws_raw[:].bitcast(I32), 0)
+        nc.gpsimd.memset(wts[:].bitcast(I32), 0)
+        nc.gpsimd.memset(warm[:], 0.0)
+        nc.scalar.activation(out=warm[:], in_=warm[:], func=ACT.Sigmoid)
+
+        nc.sync.dma_start(out=s_col[:], in_=x_scale.rearrange("o (p t) -> p (o t)", t=PACK))
+        nc.sync.dma_start(out=wi_raw[:].bitcast(I32), in_=wi_words[0].rearrange("p n t -> p (n t)").bitcast(I32))
+        nc.sync.dma_start(out=wh_raw[:].bitcast(I32), in_=wh_words[0].rearrange("p n t -> p (n t)").bitcast(I32))
+        load_x(0)
+        load_me(0)
+        load_x(1)
+        load_x(2)
+        load_me(1)
+        for h in range(4):
+            for w, hbm in enumerate((wi_scales, wh_scales)):
+                nc.sync.dma_start(
+                    out=ws_raw[32 * h + 4 * w : 32 * h + 4 * w + 4, :].bitcast(I32),
+                    in_=hbm[0, 4 * h : 4 * h + 4, :].bitcast(I32),
+                )
+        nc.sync.dma_start(out=bias_bf[:], in_=mem_bias.rearrange("(p t) -> p t", t=PACK))
+        load_me(2)
+        load_x(3)
+        load_me(3)
+        nc.sync.dma_start(out=wt[:].bitcast(I32), in_=wt_words[0].rearrange("p n t -> p (n t)").bitcast(I32))
+        for h in range(4):
+            nc.sync.dma_start(
+                out=wts[32 * h : 32 * h + 4, :].bitcast(I32), in_=wt_scales[0, 4 * h : 4 * h + 4, :].bitcast(I32)
+            )
+
+        ps = ptp.tile([P, PACK, P], F32, name="pt")
+        for t in range(PACK):
+            nc.tensor.transpose(ps[:, t, :], s_col[:, t : t + 1].to_broadcast([P, P]), ident[:])
+        for j in range(G):
+            nc.scalar.copy(
+                out=scale[:, j * K : (j + 1) * K].rearrange("p (n t) -> p n t", t=PACK),
+                in_=ps[:].rearrange("p t n -> p n t"),
+            )
+
+        for raw, dst in ((wi_raw, wi), (wh_raw, wh)):
+            nc.vector.tensor_copy(
+                out=dst[:].bitcast(I32).rearrange("p (t m) -> p t m", t=PACK),
+                in_=raw[:].bitcast(I32).rearrange("p (m t) -> p t m", t=PACK),
+            )
+
+        def permute_scales():
+            nc.vector.tensor_copy(
+                out=ws[:].rearrange("p (t m) -> p t m", t=PACK),
+                in_=ws_raw[:].rearrange("p (m t) -> p t m", t=PACK),
+            )
+
+        for s in range(GROUPS + 5):
+            if s + AHEAD < GROUPS:
+                load(s + AHEAD)
+            if 0 <= s - 2 < GROUPS:
+                quant_in(s - 2)
+            if s == 2:
+                permute_scales()
+            if s == 3:
+                nc.scalar.copy(out=bias[:], in_=bias_bf[:])
+            if 0 <= s - 4 < GROUPS:
+                gate(s - 4, pieces_of(s - 4)[0:2])
+            if 0 <= s - 3 < GROUPS:
+                gates(s - 3, (0, 1))
+            if 0 <= s - 1 < GROUPS:
+                turn_me(s - 1)
+            if 0 <= s - 3 < GROUPS:
+                gates(s - 3, (2, 3))
+            if 0 <= s - 1 < GROUPS:
+                turn_x(s - 1)
+            if s < GROUPS:
+                widen(s)
+            if 0 <= s - 4 < GROUPS:
+                quant_gated(s - 4, pieces_of(s - 4)[0:1])
+                gate(s - 4, pieces_of(s - 4)[2:])
+                quant_gated(s - 4, pieces_of(s - 4)[1:])
+            if 0 <= s - 5 < GROUPS:
+                read_out(s - 5)

@@ -22,7 +22,9 @@ TILES = TOKENS // P
 G = 4
 GROUPS = TILES // G
 GT = G * P
-AHEAD = 4
+HT = GT // 2
+AHEAD = 3
+POOL_TOKENS = 192
 
 
 def tile_lstmcell_pa_t_w8_kernel(
@@ -35,22 +37,21 @@ def tile_lstmcell_pa_t_w8_kernel(
 
     with ExitStack() as ctx:
         keep = ctx.enter_context(tc.tile_pool(name="keep", bufs=1))
-        xin = ctx.enter_context(tc.tile_pool(name="xin", bufs=6))
-        mein = ctx.enter_context(tc.tile_pool(name="mein", bufs=7))
+        xin = ctx.enter_context(tc.tile_pool(name="xin", bufs=5))
+        mein = ctx.enter_context(tc.tile_pool(name="mein", bufs=6))
         work = ctx.enter_context(tc.tile_pool(name="work", bufs=3))
+        single = ctx.enter_context(tc.tile_pool(name="single", bufs=1))
         turnp = ctx.enter_context(tc.tile_pool(name="turnp", bufs=5))
         outp = ctx.enter_context(tc.tile_pool(name="outp", bufs=3))
-        ptp = ctx.enter_context(tc.psum_pool(name="ptp", bufs=3))
+        px = ctx.enter_context(tc.psum_pool(name="px", bufs=2))
+        pmix = ctx.enter_context(tc.psum_pool(name="pmix", bufs=3))
         pmg = ctx.enter_context(tc.psum_pool(name="pmg", bufs=3))
-        pout = ctx.enter_context(tc.psum_pool(name="pout", bufs=2))
         ctx.enter_context(tc.manual_schedule())
 
         ident = keep.tile([P, P], F32, name="ident")
-        s_col = keep.tile([P, PACK], F32, name="s_col")
-        scale = keep.tile([P, G * K], F32, name="scale")
-        bias_bf = keep.tile([P, PACK], BF16, name="bias_bf")
-        bias = keep.tile([P, PACK], F32, name="bias")
-        warm = keep.tile([P, 1], F32, name="warm")
+        ones = keep.tile([P, 1], F32, name="ones")
+        s4 = keep.tile([P, PACK], F32, name="s4")
+        bias = keep.tile([P, PACK], BF16, name="bias")
         wi_raw = keep.tile([P, CH], U32, name="wi_raw", align_bytes=64)
         wh_raw = keep.tile([P, CH], U32, name="wh_raw", align_bytes=64)
         wi = keep.tile([P, CH], U32, name="wi", align_bytes=64)
@@ -60,55 +61,73 @@ def tile_lstmcell_pa_t_w8_kernel(
         ws = keep.tile([P, CH], U8, name="ws", align_bytes=64)
         wts = keep.tile([P, N_OUT], U8, name="wts", align_bytes=64)
 
-        xb, me, xw, turned, q = {}, {}, {}, {}, {}
-        sig, gated, gq = {}, {}, {}
+        xb, me, xw, xbank, turned, q = {}, {}, {}, {}, {}, {}
+        sig, gated, gq, res = {}, {}, {}, {}
 
         def load_x(g):
-            t = xin.tile([P, G, K], U8, name="xb")
-            nc.sync.dma_start(out=t[:], in_=x_hbm[:, g * G : (g + 1) * G, :])
+            t = xin.tile([P, G * K], U8, name="xb")
+            nc.sync.dma_start(out=t[:].rearrange("p (i k) -> p i k", i=G), in_=x_hbm[:, g * G : (g + 1) * G, :])
             xb[g] = t
 
         def load_me(g):
-            t = mein.tile([P, G, K], BF16, name="me")
-            nc.sync.dma_start(out=t[:], in_=me_hbm[:, g * G : (g + 1) * G, :])
+            t = mein.tile([P, G * K], BF16, name="me")
+            nc.sync.dma_start(out=t[:].rearrange("p (i k) -> p i k", i=G), in_=me_hbm[:, g * G : (g + 1) * G, :])
             me[g] = t
 
         def load(g):
             load_x(g)
             load_me(g)
 
-        def widen(g):
-            t = work.tile([P, G * K], BF16, name="xw")
-            src = xb[g][:].rearrange("p i k -> p (i k)")
-            pieces = G if g == 0 else 1
-            w = G * K // pieces
-            for j in range(pieces):
+        def widen_vector(g, b):
+            t = work.tile([P, 2 * K], BF16, name="xw%d" % b)
+            nc.vector.tensor_scalar(
+                out=t[:].rearrange("p (u m e) -> p m u e", u=2, e=2),
+                in0=xb[g][:, 2 * K * b : 2 * K * (b + 1)].bitcast(FP8).rearrange("p (m u e) -> p m u e", u=2, e=2),
+                scalar1=ones[:],
+                scalar2=None,
+                op0=MULT,
+            )
+            words = t[:].bitcast(F32)
+            xw[g, b] = [[words[:, u * HT + i * P : u * HT + (i + 1) * P] for i in range(2)] for u in range(2)]
+
+        def widen_scalar(g, b):
+            t = work.tile([P, 2 * K], BF16, name="xw%d" % b)
+            nc.scalar.copy(out=t[:], in_=xb[g][:, 2 * K * b : 2 * K * (b + 1)].bitcast(FP8))
+            words = t[:].bitcast(F32)
+            xw[g, b] = [[words[:, i * HT + u : (i + 1) * HT : 2] for i in range(2)] for u in range(2)]
+
+        def turn_x(g):
+            for b in range(2):
+                pt = px.tile([P, 2, 2, P], F32, name="xt")
+                for u in range(2):
+                    for i in range(2):
+                        nc.tensor.transpose(pt[:, u, i, :], xw[g, b][u][i], ident[:])
+                xbank[g, b] = pt
+
+        def scale_x(g):
+            for b in range(2):
+                lo = (GT + b * HT) * PACK
                 nc.vector.tensor_tensor(
-                    out=t[:, j * w : (j + 1) * w],
-                    in0=src[:, j * w : (j + 1) * w].bitcast(FP8),
-                    in1=scale[:, 0:w],
+                    out=turned[g][:, lo : lo + HT * PACK].rearrange("p (m u e) -> p m u e", u=2, e=2),
+                    in0=xbank[g, b][:].rearrange("p u i r -> p (u i r)").bitcast(BF16).rearrange("p (u m e) -> p m u e", u=2, e=2),
+                    in1=s4[:].rearrange("p (u e) -> p u e", u=2).unsqueeze(1).to_broadcast([P, HT, 2, 2]),
                     op=MULT,
                 )
-            xw[g] = t
-
-        def turn(src, dst):
-            words = src.bitcast(F32)
-            dst_w = dst.bitcast(F32).rearrange("p (i r u) -> p i r u", i=G, u=2)
-            for b in range(G // 2):
-                pt = ptp.tile([P, 2, 2, P], F32, name="pt")
-                for i in range(2):
-                    for u in range(2):
-                        base = (2 * b + i) * (K // 2)
-                        nc.tensor.transpose(pt[:, i, u, :], words[:, base + u : base + K // 2 : 2], ident[:])
-                nc.scalar.copy(out=dst_w[:, 2 * b : 2 * b + 2], in_=pt[:].rearrange("p i u r -> p i r u"))
 
         def turn_me(g):
             t = turnp.tile([P, 2 * GT * PACK], BF16, name="turned", align_bytes=64)
             turned[g] = t
-            turn(me[g][:].rearrange("p i k -> p (i k)"), t[:, 0 : GT * PACK])
-
-        def turn_x(g):
-            turn(xw[g][:], turned[g][:, GT * PACK : 2 * GT * PACK])
+            words = me[g][:].bitcast(F32)
+            for b in range(2):
+                pt = pmix.tile([P, 2, 2, P], F32, name="mix")
+                for u in range(2):
+                    for i in range(2):
+                        base = (2 * b + i) * (K // 2)
+                        nc.tensor.transpose(pt[:, u, i, :], words[:, base + u : base + K // 2 : 2], ident[:])
+                nc.scalar.copy(
+                    out=t[:, b * HT * PACK : (b + 1) * HT * PACK].bitcast(F32).rearrange("p (m u) -> p m u", u=2),
+                    in_=pt[:].rearrange("p u i r -> p (i r) u"),
+                )
 
         def quant_in(g):
             codes = work.tile([P, 2 * GT], U32, name="qc", align_bytes=64)
@@ -134,128 +153,127 @@ def tile_lstmcell_pa_t_w8_kernel(
                 )
                 nc.scalar.activation(out=s[:, t, :], in_=pm[:], func=ACT.Sigmoid, bias=bias[:, t : t + 1])
 
-        def pieces_of(g):
-            return ((0, 2), (2, 3), (3, 4)) if g == GROUPS - 1 else ((0, G),)
-
-        def gate(g, pieces):
+        def gate(engine, g, lo, hi):
             if g not in gated:
-                fresh = work.tile([P, GT * PACK], BF16, name="gated", align_bytes=64)
+                fresh = single.tile([P, GT * PACK], BF16, name="gated_last" if g == GROUPS - 1 else "gated", align_bytes=64)
                 gated[g] = fresh
-            t = gated[g]
-            for i0, i1 in pieces:
-                rows = slice(i0 * P, i1 * P)
-                cols = slice(i0 * P * PACK, i1 * P * PACK)
-                nc.vector.tensor_tensor(
-                    out=t[:, cols].rearrange("p (c i t) -> p c t i", i=4, t=PACK),
-                    in0=sig[g][:, :, rows].rearrange("p t (c i) -> p c t i", i=4),
-                    in1=turned[g][:, cols].rearrange("p (c i t) -> p c t i", i=4, t=PACK),
-                    op=MULT,
-                )
+            cols = slice(lo * PACK, hi * PACK)
+            engine.tensor_tensor(
+                out=gated[g][:, cols].rearrange("p (c i t) -> p c t i", i=4, t=PACK),
+                in0=sig[g][:, :, lo:hi].rearrange("p t (c i) -> p c t i", i=4),
+                in1=turned[g][:, cols].rearrange("p (c i t) -> p c t i", i=4, t=PACK),
+                op=MULT,
+            )
 
-        def quant_gated(g, pieces):
+        def quant_gated(g, lo, hi):
             if g not in gq:
                 codes = work.tile([P, GT], U32, name="gc", align_bytes=64)
                 scales = work.tile([P, GT], U8, name="gs", align_bytes=64)
                 gq[g] = (codes, scales)
             codes, scales = gq[g]
-            for i0, i1 in pieces:
-                rows = slice(i0 * P, i1 * P)
-                nc.vector.quantize_mx(
-                    out=codes[:, rows].bitcast(FP8X4),
-                    scales=scales[:, rows],
-                    in_=gated[g][:, i0 * P * PACK : i1 * P * PACK],
+            nc.vector.quantize_mx(
+                out=codes[:, lo:hi].bitcast(FP8X4), scales=scales[:, lo:hi], in_=gated[g][:, lo * PACK : hi * PACK]
+            )
+
+        def read_out(g, i0, i1):
+            if g not in res:
+                fresh = outp.tile([P, G, N_OUT], F32, name="res")
+                res[g] = fresh
+            o = res[g]
+            for b in range(i0, i1, 2):
+                e = min(b + 2, i1)
+                po = pmix.tile([P, 2, N_OUT], F32, name="mix")
+                for i in range(b, e):
+                    cols = slice(i * P, (i + 1) * P)
+                    nc.tensor.matmul_mx(
+                        out=po[:, i - b, :], lhsT=gq[g][0][:, cols].bitcast(FP8X4), lhsT_scale=gq[g][1][:, cols],
+                        rhs=wt[:].bitcast(FP8X4), rhs_scale=wts[:], start=True, stop=True,
+                    )
+                nc.scalar.copy(out=o[:, b:e, :], in_=po[:, 0 : e - b, :])
+            nc.sync.dma_start(out=out_hbm[:, g * G + i0 : g * G + i1, :], in_=o[:, i0:i1, :])
+
+        def permute(dst, src):
+            nc.vector.tensor_copy(
+                out=dst.rearrange("p (t m) -> p t m", t=PACK), in_=src.rearrange("p (m t) -> p t m", t=PACK)
+            )
+
+        def load_scale_rows(queue, tile, row0, hbm):
+            for h in range(4):
+                queue.dma_start(
+                    out=tile[32 * h + row0 : 32 * h + row0 + 4, :].bitcast(I32), in_=hbm[0, 4 * h : 4 * h + 4, :].bitcast(I32)
                 )
 
-        def read_out(g):
-            o = outp.tile([P, G, N_OUT], F32, name="res")
-            for i0, i1 in pieces_of(g):
-                for b in range(i0, i1, 2):
-                    e = min(b + 2, i1)
-                    po = pout.tile([P, 2, N_OUT], F32, name="po")
-                    for i in range(b, e):
-                        cols = slice(i * P, (i + 1) * P)
-                        nc.tensor.matmul_mx(
-                            out=po[:, i - b, :], lhsT=gq[g][0][:, cols].bitcast(FP8X4), lhsT_scale=gq[g][1][:, cols],
-                            rhs=wt[:].bitcast(FP8X4), rhs_scale=wts[:], start=True, stop=True,
-                        )
-                    nc.scalar.copy(out=o[:, b:e, :], in_=po[:, 0 : e - b, :])
-                nc.sync.dma_start(out=out_hbm[:, g * G + i0 : g * G + i1, :], in_=o[:, i0:i1, :])
+        def load_words(tile, hbm):
+            nc.sync.dma_start(out=tile[:].bitcast(I32), in_=hbm[0].rearrange("p n t -> p (n t)").bitcast(I32))
 
-        make_identity(nc, ident[:])
+        nc.gpsimd.memset(ones[:], 1.0)
         nc.gpsimd.memset(ws_raw[:].bitcast(I32), 0)
+        make_identity(nc, ident[:])
+        load_scale_rows(nc.gpsimd, ws_raw, 4, wh_scales)
         nc.gpsimd.memset(wts[:].bitcast(I32), 0)
-        nc.gpsimd.memset(warm[:], 0.0)
-        nc.scalar.activation(out=warm[:], in_=warm[:], func=ACT.Sigmoid)
 
-        nc.sync.dma_start(out=s_col[:], in_=x_scale.rearrange("o (p t) -> p (o t)", t=PACK))
-        nc.sync.dma_start(out=wi_raw[:].bitcast(I32), in_=wi_words[0].rearrange("p n t -> p (n t)").bitcast(I32))
-        nc.sync.dma_start(out=wh_raw[:].bitcast(I32), in_=wh_words[0].rearrange("p n t -> p (n t)").bitcast(I32))
         load_x(0)
-        load_me(0)
+        nc.sync.dma_start(out=s4[:], in_=x_scale.rearrange("o (p t) -> p (o t)", t=PACK))
         load_x(1)
-        load_x(2)
+        load_me(0)
+        load_words(wi_raw, wi_words)
+        load_words(wh_raw, wh_words)
         load_me(1)
-        for h in range(4):
-            for w, hbm in enumerate((wi_scales, wh_scales)):
-                nc.sync.dma_start(
-                    out=ws_raw[32 * h + 4 * w : 32 * h + 4 * w + 4, :].bitcast(I32),
-                    in_=hbm[0, 4 * h : 4 * h + 4, :].bitcast(I32),
-                )
-        nc.sync.dma_start(out=bias_bf[:], in_=mem_bias.rearrange("(p t) -> p t", t=PACK))
+        load_x(2)
+        load_scale_rows(nc.sync, ws_raw, 0, wi_scales)
+        nc.sync.dma_start(out=bias[:], in_=mem_bias.rearrange("(p t) -> p t", t=PACK))
         load_me(2)
-        load_x(3)
-        load_me(3)
-        nc.sync.dma_start(out=wt[:].bitcast(I32), in_=wt_words[0].rearrange("p n t -> p (n t)").bitcast(I32))
-        for h in range(4):
-            nc.sync.dma_start(
-                out=wts[32 * h : 32 * h + 4, :].bitcast(I32), in_=wt_scales[0, 4 * h : 4 * h + 4, :].bitcast(I32)
-            )
 
-        ps = ptp.tile([P, PACK, P], F32, name="pt")
-        for t in range(PACK):
-            nc.tensor.transpose(ps[:, t, :], s_col[:, t : t + 1].to_broadcast([P, P]), ident[:])
-        for j in range(G):
-            nc.scalar.copy(
-                out=scale[:, j * K : (j + 1) * K].rearrange("p (n t) -> p n t", t=PACK),
-                in_=ps[:].rearrange("p t n -> p n t"),
-            )
-
-        for raw, dst in ((wi_raw, wi), (wh_raw, wh)):
-            nc.vector.tensor_copy(
-                out=dst[:].bitcast(I32).rearrange("p (t m) -> p t m", t=PACK),
-                in_=raw[:].bitcast(I32).rearrange("p (m t) -> p t m", t=PACK),
-            )
-
-        def permute_scales():
-            nc.vector.tensor_copy(
-                out=ws[:].rearrange("p (t m) -> p t m", t=PACK),
-                in_=ws_raw[:].rearrange("p (m t) -> p t m", t=PACK),
-            )
-
-        for s in range(GROUPS + 5):
+        last = GROUPS - 1
+        for s in range(GROUPS + 4):
             if s + AHEAD < GROUPS:
                 load(s + AHEAD)
+            if s == 1:
+                load_words(wt, wt_words)
+                load_scale_rows(nc.sync, wts, 0, wt_scales)
+            if 0 <= s - 5:
+                quant_gated(s - 5, 0, GT)
+            if s == 1:
+                turn_x(0)
+            if s < GROUPS:
+                widen_scalar(s, 1)
+            if 0 <= s - 3 < GROUPS:
+                gates(s - 3, (0, 1))
+            shared = 0 <= s - 4 and s - 2 < GROUPS
+            if 0 <= s - 2 < GROUPS:
+                scale_x(s - 2)
+            if shared:
+                gate(nc.gpsimd, s - 4, 0, POOL_TOKENS)
+            if 0 <= s - 1 < GROUPS and s != 3:
+                turn_me(s - 1)
+            if 0 <= s - 4 < last:
+                gate(nc.vector, s - 4, POOL_TOKENS if shared else 0, GT)
+            if s == 2:
+                widen_vector(1, 0)
+                permute(wi[:].bitcast(I32), wi_raw[:].bitcast(I32))
+                permute(wh[:].bitcast(I32), wh_raw[:].bitcast(I32))
+            elif s < GROUPS and s != 1:
+                widen_vector(s, 0)
+            if 0 <= s - 3 < GROUPS:
+                gates(s - 3, (2, 3))
+            if 0 <= s - 5:
+                read_out(s - 5, 0, G)
+            if 1 <= s - 1 < GROUPS:
+                turn_x(s - 1)
+            if s == 3:
+                turn_me(s - 1)
             if 0 <= s - 2 < GROUPS:
                 quant_in(s - 2)
             if s == 2:
-                permute_scales()
-            if s == 3:
-                nc.scalar.copy(out=bias[:], in_=bias_bf[:])
-            if 0 <= s - 4 < GROUPS:
-                gate(s - 4, pieces_of(s - 4)[0:2])
-            if 0 <= s - 3 < GROUPS:
-                gates(s - 3, (0, 1))
-            if 0 <= s - 1 < GROUPS:
-                turn_me(s - 1)
-            if 0 <= s - 3 < GROUPS:
-                gates(s - 3, (2, 3))
-            if 0 <= s - 1 < GROUPS:
-                turn_x(s - 1)
-            if s < GROUPS:
-                widen(s)
-            if 0 <= s - 4 < GROUPS:
-                quant_gated(s - 4, pieces_of(s - 4)[0:1])
-                gate(s - 4, pieces_of(s - 4)[2:])
-                quant_gated(s - 4, pieces_of(s - 4)[1:])
-            if 0 <= s - 5 < GROUPS:
-                read_out(s - 5)
+                widen_vector(2, 0)
+                permute(ws[:], ws_raw[:])
+
+        gate(nc.vector, last, 0, 2 * P)
+        gate(nc.vector, last, 2 * P, 3 * P)
+        quant_gated(last, 0, 2 * P)
+        gate(nc.vector, last, 3 * P, 4 * P)
+        read_out(last, 0, 2)
+        quant_gated(last, 2 * P, 3 * P)
+        read_out(last, 2, 3)
+        quant_gated(last, 3 * P, 4 * P)
+        read_out(last, 3, 4)

@@ -25,6 +25,7 @@ GT = G * P
 HT = GT // 2
 AHEAD = 3
 POOL_TOKENS = 192
+VECTOR_SLABS = 3
 
 
 def tile_lstmcell_pa_t_w8_kernel(
@@ -78,30 +79,33 @@ def tile_lstmcell_pa_t_w8_kernel(
             load_x(g)
             load_me(g)
 
-        def widen_vector(g, b):
-            t = work.tile([P, 2 * K], BF16, name="xw%d" % b)
+        def widen_vector(g):
+            n = VECTOR_SLABS * P
+            t = work.tile([P, VECTOR_SLABS * K], BF16, name="xw_vector")
             nc.vector.tensor_scalar(
                 out=t[:].rearrange("p (u m e) -> p m u e", u=2, e=2),
-                in0=xb[g][:, 2 * K * b : 2 * K * (b + 1)].bitcast(FP8).rearrange("p (m u e) -> p m u e", u=2, e=2),
+                in0=xb[g][:, 0 : VECTOR_SLABS * K].bitcast(FP8).rearrange("p (m u e) -> p m u e", u=2, e=2),
                 scalar1=ones[:],
                 scalar2=None,
                 op0=MULT,
             )
             words = t[:].bitcast(F32)
-            xw[g, b] = [[words[:, u * HT + i * P : u * HT + (i + 1) * P] for i in range(2)] for u in range(2)]
+            for i in range(VECTOR_SLABS):
+                xw[g, i] = [words[:, u * n + i * P : u * n + (i + 1) * P] for u in range(2)]
 
-        def widen_scalar(g, b):
-            t = work.tile([P, 2 * K], BF16, name="xw%d" % b)
-            nc.scalar.copy(out=t[:], in_=xb[g][:, 2 * K * b : 2 * K * (b + 1)].bitcast(FP8))
+        def widen_scalar(g):
+            t = work.tile([P, (G - VECTOR_SLABS) * K], BF16, name="xw_scalar")
+            nc.scalar.copy(out=t[:], in_=xb[g][:, VECTOR_SLABS * K :].bitcast(FP8))
             words = t[:].bitcast(F32)
-            xw[g, b] = [[words[:, i * HT + u : (i + 1) * HT : 2] for i in range(2)] for u in range(2)]
+            for i in range(G - VECTOR_SLABS):
+                xw[g, VECTOR_SLABS + i] = [words[:, i * HT + u : (i + 1) * HT : 2] for u in range(2)]
 
         def turn_x(g):
             for b in range(2):
                 pt = px.tile([P, 2, 2, P], F32, name="xt")
-                for u in range(2):
-                    for i in range(2):
-                        nc.tensor.transpose(pt[:, u, i, :], xw[g, b][u][i], ident[:])
+                for i in range(2):
+                    for u in range(2):
+                        nc.tensor.transpose(pt[:, u, i, :], xw[g, 2 * b + i][u], ident[:])
                 xbank[g, b] = pt
 
         def scale_x(g):
@@ -236,7 +240,7 @@ def tile_lstmcell_pa_t_w8_kernel(
             if s == 1:
                 turn_x(0)
             if s < GROUPS:
-                widen_scalar(s, 1)
+                widen_scalar(s)
             if 0 <= s - 3 < GROUPS:
                 gates(s - 3, (0, 1))
             shared = 0 <= s - 4 and s - 2 < GROUPS
@@ -249,11 +253,11 @@ def tile_lstmcell_pa_t_w8_kernel(
             if 0 <= s - 4 < last:
                 gate(nc.vector, s - 4, POOL_TOKENS if shared else 0, GT)
             if s == 2:
-                widen_vector(1, 0)
+                widen_vector(1)
                 permute(wi[:].bitcast(I32), wi_raw[:].bitcast(I32))
                 permute(wh[:].bitcast(I32), wh_raw[:].bitcast(I32))
             elif s < GROUPS and s != 1:
-                widen_vector(s, 0)
+                widen_vector(s)
             if 0 <= s - 3 < GROUPS:
                 gates(s - 3, (2, 3))
             if 0 <= s - 5:
@@ -265,7 +269,7 @@ def tile_lstmcell_pa_t_w8_kernel(
             if 0 <= s - 2 < GROUPS:
                 quant_in(s - 2)
             if s == 2:
-                widen_vector(2, 0)
+                widen_vector(2)
                 permute(ws[:], ws_raw[:])
 
         gate(nc.vector, last, 0, 2 * P)

@@ -24,8 +24,7 @@ GROUPS = TILES // G
 GT = G * P
 HT = GT // 2
 AHEAD = 3
-POOL_TOKENS = 192
-VECTOR_SLABS = 3
+POOL_TOKENS = 224
 
 
 def tile_lstmcell_pa_t_w8_kernel(
@@ -41,7 +40,6 @@ def tile_lstmcell_pa_t_w8_kernel(
         xin = ctx.enter_context(tc.tile_pool(name="xin", bufs=5))
         mein = ctx.enter_context(tc.tile_pool(name="mein", bufs=6))
         work = ctx.enter_context(tc.tile_pool(name="work", bufs=3))
-        single = ctx.enter_context(tc.tile_pool(name="single", bufs=1))
         turnp = ctx.enter_context(tc.tile_pool(name="turnp", bufs=5))
         outp = ctx.enter_context(tc.tile_pool(name="outp", bufs=3))
         px = ctx.enter_context(tc.psum_pool(name="px", bufs=2))
@@ -60,6 +58,7 @@ def tile_lstmcell_pa_t_w8_kernel(
         wt = keep.tile([P, N_OUT], U32, name="wt", align_bytes=64)
         ws_raw = keep.tile([P, CH], U8, name="ws_raw", align_bytes=64)
         ws = keep.tile([P, CH], U8, name="ws", align_bytes=64)
+        gated_last = keep.tile([P, GT * PACK], BF16, name="gated_last", align_bytes=64)
         wts = keep.tile([P, N_OUT], U8, name="wts", align_bytes=64)
 
         xb, me, xw, xbank, turned, q = {}, {}, {}, {}, {}, {}
@@ -79,26 +78,33 @@ def tile_lstmcell_pa_t_w8_kernel(
             load_x(g)
             load_me(g)
 
+        def vector_slabs(g):
+            return 0 if g == 1 else 2 - g % 2
+
         def widen_vector(g):
-            n = VECTOR_SLABS * P
-            t = work.tile([P, VECTOR_SLABS * K], BF16, name="xw_vector")
+            slabs = vector_slabs(g)
+            if slabs == 0:
+                return
+            n = slabs * P
+            t = work.tile([P, slabs * K], BF16, name="xw_vector")
             nc.vector.tensor_scalar(
                 out=t[:].rearrange("p (u m e) -> p m u e", u=2, e=2),
-                in0=xb[g][:, 0 : VECTOR_SLABS * K].bitcast(FP8).rearrange("p (m u e) -> p m u e", u=2, e=2),
+                in0=xb[g][:, 0 : slabs * K].bitcast(FP8).rearrange("p (m u e) -> p m u e", u=2, e=2),
                 scalar1=ones[:],
                 scalar2=None,
                 op0=MULT,
             )
             words = t[:].bitcast(F32)
-            for i in range(VECTOR_SLABS):
+            for i in range(slabs):
                 xw[g, i] = [words[:, u * n + i * P : u * n + (i + 1) * P] for u in range(2)]
 
         def widen_scalar(g):
-            t = work.tile([P, (G - VECTOR_SLABS) * K], BF16, name="xw_scalar")
-            nc.scalar.copy(out=t[:], in_=xb[g][:, VECTOR_SLABS * K :].bitcast(FP8))
+            slabs = vector_slabs(g)
+            t = work.tile([P, (G - slabs) * K], BF16, name="xw_scalar")
+            nc.scalar.copy(out=t[:], in_=xb[g][:, slabs * K :].bitcast(FP8))
             words = t[:].bitcast(F32)
-            for i in range(G - VECTOR_SLABS):
-                xw[g, VECTOR_SLABS + i] = [words[:, i * HT + u : (i + 1) * HT : 2] for u in range(2)]
+            for i in range(G - slabs):
+                xw[g, slabs + i] = [words[:, i * HT + u : (i + 1) * HT : 2] for u in range(2)]
 
         def turn_x(g):
             for b in range(2):
@@ -158,9 +164,7 @@ def tile_lstmcell_pa_t_w8_kernel(
                 nc.scalar.activation(out=s[:, t, :], in_=pm[:], func=ACT.Sigmoid, bias=bias[:, t : t + 1])
 
         def gate(engine, g, lo, hi):
-            if g not in gated:
-                fresh = single.tile([P, GT * PACK], BF16, name="gated_last" if g == GROUPS - 1 else "gated", align_bytes=64)
-                gated[g] = fresh
+            gated[g] = gated_last[:] if g == GROUPS - 1 else turned[g + 1][:, GT * PACK :]
             cols = slice(lo * PACK, hi * PACK)
             engine.tensor_tensor(
                 out=gated[g][:, cols].rearrange("p (c i t) -> p c t i", i=4, t=PACK),
@@ -218,9 +222,9 @@ def tile_lstmcell_pa_t_w8_kernel(
 
         load_x(0)
         nc.sync.dma_start(out=s4[:], in_=x_scale.rearrange("o (p t) -> p (o t)", t=PACK))
+        load_words(wi_raw, wi_words)
         load_x(1)
         load_me(0)
-        load_words(wi_raw, wi_words)
         load_words(wh_raw, wh_words)
         load_me(1)
         load_x(2)
@@ -253,11 +257,11 @@ def tile_lstmcell_pa_t_w8_kernel(
             if 0 <= s - 4 < last:
                 gate(nc.vector, s - 4, POOL_TOKENS if shared else 0, GT)
             if s == 2:
-                widen_vector(1)
-                permute(wi[:].bitcast(I32), wi_raw[:].bitcast(I32))
                 permute(wh[:].bitcast(I32), wh_raw[:].bitcast(I32))
             elif s < GROUPS and s != 1:
                 widen_vector(s)
+            if s == 0:
+                permute(wi[:].bitcast(I32), wi_raw[:].bitcast(I32))
             if 0 <= s - 3 < GROUPS:
                 gates(s - 3, (2, 3))
             if 0 <= s - 5:

@@ -24,7 +24,7 @@ GROUPS = TILES // G
 GT = G * P
 HT = GT // 2
 AHEAD = 3
-POOL_TOKENS = 224
+VECTOR_TOKENS = 192
 
 
 def tile_lstmcell_pa_t_w8_kernel(
@@ -43,8 +43,8 @@ def tile_lstmcell_pa_t_w8_kernel(
         turnp = ctx.enter_context(tc.tile_pool(name="turnp", bufs=5))
         outp = ctx.enter_context(tc.tile_pool(name="outp", bufs=3))
         px = ctx.enter_context(tc.psum_pool(name="px", bufs=2))
-        pmix = ctx.enter_context(tc.psum_pool(name="pmix", bufs=3))
-        pmg = ctx.enter_context(tc.psum_pool(name="pmg", bufs=3))
+        pkeep = ctx.enter_context(tc.psum_pool(name="pkeep", bufs=2))
+        pmix = ctx.enter_context(tc.psum_pool(name="pmix", bufs=4))
         ctx.enter_context(tc.manual_schedule())
 
         ident = keep.tile([P, P], F32, name="ident")
@@ -61,7 +61,7 @@ def tile_lstmcell_pa_t_w8_kernel(
         gated_last = keep.tile([P, GT * PACK], BF16, name="gated_last", align_bytes=64)
         wts = keep.tile([P, N_OUT], U8, name="wts", align_bytes=64)
 
-        xb, me, xw, xbank, turned, q = {}, {}, {}, {}, {}, {}
+        xb, me, xw, xbank, mbank, turned, q = {}, {}, {}, {}, {}, {}, {}
         sig, gated, gq, res = {}, {}, {}, {}
 
         def load_x(g):
@@ -79,7 +79,7 @@ def tile_lstmcell_pa_t_w8_kernel(
             load_me(g)
 
         def vector_slabs(g):
-            return 0 if g == 1 else 2 - g % 2
+            return 0 if g == 1 else 2
 
         def widen_vector(g):
             slabs = vector_slabs(g)
@@ -115,6 +115,8 @@ def tile_lstmcell_pa_t_w8_kernel(
                 xbank[g, b] = pt
 
         def scale_x(g):
+            t = turnp.tile([P, 2 * GT * PACK], BF16, name="turned", align_bytes=64)
+            turned[g] = t
             for b in range(2):
                 lo = (GT + b * HT) * PACK
                 nc.vector.tensor_tensor(
@@ -125,19 +127,20 @@ def tile_lstmcell_pa_t_w8_kernel(
                 )
 
         def turn_me(g):
-            t = turnp.tile([P, 2 * GT * PACK], BF16, name="turned", align_bytes=64)
-            turned[g] = t
             words = me[g][:].bitcast(F32)
-            for b in range(2):
-                pt = pmix.tile([P, 2, 2, P], F32, name="mix")
-                for u in range(2):
-                    for i in range(2):
+            for b, pool in enumerate((pkeep, pmix)):
+                dst = turned[g][:, b * HT * PACK : (b + 1) * HT * PACK].bitcast(F32)
+                pt = pool.tile([P, 2 * HT], F32, name="mix")
+                if b == 0:
+                    mbank[g] = pt
+                    bank = pt[:].rearrange("p (c u i) -> p u c i", u=2, i=4)
+                else:
+                    bank = pt[:].rearrange("p (u c i) -> p u c i", u=2, i=4)
+                for i in range(2):
+                    for u in range(2):
                         base = (2 * b + i) * (K // 2)
-                        nc.tensor.transpose(pt[:, u, i, :], words[:, base + u : base + K // 2 : 2], ident[:])
-                nc.scalar.copy(
-                    out=t[:, b * HT * PACK : (b + 1) * HT * PACK].bitcast(F32).rearrange("p (m u) -> p m u", u=2),
-                    in_=pt[:].rearrange("p u i r -> p (i r) u"),
-                )
+                        nc.tensor.transpose(bank[:, u, 32 * i : 32 * (i + 1), :], words[:, base + u : base + K // 2 : 2], ident[:])
+                nc.scalar.copy(out=dst.rearrange("p (c i u) -> p c i u", i=4, u=2), in_=bank.rearrange("p u c i -> p c i u"))
 
         def quant_in(g):
             codes = work.tile([P, 2 * GT], U32, name="qc", align_bytes=64)
@@ -152,7 +155,7 @@ def tile_lstmcell_pa_t_w8_kernel(
             s = sig[g]
             for t in ts:
                 cols = slice(t * P, (t + 1) * P)
-                pm = pmg.tile([P, GT], F32, name="pm")
+                pm = pmix.tile([P, GT], F32, name="mix")
                 nc.tensor.matmul_mx(
                     out=pm[:], lhsT=wi[:, cols].bitcast(FP8X4), lhsT_scale=ws[:, cols],
                     rhs=q[g][0][:, GT:].bitcast(FP8X4), rhs_scale=q[g][1][:, GT:], start=True, stop=False,
@@ -163,13 +166,17 @@ def tile_lstmcell_pa_t_w8_kernel(
                 )
                 nc.scalar.activation(out=s[:, t, :], in_=pm[:], func=ACT.Sigmoid, bias=bias[:, t : t + 1])
 
-        def gate(engine, g, lo, hi):
+        def gate(engine, g, lo, hi, from_psum):
             gated[g] = gated_last[:] if g == GROUPS - 1 else turned[g + 1][:, GT * PACK :]
             cols = slice(lo * PACK, hi * PACK)
+            if from_psum:
+                me_turned = mbank[g][:].bitcast(BF16)[:, cols].rearrange("p (c u i e) -> p c u e i", u=2, i=4, e=2)
+            else:
+                me_turned = turned[g][:, cols].rearrange("p (c i u e) -> p c u e i", i=4, u=2, e=2)
             engine.tensor_tensor(
-                out=gated[g][:, cols].rearrange("p (c i t) -> p c t i", i=4, t=PACK),
-                in0=sig[g][:, :, lo:hi].rearrange("p t (c i) -> p c t i", i=4),
-                in1=turned[g][:, cols].rearrange("p (c i t) -> p c t i", i=4, t=PACK),
+                out=gated[g][:, cols].rearrange("p (c i u e) -> p c u e i", i=4, u=2, e=2),
+                in0=sig[g][:, :, lo:hi].rearrange("p (u e) (c i) -> p c u e i", i=4, u=2),
+                in1=me_turned,
                 op=MULT,
             )
 
@@ -243,22 +250,22 @@ def tile_lstmcell_pa_t_w8_kernel(
                 quant_gated(s - 5, 0, GT)
             if s == 1:
                 turn_x(0)
-            if s < GROUPS:
-                widen_scalar(s)
             if 0 <= s - 3 < GROUPS:
                 gates(s - 3, (0, 1))
-            shared = 0 <= s - 4 and s - 2 < GROUPS
+            if 0 <= s - 4:
+                if s - 2 < GROUPS:
+                    gate(nc.gpsimd, s - 4, VECTOR_TOKENS, GT, False)
+                    gate(nc.vector, s - 4, 0, VECTOR_TOKENS, True)
+                else:
+                    gate(nc.gpsimd, s - 4, 3 * P, GT, False)
+                    gate(nc.vector, s - 4, 0, HT, True)
+                    gate(nc.vector, s - 4, HT, 3 * P, False)
             if 0 <= s - 2 < GROUPS:
                 scale_x(s - 2)
-            if shared:
-                gate(nc.gpsimd, s - 4, 0, POOL_TOKENS)
-            if 0 <= s - 1 < GROUPS and s != 3:
-                turn_me(s - 1)
-            if 0 <= s - 4 < last:
-                gate(nc.vector, s - 4, POOL_TOKENS if shared else 0, GT)
+                turn_me(s - 2)
             if s == 2:
                 permute(wh[:].bitcast(I32), wh_raw[:].bitcast(I32))
-            elif s < GROUPS and s != 1:
+            elif s < GROUPS:
                 widen_vector(s)
             if s == 0:
                 permute(wi[:].bitcast(I32), wi_raw[:].bitcast(I32))
@@ -268,20 +275,14 @@ def tile_lstmcell_pa_t_w8_kernel(
                 read_out(s - 5, 0, G)
             if 1 <= s - 1 < GROUPS:
                 turn_x(s - 1)
-            if s == 3:
-                turn_me(s - 1)
+            if s < GROUPS:
+                widen_scalar(s)
             if 0 <= s - 2 < GROUPS:
                 quant_in(s - 2)
             if s == 2:
                 widen_vector(2)
                 permute(ws[:], ws_raw[:])
 
-        gate(nc.vector, last, 0, 2 * P)
-        gate(nc.vector, last, 2 * P, 3 * P)
-        quant_gated(last, 0, 2 * P)
-        gate(nc.vector, last, 3 * P, 4 * P)
-        read_out(last, 0, 2)
-        quant_gated(last, 2 * P, 3 * P)
-        read_out(last, 2, 3)
-        quant_gated(last, 3 * P, 4 * P)
-        read_out(last, 3, 4)
+        for i0, i1 in ((0, 2), (2, 3), (3, 4)):
+            quant_gated(last, i0 * P, i1 * P)
+            read_out(last, i0, i1)

@@ -24,7 +24,7 @@ GROUPS = TILES // G
 GT = G * P
 HT = GT // 2
 AHEAD = 3
-VECTOR_TOKENS = 192
+VECTOR_TOKENS = 176
 
 
 def tile_lstmcell_pa_t_w8_kernel(
@@ -38,10 +38,10 @@ def tile_lstmcell_pa_t_w8_kernel(
     with ExitStack() as ctx:
         keep = ctx.enter_context(tc.tile_pool(name="keep", bufs=1))
         xin = ctx.enter_context(tc.tile_pool(name="xin", bufs=5))
-        mein = ctx.enter_context(tc.tile_pool(name="mein", bufs=6))
+        mein = ctx.enter_context(tc.tile_pool(name="mein", bufs=4))
         work = ctx.enter_context(tc.tile_pool(name="work", bufs=3))
         turnp = ctx.enter_context(tc.tile_pool(name="turnp", bufs=5))
-        outp = ctx.enter_context(tc.tile_pool(name="outp", bufs=3))
+        outp = ctx.enter_context(tc.tile_pool(name="outp", bufs=4))
         px = ctx.enter_context(tc.psum_pool(name="px", bufs=2))
         pkeep = ctx.enter_context(tc.psum_pool(name="pkeep", bufs=2))
         pmix = ctx.enter_context(tc.psum_pool(name="pmix", bufs=4))
@@ -69,22 +69,17 @@ def tile_lstmcell_pa_t_w8_kernel(
             nc.sync.dma_start(out=t[:].rearrange("p (i k) -> p i k", i=G), in_=x_hbm[:, g * G : (g + 1) * G, :])
             xb[g] = t
 
-        def load_me(g):
-            t = mein.tile([P, G * K], BF16, name="me")
-            nc.sync.dma_start(out=t[:].rearrange("p (i k) -> p i k", i=G), in_=me_hbm[:, g * G : (g + 1) * G, :])
-            me[g] = t
-
-        def load(g):
-            load_x(g)
-            load_me(g)
+        def load_me(g, n):
+            t = mein.tile([P, n * G * K], BF16, name="me")
+            nc.sync.dma_start(out=t[:].rearrange("p (i k) -> p i k", k=K), in_=me_hbm[:, g * G : (g + n) * G, :])
+            for j in range(n):
+                me[g + j] = t[:, j * G * K : (j + 1) * G * K]
 
         def vector_slabs(g):
-            return 0 if g == 1 else 2
+            return 0 if g == 2 else 3 if g % 3 == 2 else 2
 
         def widen_vector(g):
             slabs = vector_slabs(g)
-            if slabs == 0:
-                return
             n = slabs * P
             t = work.tile([P, slabs * K], BF16, name="xw_vector")
             nc.vector.tensor_scalar(
@@ -127,10 +122,10 @@ def tile_lstmcell_pa_t_w8_kernel(
                 )
 
         def turn_me(g):
-            words = me[g][:].bitcast(F32)
-            for b, pool in enumerate((pkeep, pmix)):
+            words = me[g].bitcast(F32)
+            for b, (pool, name) in enumerate(((pkeep, "kept"), (pmix, "mix"))):
                 dst = turned[g][:, b * HT * PACK : (b + 1) * HT * PACK].bitcast(F32)
-                pt = pool.tile([P, 2 * HT], F32, name="mix")
+                pt = pool.tile([P, 2 * HT], F32, name=name)
                 if b == 0:
                     mbank[g] = pt
                     bank = pt[:].rearrange("p (c u i) -> p u c i", u=2, i=4)
@@ -155,7 +150,7 @@ def tile_lstmcell_pa_t_w8_kernel(
             s = sig[g]
             for t in ts:
                 cols = slice(t * P, (t + 1) * P)
-                pm = pmix.tile([P, GT], F32, name="mix")
+                pm = px.tile([P, GT], F32, name="xt") if g == GROUPS - 1 and t >= 2 else pmix.tile([P, GT], F32, name="mix")
                 nc.tensor.matmul_mx(
                     out=pm[:], lhsT=wi[:, cols].bitcast(FP8X4), lhsT_scale=ws[:, cols],
                     rhs=q[g][0][:, GT:].bitcast(FP8X4), rhs_scale=q[g][1][:, GT:], start=True, stop=False,
@@ -190,7 +185,7 @@ def tile_lstmcell_pa_t_w8_kernel(
                 out=codes[:, lo:hi].bitcast(FP8X4), scales=scales[:, lo:hi], in_=gated[g][:, lo * PACK : hi * PACK]
             )
 
-        def read_out(g, i0, i1):
+        def read_out(g, i0, i1, copy):
             if g not in res:
                 fresh = outp.tile([P, G, N_OUT], F32, name="res")
                 res[g] = fresh
@@ -204,7 +199,7 @@ def tile_lstmcell_pa_t_w8_kernel(
                         out=po[:, i - b, :], lhsT=gq[g][0][:, cols].bitcast(FP8X4), lhsT_scale=gq[g][1][:, cols],
                         rhs=wt[:].bitcast(FP8X4), rhs_scale=wts[:], start=True, stop=True,
                     )
-                nc.scalar.copy(out=o[:, b:e, :], in_=po[:, 0 : e - b, :])
+                copy(out=o[:, b:e, :], in_=po[:, 0 : e - b, :])
             nc.sync.dma_start(out=out_hbm[:, g * G + i0 : g * G + i1, :], in_=o[:, i0:i1, :])
 
         def permute(dst, src):
@@ -230,19 +225,20 @@ def tile_lstmcell_pa_t_w8_kernel(
         load_x(0)
         nc.sync.dma_start(out=s4[:], in_=x_scale.rearrange("o (p t) -> p (o t)", t=PACK))
         load_words(wi_raw, wi_words)
-        load_x(1)
-        load_me(0)
         load_words(wh_raw, wh_words)
-        load_me(1)
+        load_x(1)
+        load_me(0, 1)
+        load_me(1, 1)
         load_x(2)
         load_scale_rows(nc.sync, ws_raw, 0, wi_scales)
         nc.sync.dma_start(out=bias[:], in_=mem_bias.rearrange("(p t) -> p t", t=PACK))
-        load_me(2)
 
         last = GROUPS - 1
         for s in range(GROUPS + 4):
             if s + AHEAD < GROUPS:
-                load(s + AHEAD)
+                load_x(s + AHEAD)
+            if s % 2 == 0 and s + 2 < GROUPS:
+                load_me(s + 2, 2)
             if s == 1:
                 load_words(wt, wt_words)
                 load_scale_rows(nc.sync, wts, 0, wt_scales)
@@ -250,6 +246,9 @@ def tile_lstmcell_pa_t_w8_kernel(
                 quant_gated(s - 5, 0, GT)
             if s == 1:
                 turn_x(0)
+            if s == 3:
+                scale_x(1)
+                turn_me(1)
             if 0 <= s - 3 < GROUPS:
                 gates(s - 3, (0, 1))
             if 0 <= s - 4:
@@ -260,19 +259,20 @@ def tile_lstmcell_pa_t_w8_kernel(
                     gate(nc.gpsimd, s - 4, 3 * P, GT, False)
                     gate(nc.vector, s - 4, 0, HT, True)
                     gate(nc.vector, s - 4, HT, 3 * P, False)
-            if 0 <= s - 2 < GROUPS:
+            if 0 <= s - 2 < GROUPS and s != 3:
                 scale_x(s - 2)
                 turn_me(s - 2)
             if s == 2:
-                permute(wh[:].bitcast(I32), wh_raw[:].bitcast(I32))
-            elif s < GROUPS:
+                widen_vector(1)
+            elif s < GROUPS and s != 1:
                 widen_vector(s)
             if s == 0:
                 permute(wi[:].bitcast(I32), wi_raw[:].bitcast(I32))
+                permute(wh[:].bitcast(I32), wh_raw[:].bitcast(I32))
             if 0 <= s - 3 < GROUPS:
                 gates(s - 3, (2, 3))
             if 0 <= s - 5:
-                read_out(s - 5, 0, G)
+                read_out(s - 5, 0, G, nc.scalar.copy)
             if 1 <= s - 1 < GROUPS:
                 turn_x(s - 1)
             if s < GROUPS:
@@ -280,9 +280,10 @@ def tile_lstmcell_pa_t_w8_kernel(
             if 0 <= s - 2 < GROUPS:
                 quant_in(s - 2)
             if s == 2:
-                widen_vector(2)
                 permute(ws[:], ws_raw[:])
 
-        for i0, i1 in ((0, 2), (2, 3), (3, 4)):
+        pieces = ((0, 2, nc.scalar.copy), (2, 3, nc.vector.tensor_copy), (3, 4, nc.scalar.copy))
+        for i0, i1, copy in pieces:
             quant_gated(last, i0 * P, i1 * P)
-            read_out(last, i0, i1)
+        for i0, i1, copy in pieces:
+            read_out(last, i0, i1, copy)

@@ -24,7 +24,7 @@ GROUPS = TILES // G
 GT = G * P
 HT = GT // 2
 AHEAD = 3
-VECTOR_TOKENS = 176
+VECTOR_TOKENS = 192
 
 
 def tile_lstmcell_pa_t_w8_kernel(
@@ -49,6 +49,7 @@ def tile_lstmcell_pa_t_w8_kernel(
 
         ident = keep.tile([P, P], F32, name="ident")
         ones = keep.tile([P, 1], F32, name="ones")
+        warm = keep.tile([P, 1], F32, name="warm")
         s4 = keep.tile([P, PACK], F32, name="s4")
         bias = keep.tile([P, PACK], BF16, name="bias")
         wi_raw = keep.tile([P, CH], U32, name="wi_raw", align_bytes=64)
@@ -76,22 +77,21 @@ def tile_lstmcell_pa_t_w8_kernel(
                 me[g + j] = t[:, j * G * K : (j + 1) * G * K]
 
         def vector_slabs(g):
-            return 0 if g == 2 else 3 if g % 3 == 2 else 2
+            return {1: 1, 2: 0}.get(g, 2)
 
-        def widen_vector(g):
-            slabs = vector_slabs(g)
+        def widen_vector(g, first, slabs):
             n = slabs * P
             t = work.tile([P, slabs * K], BF16, name="xw_vector")
             nc.vector.tensor_scalar(
                 out=t[:].rearrange("p (u m e) -> p m u e", u=2, e=2),
-                in0=xb[g][:, 0 : slabs * K].bitcast(FP8).rearrange("p (m u e) -> p m u e", u=2, e=2),
+                in0=xb[g][:, first * K : (first + slabs) * K].bitcast(FP8).rearrange("p (m u e) -> p m u e", u=2, e=2),
                 scalar1=ones[:],
                 scalar2=None,
                 op0=MULT,
             )
             words = t[:].bitcast(F32)
             for i in range(slabs):
-                xw[g, i] = [words[:, u * n + i * P : u * n + (i + 1) * P] for u in range(2)]
+                xw[g, first + i] = [words[:, u * n + i * P : u * n + (i + 1) * P] for u in range(2)]
 
         def widen_scalar(g):
             slabs = vector_slabs(g)
@@ -123,19 +123,18 @@ def tile_lstmcell_pa_t_w8_kernel(
 
         def turn_me(g):
             words = me[g].bitcast(F32)
-            for b, (pool, name) in enumerate(((pkeep, "kept"), (pmix, "mix"))):
+            for b, (pool, name, run) in enumerate(((pkeep, "kept", 2), (pmix, "mix", P))):
                 dst = turned[g][:, b * HT * PACK : (b + 1) * HT * PACK].bitcast(F32)
                 pt = pool.tile([P, 2 * HT], F32, name=name)
-                if b == 0:
-                    mbank[g] = pt
-                    bank = pt[:].rearrange("p (c u i) -> p u c i", u=2, i=4)
-                else:
-                    bank = pt[:].rearrange("p (u c i) -> p u c i", u=2, i=4)
+                bank = pt[:].rearrange("p (c u i) -> p u c i", u=2, i=run)
+                per = P // run
                 for i in range(2):
                     for u in range(2):
                         base = (2 * b + i) * (K // 2)
-                        nc.tensor.transpose(bank[:, u, 32 * i : 32 * (i + 1), :], words[:, base + u : base + K // 2 : 2], ident[:])
-                nc.scalar.copy(out=dst.rearrange("p (c i u) -> p c i u", i=4, u=2), in_=bank.rearrange("p u c i -> p c i u"))
+                        nc.tensor.transpose(bank[:, u, per * i : per * (i + 1), :], words[:, base + u : base + K // 2 : 2], ident[:])
+                nc.scalar.copy(out=dst.rearrange("p (c i u) -> p c i u", i=run, u=2), in_=bank.rearrange("p u c i -> p c i u"))
+                if b == 0:
+                    mbank[g] = pt
 
         def quant_in(g):
             codes = work.tile([P, 2 * GT], U32, name="qc", align_bytes=64)
@@ -165,13 +164,15 @@ def tile_lstmcell_pa_t_w8_kernel(
             gated[g] = gated_last[:] if g == GROUPS - 1 else turned[g + 1][:, GT * PACK :]
             cols = slice(lo * PACK, hi * PACK)
             if from_psum:
-                me_turned = mbank[g][:].bitcast(BF16)[:, cols].rearrange("p (c u i e) -> p c u e i", u=2, i=4, e=2)
+                run = 2
+                me_turned = mbank[g][:].bitcast(BF16)[:, cols].rearrange("p (c u i e) -> p c u e i", u=2, i=run, e=2)
             else:
-                me_turned = turned[g][:, cols].rearrange("p (c i u e) -> p c u e i", i=4, u=2, e=2)
+                run = 4
+                me_turned = turned[g][:, cols].rearrange("p (c i u e) -> p c u e i", i=run, u=2, e=2)
             engine.tensor_tensor(
-                out=gated[g][:, cols].rearrange("p (c i u e) -> p c u e i", i=4, u=2, e=2),
-                in0=sig[g][:, :, lo:hi].rearrange("p (u e) (c i) -> p c u e i", i=4, u=2),
-                in1=me_turned,
+                out=gated[g][:, cols].rearrange("p (c i u e) -> p c u e i", i=run, u=2, e=2),
+                in0=me_turned,
+                in1=sig[g][:, :, lo:hi].rearrange("p (u e) (c i) -> p c u e i", i=run, u=2),
                 op=MULT,
             )
 
@@ -189,26 +190,25 @@ def tile_lstmcell_pa_t_w8_kernel(
             if g not in res:
                 fresh = outp.tile([P, G, N_OUT], F32, name="res")
                 res[g] = fresh
-            o = res[g]
-            for b in range(i0, i1, 2):
-                e = min(b + 2, i1)
-                po = pmix.tile([P, 2, N_OUT], F32, name="mix")
-                for i in range(b, e):
-                    cols = slice(i * P, (i + 1) * P)
-                    nc.tensor.matmul_mx(
-                        out=po[:, i - b, :], lhsT=gq[g][0][:, cols].bitcast(FP8X4), lhsT_scale=gq[g][1][:, cols],
-                        rhs=wt[:].bitcast(FP8X4), rhs_scale=wts[:], start=True, stop=True,
-                    )
-                copy(out=o[:, b:e, :], in_=po[:, 0 : e - b, :])
-            nc.sync.dma_start(out=out_hbm[:, g * G + i0 : g * G + i1, :], in_=o[:, i0:i1, :])
+            po = pmix.tile([P, 2, N_OUT], F32, name="mix")
+            for i in range(i0, i1):
+                cols = slice(i * P, (i + 1) * P)
+                nc.tensor.matmul_mx(
+                    out=po[:, i - i0, :], lhsT=gq[g][0][:, cols].bitcast(FP8X4), lhsT_scale=gq[g][1][:, cols],
+                    rhs=wt[:].bitcast(FP8X4), rhs_scale=wts[:], start=True, stop=True,
+                )
+            copy(out=res[g][:, i0:i1, :], in_=po[:, 0 : i1 - i0, :])
+
+        def store(g, i0, i1):
+            nc.sync.dma_start(out=out_hbm[:, g * G + i0 : g * G + i1, :], in_=res[g][:, i0:i1, :])
 
         def permute(dst, src):
             nc.vector.tensor_copy(
                 out=dst.rearrange("p (t m) -> p t m", t=PACK), in_=src.rearrange("p (m t) -> p t m", t=PACK)
             )
 
-        def load_scale_rows(queue, tile, row0, hbm):
-            for h in range(4):
+        def load_scale_rows(queue, tile, row0, hbm, quadrants):
+            for h in quadrants:
                 queue.dma_start(
                     out=tile[32 * h + row0 : 32 * h + row0 + 4, :].bitcast(I32), in_=hbm[0, 4 * h : 4 * h + 4, :].bitcast(I32)
                 )
@@ -217,9 +217,10 @@ def tile_lstmcell_pa_t_w8_kernel(
             nc.sync.dma_start(out=tile[:].bitcast(I32), in_=hbm[0].rearrange("p n t -> p (n t)").bitcast(I32))
 
         nc.gpsimd.memset(ones[:], 1.0)
+        nc.scalar.activation(out=warm[:], in_=ones[:], func=ACT.Sigmoid)
         nc.gpsimd.memset(ws_raw[:].bitcast(I32), 0)
         make_identity(nc, ident[:])
-        load_scale_rows(nc.gpsimd, ws_raw, 4, wh_scales)
+        load_scale_rows(nc.gpsimd, ws_raw, 4, wh_scales, (0, 1))
         nc.gpsimd.memset(wts[:].bitcast(I32), 0)
 
         load_x(0)
@@ -230,7 +231,8 @@ def tile_lstmcell_pa_t_w8_kernel(
         load_me(0, 1)
         load_me(1, 1)
         load_x(2)
-        load_scale_rows(nc.sync, ws_raw, 0, wi_scales)
+        load_scale_rows(nc.sync, ws_raw, 0, wi_scales, range(4))
+        load_scale_rows(nc.sync, ws_raw, 4, wh_scales, (2, 3))
         nc.sync.dma_start(out=bias[:], in_=mem_bias.rearrange("(p t) -> p t", t=PACK))
 
         last = GROUPS - 1
@@ -241,7 +243,7 @@ def tile_lstmcell_pa_t_w8_kernel(
                 load_me(s + 2, 2)
             if s == 1:
                 load_words(wt, wt_words)
-                load_scale_rows(nc.sync, wts, 0, wt_scales)
+                load_scale_rows(nc.sync, wts, 0, wt_scales, range(4))
             if 0 <= s - 5:
                 quant_gated(s - 5, 0, GT)
             if s == 1:
@@ -263,16 +265,20 @@ def tile_lstmcell_pa_t_w8_kernel(
                 scale_x(s - 2)
                 turn_me(s - 2)
             if s == 2:
-                widen_vector(1)
-            elif s < GROUPS and s != 1:
-                widen_vector(s)
+                widen_vector(1, 0, vector_slabs(1))
+            elif 3 <= s < GROUPS:
+                widen_vector(s, 0, vector_slabs(s))
             if s == 0:
+                widen_vector(0, 0, 1)
+                widen_vector(0, 1, 1)
                 permute(wi[:].bitcast(I32), wi_raw[:].bitcast(I32))
                 permute(wh[:].bitcast(I32), wh_raw[:].bitcast(I32))
             if 0 <= s - 3 < GROUPS:
                 gates(s - 3, (2, 3))
             if 0 <= s - 5:
-                read_out(s - 5, 0, G, nc.scalar.copy)
+                read_out(s - 5, 0, 2, nc.scalar.copy)
+                read_out(s - 5, 2, 4, nc.scalar.copy)
+                store(s - 5, 0, G)
             if 1 <= s - 1 < GROUPS:
                 turn_x(s - 1)
             if s < GROUPS:
@@ -282,8 +288,8 @@ def tile_lstmcell_pa_t_w8_kernel(
             if s == 2:
                 permute(ws[:], ws_raw[:])
 
-        pieces = ((0, 2, nc.scalar.copy), (2, 3, nc.vector.tensor_copy), (3, 4, nc.scalar.copy))
-        for i0, i1, copy in pieces:
-            quant_gated(last, i0 * P, i1 * P)
-        for i0, i1, copy in pieces:
-            read_out(last, i0, i1, copy)
+        for lo, hi in ((0, 2 * P), (2 * P, 3 * P), (3 * P, 4 * P)):
+            quant_gated(last, lo, hi)
+        for i in range(G):
+            read_out(last, i, i + 1, nc.vector.tensor_copy if i % 2 else nc.scalar.copy)
+            store(last, i, i + 1)

@@ -77,7 +77,7 @@ def tile_lstmcell_pa_t_w8_kernel(
                 me[g + j] = t[:, j * G * K : (j + 1) * G * K]
 
         def vector_slabs(g):
-            return {1: 1, 2: 0}.get(g, 2)
+            return {0: 2, 2: 0}.get(g, 1)
 
         def widen_vector(g, first, slabs):
             n = slabs * P

@@ -24,7 +24,8 @@ GROUPS = TILES // G
 GT = G * P
 HT = GT // 2
 AHEAD = 3
-VECTOR_TOKENS = 192
+VECTOR_TOKENS = 144
+NARROW_TOKENS = 192
 
 
 def tile_lstmcell_pa_t_w8_kernel(
@@ -42,9 +43,9 @@ def tile_lstmcell_pa_t_w8_kernel(
         work = ctx.enter_context(tc.tile_pool(name="work", bufs=3))
         turnp = ctx.enter_context(tc.tile_pool(name="turnp", bufs=5))
         outp = ctx.enter_context(tc.tile_pool(name="outp", bufs=4))
-        px = ctx.enter_context(tc.psum_pool(name="px", bufs=2))
         pkeep = ctx.enter_context(tc.psum_pool(name="pkeep", bufs=2))
-        pmix = ctx.enter_context(tc.psum_pool(name="pmix", bufs=4))
+        pmix = ctx.enter_context(tc.psum_pool(name="pmix", bufs=5))
+        plate = ctx.enter_context(tc.psum_pool(name="plate", bufs=1))
         ctx.enter_context(tc.manual_schedule())
 
         ident = keep.tile([P, P], F32, name="ident")
@@ -59,11 +60,10 @@ def tile_lstmcell_pa_t_w8_kernel(
         wt = keep.tile([P, N_OUT], U32, name="wt", align_bytes=64)
         ws_raw = keep.tile([P, CH], U8, name="ws_raw", align_bytes=64)
         ws = keep.tile([P, CH], U8, name="ws", align_bytes=64)
-        gated_last = keep.tile([P, GT * PACK], BF16, name="gated_last", align_bytes=64)
         wts = keep.tile([P, N_OUT], U8, name="wts", align_bytes=64)
 
         xb, me, xw, xbank, mbank, turned, q = {}, {}, {}, {}, {}, {}, {}
-        sig, gated, gq, res = {}, {}, {}, {}
+        sig, gated, gq, res, obank = {}, {}, {}, {}, {}
 
         def load_x(g):
             t = xin.tile([P, G * K], U8, name="xb")
@@ -75,9 +75,6 @@ def tile_lstmcell_pa_t_w8_kernel(
             nc.sync.dma_start(out=t[:].rearrange("p (i k) -> p i k", k=K), in_=me_hbm[:, g * G : (g + n) * G, :])
             for j in range(n):
                 me[g + j] = t[:, j * G * K : (j + 1) * G * K]
-
-        def vector_slabs(g):
-            return {0: 2, 2: 0}.get(g, 1)
 
         def widen_vector(g, first, slabs):
             n = slabs * P
@@ -93,37 +90,39 @@ def tile_lstmcell_pa_t_w8_kernel(
             for i in range(slabs):
                 xw[g, first + i] = [words[:, u * n + i * P : u * n + (i + 1) * P] for u in range(2)]
 
-        def widen_scalar(g):
-            slabs = vector_slabs(g)
-            t = work.tile([P, (G - slabs) * K], BF16, name="xw_scalar")
-            nc.scalar.copy(out=t[:], in_=xb[g][:, slabs * K :].bitcast(FP8))
+        def widen_scalar(g, first):
+            t = work.tile([P, (G - first) * K], BF16, name="xw_scalar")
+            nc.scalar.copy(out=t[:], in_=xb[g][:, first * K :].bitcast(FP8))
             words = t[:].bitcast(F32)
-            for i in range(G - slabs):
-                xw[g, slabs + i] = [words[:, i * HT + u : (i + 1) * HT : 2] for u in range(2)]
+            for i in range(G - first):
+                xw[g, first + i] = [words[:, i * HT + u : (i + 1) * HT : 2] for u in range(2)]
 
-        def turn_x(g):
-            for b in range(2):
-                pt = px.tile([P, 2, 2, P], F32, name="xt")
+        def turn_x(g, banks=(0, 1)):
+            for b in banks:
+                pt = pmix.tile([P, 2 * HT], F32, name="mix")
+                bank = pt[:].rearrange("p (u i r) -> p u i r", u=2, i=2)
                 for i in range(2):
                     for u in range(2):
-                        nc.tensor.transpose(pt[:, u, i, :], xw[g, 2 * b + i][u], ident[:])
+                        nc.tensor.transpose(bank[:, u, i, :], xw[g, 2 * b + i][u], ident[:])
                 xbank[g, b] = pt
 
-        def scale_x(g):
-            t = turnp.tile([P, 2 * GT * PACK], BF16, name="turned", align_bytes=64)
-            turned[g] = t
-            for b in range(2):
+        def scale_x(g, banks=(0, 1)):
+            if g not in turned:
+                t = turnp.tile([P, 2 * GT * PACK], BF16, name="turned", align_bytes=64)
+                turned[g] = t
+            for b in banks:
                 lo = (GT + b * HT) * PACK
                 nc.vector.tensor_tensor(
                     out=turned[g][:, lo : lo + HT * PACK].rearrange("p (m u e) -> p m u e", u=2, e=2),
-                    in0=xbank[g, b][:].rearrange("p u i r -> p (u i r)").bitcast(BF16).rearrange("p (u m e) -> p m u e", u=2, e=2),
+                    in0=xbank[g, b][:].bitcast(BF16).rearrange("p (u m e) -> p m u e", u=2, e=2),
                     in1=s4[:].rearrange("p (u e) -> p u e", u=2).unsqueeze(1).to_broadcast([P, HT, 2, 2]),
                     op=MULT,
                 )
 
         def turn_me(g):
             words = me[g].bitcast(F32)
-            for b, (pool, name, run) in enumerate(((pkeep, "kept", 2), (pmix, "mix", P))):
+            hold = (plate, "late") if g == 2 else (pkeep, "kept")
+            for b, (pool, name), run in ((1, (pmix, "mix"), P), (0, hold, 2)):
                 dst = turned[g][:, b * HT * PACK : (b + 1) * HT * PACK].bitcast(F32)
                 pt = pool.tile([P, 2 * HT], F32, name=name)
                 bank = pt[:].rearrange("p (c u i) -> p u c i", u=2, i=run)
@@ -142,14 +141,12 @@ def tile_lstmcell_pa_t_w8_kernel(
             nc.vector.quantize_mx(out=codes[:].bitcast(FP8X4), scales=scales[:], in_=turned[g][:])
             q[g] = (codes, scales)
 
-        def gates(g, ts):
-            if g not in sig:
-                s = work.tile([P, PACK, GT], F32, name="sig")
-                sig[g] = s
-            s = sig[g]
-            for t in ts:
+        def gates(g):
+            s = work.tile([P, PACK, GT], F32, name="sig")
+            sig[g] = s
+            for t in range(PACK):
                 cols = slice(t * P, (t + 1) * P)
-                pm = px.tile([P, GT], F32, name="xt") if g == GROUPS - 1 and t >= 2 else pmix.tile([P, GT], F32, name="mix")
+                pm = pmix.tile([P, GT], F32, name="mix")
                 nc.tensor.matmul_mx(
                     out=pm[:], lhsT=wi[:, cols].bitcast(FP8X4), lhsT_scale=ws[:, cols],
                     rhs=q[g][0][:, GT:].bitcast(FP8X4), rhs_scale=q[g][1][:, GT:], start=True, stop=False,
@@ -161,7 +158,7 @@ def tile_lstmcell_pa_t_w8_kernel(
                 nc.scalar.activation(out=s[:, t, :], in_=pm[:], func=ACT.Sigmoid, bias=bias[:, t : t + 1])
 
         def gate(engine, g, lo, hi, from_psum):
-            gated[g] = gated_last[:] if g == GROUPS - 1 else turned[g + 1][:, GT * PACK :]
+            gated[g] = turned[g - 1][:, : GT * PACK] if g == GROUPS - 1 else turned[g + 1][:, GT * PACK :]
             cols = slice(lo * PACK, hi * PACK)
             if from_psum:
                 run = 2
@@ -186,26 +183,27 @@ def tile_lstmcell_pa_t_w8_kernel(
                 out=codes[:, lo:hi].bitcast(FP8X4), scales=scales[:, lo:hi], in_=gated[g][:, lo * PACK : hi * PACK]
             )
 
-        def read_out(g, i0, i1, copy):
+        def read_out(g, i0, i1, late=False):
             if g not in res:
                 fresh = outp.tile([P, G, N_OUT], F32, name="res")
                 res[g] = fresh
-            po = pmix.tile([P, 2, N_OUT], F32, name="mix")
+            po = plate.tile([P, 2 * N_OUT], F32, name="late") if late else pmix.tile([P, 2 * N_OUT], F32, name="mix")
             for i in range(i0, i1):
                 cols = slice(i * P, (i + 1) * P)
                 nc.tensor.matmul_mx(
-                    out=po[:, i - i0, :], lhsT=gq[g][0][:, cols].bitcast(FP8X4), lhsT_scale=gq[g][1][:, cols],
+                    out=po[:, (i - i0) * N_OUT : (i - i0 + 1) * N_OUT], lhsT=gq[g][0][:, cols].bitcast(FP8X4), lhsT_scale=gq[g][1][:, cols],
                     rhs=wt[:].bitcast(FP8X4), rhs_scale=wts[:], start=True, stop=True,
                 )
-            copy(out=res[g][:, i0:i1, :], in_=po[:, 0 : i1 - i0, :])
+            obank[g, i0] = po[:, 0 : (i1 - i0) * N_OUT]
+
+        def empty_out(g, i0, i1, copy):
+            copy(out=res[g][:, i0:i1, :].rearrange("p i n -> p (i n)"), in_=obank[g, i0])
 
         def store(g, i0, i1):
             nc.sync.dma_start(out=out_hbm[:, g * G + i0 : g * G + i1, :], in_=res[g][:, i0:i1, :])
 
-        def permute(dst, src):
-            nc.vector.tensor_copy(
-                out=dst.rearrange("p (t m) -> p t m", t=PACK), in_=src.rearrange("p (m t) -> p t m", t=PACK)
-            )
+        def permute(copy, dst, src):
+            copy(out=dst.rearrange("p (t m) -> p t m", t=PACK), in_=src.rearrange("p (m t) -> p t m", t=PACK))
 
         def load_scale_rows(queue, tile, row0, hbm, quadrants):
             for h in quadrants:
@@ -220,76 +218,102 @@ def tile_lstmcell_pa_t_w8_kernel(
         nc.scalar.activation(out=warm[:], in_=ones[:], func=ACT.Sigmoid)
         nc.gpsimd.memset(ws_raw[:].bitcast(I32), 0)
         make_identity(nc, ident[:])
-        load_scale_rows(nc.gpsimd, ws_raw, 4, wh_scales, (0, 1))
-        nc.gpsimd.memset(wts[:].bitcast(I32), 0)
+        load_scale_rows(nc.gpsimd, ws_raw, 4, wh_scales, range(3))
 
         load_x(0)
         nc.sync.dma_start(out=s4[:], in_=x_scale.rearrange("o (p t) -> p (o t)", t=PACK))
+        load_me(0, 1)
+        load_x(1)
+        load_scale_rows(nc.sync, ws_raw, 0, wi_scales, range(4))
+        load_scale_rows(nc.sync, ws_raw, 4, wh_scales, (3,))
+        load_me(1, 1)
         load_words(wi_raw, wi_words)
         load_words(wh_raw, wh_words)
-        load_x(1)
-        load_me(0, 1)
-        load_me(1, 1)
         load_x(2)
-        load_scale_rows(nc.sync, ws_raw, 0, wi_scales, range(4))
-        load_scale_rows(nc.sync, ws_raw, 4, wh_scales, (2, 3))
         nc.sync.dma_start(out=bias[:], in_=mem_bias.rearrange("(p t) -> p t", t=PACK))
 
-        last = GROUPS - 1
-        for s in range(GROUPS + 4):
+        def loads(s):
             if s + AHEAD < GROUPS:
                 load_x(s + AHEAD)
             if s % 2 == 0 and s + 2 < GROUPS:
                 load_me(s + 2, 2)
-            if s == 1:
-                load_words(wt, wt_words)
-                load_scale_rows(nc.sync, wts, 0, wt_scales, range(4))
-            if 0 <= s - 5:
-                quant_gated(s - 5, 0, GT)
-            if s == 1:
-                turn_x(0)
-            if s == 3:
-                scale_x(1)
-                turn_me(1)
-            if 0 <= s - 3 < GROUPS:
-                gates(s - 3, (0, 1))
-            if 0 <= s - 4:
-                if s - 2 < GROUPS:
-                    gate(nc.gpsimd, s - 4, VECTOR_TOKENS, GT, False)
-                    gate(nc.vector, s - 4, 0, VECTOR_TOKENS, True)
-                else:
-                    gate(nc.gpsimd, s - 4, 3 * P, GT, False)
-                    gate(nc.vector, s - 4, 0, HT, True)
-                    gate(nc.vector, s - 4, HT, 3 * P, False)
-            if 0 <= s - 2 < GROUPS and s != 3:
-                scale_x(s - 2)
-                turn_me(s - 2)
-            if s == 2:
-                widen_vector(1, 0, vector_slabs(1))
-            elif 3 <= s < GROUPS:
-                widen_vector(s, 0, vector_slabs(s))
-            if s == 0:
-                widen_vector(0, 0, 1)
-                widen_vector(0, 1, 1)
-                permute(wi[:].bitcast(I32), wi_raw[:].bitcast(I32))
-                permute(wh[:].bitcast(I32), wh_raw[:].bitcast(I32))
-            if 0 <= s - 3 < GROUPS:
-                gates(s - 3, (2, 3))
-            if 0 <= s - 5:
-                read_out(s - 5, 0, 2, nc.scalar.copy)
-                read_out(s - 5, 2, 4, nc.scalar.copy)
-                store(s - 5, 0, G)
-            if 1 <= s - 1 < GROUPS:
-                turn_x(s - 1)
-            if s < GROUPS:
-                widen_scalar(s)
-            if 0 <= s - 2 < GROUPS:
-                quant_in(s - 2)
-            if s == 2:
-                permute(ws[:], ws_raw[:])
 
-        for lo, hi in ((0, 2 * P), (2 * P, 3 * P), (3 * P, 4 * P)):
+        last = GROUPS - 1
+
+        loads(0)
+        loads(1)
+        loads(2)
+        widen_vector(0, 0, 1)
+        widen_vector(0, 1, 1)
+        nc.vector.memset(wts[:].bitcast(I32), 0)
+        widen_scalar(0, 2)
+        turn_x(0)
+        widen_scalar(1, 0)
+        scale_x(0)
+        turn_me(0)
+        permute(nc.vector.tensor_copy, ws[:], ws_raw[:])
+        permute(nc.scalar.copy, wi[:], wi_raw[:])
+        permute(nc.scalar.copy, wh[:], wh_raw[:])
+        turn_x(1)
+        widen_scalar(2, 0)
+        quant_in(0)
+        scale_x(1)
+        turn_me(1)
+        quant_in(1)
+        load_words(wt, wt_words)
+        load_scale_rows(nc.sync, wts, 0, wt_scales, range(4))
+
+        for s in range(3, GROUPS + 1):
+            cast, turn, mix, leave = s, s - 1, s - 3, s - 5
+            loads(s)
+            shared = 1 <= leave and cast < GROUPS
+            share = VECTOR_TOKENS if shared else NARROW_TOKENS
+            gates(mix)
+            gate(nc.gpsimd, mix, share, GT, False)
+            gate(nc.vector, mix, 0, share, True)
+            if 0 <= leave:
+                read_out(leave, 0, 2)
+                empty_out(leave, 0, 2, nc.scalar.copy)
+                read_out(leave, 2, 4, shared)
+                if not shared:
+                    empty_out(leave, 2, 4, nc.scalar.copy)
+            turn_x(turn)
+            if cast < GROUPS:
+                widen_scalar(cast, 0)
+            scale_x(turn)
+            if shared:
+                empty_out(leave, 2, 4, nc.vector.tensor_copy)
+            if 0 <= leave:
+                store(leave, 0, G)
+            turn_me(turn)
+            quant_in(turn)
+            quant_gated(mix, 0, GT)
+
+        def leave_by_scalar(g):
+            for i in (0, 2):
+                read_out(g, i, i + 2)
+                empty_out(g, i, i + 2, nc.scalar.copy)
+            store(g, 0, G)
+
+        gates(last - 1)
+        gate(nc.gpsimd, last - 1, 3 * P, GT, False)
+        gate(nc.vector, last - 1, 0, HT, True)
+        read_out(last - 3, 0, 2)
+        empty_out(last - 3, 0, 2, nc.scalar.copy)
+        read_out(last - 3, 2, 4, True)
+        empty_out(last - 3, 2, 4, nc.vector.tensor_copy)
+        store(last - 3, 0, G)
+        gates(last)
+        gate(nc.vector, last - 1, HT, 3 * P, False)
+        quant_gated(last - 1, 0, GT)
+        leave_by_scalar(last - 2)
+        gate(nc.gpsimd, last, HT, 3 * P, False)
+        gate(nc.vector, last, 0, HT, True)
+        leave_by_scalar(last - 1)
+        gate(nc.vector, last, 3 * P, GT, False)
+        for lo, hi in ((0, 2 * P), (2 * P, 4 * P)):
             quant_gated(last, lo, hi)
         for i in range(G):
-            read_out(last, i, i + 1, nc.vector.tensor_copy if i % 2 else nc.scalar.copy)
+            read_out(last, i, i + 1)
+            empty_out(last, i, i + 1, nc.vector.tensor_copy if i % 2 else nc.scalar.copy)
             store(last, i, i + 1)

@@ -44,7 +44,7 @@ def tile_lstmcell_pa_t_w8_kernel(
         turnp = ctx.enter_context(tc.tile_pool(name="turnp", bufs=5))
         outp = ctx.enter_context(tc.tile_pool(name="outp", bufs=4))
         pkeep = ctx.enter_context(tc.psum_pool(name="pkeep", bufs=2))
-        pmix = ctx.enter_context(tc.psum_pool(name="pmix", bufs=5))
+        pmix = ctx.enter_context(tc.psum_pool(name="pmix", bufs=1))
         plate = ctx.enter_context(tc.psum_pool(name="plate", bufs=1))
         ctx.enter_context(tc.manual_schedule())
 
@@ -64,6 +64,12 @@ def tile_lstmcell_pa_t_w8_kernel(
 
         xb, me, xw, xbank, mbank, turned, q = {}, {}, {}, {}, {}, {}, {}
         sig, gated, gq, res, obank = {}, {}, {}, {}, {}
+
+        free_banks = ["bank%d" % i for i in range(5)]
+
+        def take_bank():
+            name = free_banks.pop(0)
+            return pmix.tile([P, GT], F32, name=name), name
 
         def load_x(g):
             t = xin.tile([P, G * K], U8, name="xb")
@@ -98,33 +104,37 @@ def tile_lstmcell_pa_t_w8_kernel(
                 xw[g, first + i] = [words[:, i * HT + u : (i + 1) * HT : 2] for u in range(2)]
 
         def turn_x(g, banks=(0, 1)):
+            t = turnp.tile([P, 2 * GT * PACK], BF16, name="turned", align_bytes=64)
+            turned[g] = t
             for b in banks:
-                pt = pmix.tile([P, 2 * HT], F32, name="mix")
+                pt, name = take_bank()
                 bank = pt[:].rearrange("p (u i r) -> p u i r", u=2, i=2)
                 for i in range(2):
                     for u in range(2):
                         nc.tensor.transpose(bank[:, u, i, :], xw[g, 2 * b + i][u], ident[:])
-                xbank[g, b] = pt
+                xbank[g, b] = (pt, name)
 
         def scale_x(g, banks=(0, 1)):
-            if g not in turned:
-                t = turnp.tile([P, 2 * GT * PACK], BF16, name="turned", align_bytes=64)
-                turned[g] = t
             for b in banks:
                 lo = (GT + b * HT) * PACK
                 nc.vector.tensor_tensor(
                     out=turned[g][:, lo : lo + HT * PACK].rearrange("p (m u e) -> p m u e", u=2, e=2),
-                    in0=xbank[g, b][:].bitcast(BF16).rearrange("p (u m e) -> p m u e", u=2, e=2),
+                    in0=xbank[g, b][0][:].bitcast(BF16).rearrange("p (u m e) -> p m u e", u=2, e=2),
                     in1=s4[:].rearrange("p (u e) -> p u e", u=2).unsqueeze(1).to_broadcast([P, HT, 2, 2]),
                     op=MULT,
                 )
+                free_banks.append(xbank[g, b][1])
 
         def turn_me(g):
             words = me[g].bitcast(F32)
-            hold = (plate, "late") if g == 2 else (pkeep, "kept")
-            for b, (pool, name), run in ((1, (pmix, "mix"), P), (0, hold, 2)):
+            for b, run in ((1, P), (0, 2)):
                 dst = turned[g][:, b * HT * PACK : (b + 1) * HT * PACK].bitcast(F32)
-                pt = pool.tile([P, 2 * HT], F32, name=name)
+                if b == 1:
+                    pt, name = take_bank()
+                elif g == 2:
+                    pt = plate.tile([P, GT], F32, name="late")
+                else:
+                    pt = pkeep.tile([P, GT], F32, name="kept")
                 bank = pt[:].rearrange("p (c u i) -> p u c i", u=2, i=run)
                 per = P // run
                 for i in range(2):
@@ -134,6 +144,8 @@ def tile_lstmcell_pa_t_w8_kernel(
                 nc.scalar.copy(out=dst.rearrange("p (c i u) -> p c i u", i=run, u=2), in_=bank.rearrange("p u c i -> p c i u"))
                 if b == 0:
                     mbank[g] = pt
+                else:
+                    free_banks.append(name)
 
         def quant_in(g):
             codes = work.tile([P, 2 * GT], U32, name="qc", align_bytes=64)
@@ -141,12 +153,14 @@ def tile_lstmcell_pa_t_w8_kernel(
             nc.vector.quantize_mx(out=codes[:].bitcast(FP8X4), scales=scales[:], in_=turned[g][:])
             q[g] = (codes, scales)
 
-        def gates(g):
-            s = work.tile([P, PACK, GT], F32, name="sig")
-            sig[g] = s
-            for t in range(PACK):
+        def gates(g, ts=range(PACK)):
+            if g not in sig:
+                fresh = work.tile([P, PACK, GT], F32, name="sig")
+                sig[g] = fresh
+            s = sig[g]
+            for t in ts:
                 cols = slice(t * P, (t + 1) * P)
-                pm = pmix.tile([P, GT], F32, name="mix")
+                pm, name = take_bank()
                 nc.tensor.matmul_mx(
                     out=pm[:], lhsT=wi[:, cols].bitcast(FP8X4), lhsT_scale=ws[:, cols],
                     rhs=q[g][0][:, GT:].bitcast(FP8X4), rhs_scale=q[g][1][:, GT:], start=True, stop=False,
@@ -156,6 +170,7 @@ def tile_lstmcell_pa_t_w8_kernel(
                     rhs=q[g][0][:, 0:GT].bitcast(FP8X4), rhs_scale=q[g][1][:, 0:GT], start=False, stop=True,
                 )
                 nc.scalar.activation(out=s[:, t, :], in_=pm[:], func=ACT.Sigmoid, bias=bias[:, t : t + 1])
+                free_banks.append(name)
 
         def gate(engine, g, lo, hi, from_psum):
             gated[g] = turned[g - 1][:, : GT * PACK] if g == GROUPS - 1 else turned[g + 1][:, GT * PACK :]
@@ -187,17 +202,19 @@ def tile_lstmcell_pa_t_w8_kernel(
             if g not in res:
                 fresh = outp.tile([P, G, N_OUT], F32, name="res")
                 res[g] = fresh
-            po = plate.tile([P, 2 * N_OUT], F32, name="late") if late else pmix.tile([P, 2 * N_OUT], F32, name="mix")
+            po, name = (plate.tile([P, GT], F32, name="late"), None) if late else take_bank()
             for i in range(i0, i1):
                 cols = slice(i * P, (i + 1) * P)
                 nc.tensor.matmul_mx(
                     out=po[:, (i - i0) * N_OUT : (i - i0 + 1) * N_OUT], lhsT=gq[g][0][:, cols].bitcast(FP8X4), lhsT_scale=gq[g][1][:, cols],
                     rhs=wt[:].bitcast(FP8X4), rhs_scale=wts[:], start=True, stop=True,
                 )
-            obank[g, i0] = po[:, 0 : (i1 - i0) * N_OUT]
+            obank[g, i0] = (po[:, 0 : (i1 - i0) * N_OUT], name)
 
         def empty_out(g, i0, i1, copy):
-            copy(out=res[g][:, i0:i1, :].rearrange("p i n -> p (i n)"), in_=obank[g, i0])
+            copy(out=res[g][:, i0:i1, :].rearrange("p i n -> p (i n)"), in_=obank[g, i0][0])
+            if obank[g, i0][1]:
+                free_banks.append(obank[g, i0][1])
 
         def store(g, i0, i1):
             nc.sync.dma_start(out=out_hbm[:, g * G + i0 : g * G + i1, :], in_=res[g][:, i0:i1, :])
@@ -271,21 +288,21 @@ def tile_lstmcell_pa_t_w8_kernel(
             gates(mix)
             gate(nc.gpsimd, mix, share, GT, False)
             gate(nc.vector, mix, 0, share, True)
+            turn_x(turn)
+            if cast < GROUPS:
+                widen_scalar(cast, 0)
             if 0 <= leave:
                 read_out(leave, 0, 2)
                 empty_out(leave, 0, 2, nc.scalar.copy)
                 read_out(leave, 2, 4, shared)
                 if not shared:
                     empty_out(leave, 2, 4, nc.scalar.copy)
-            turn_x(turn)
-            if cast < GROUPS:
-                widen_scalar(cast, 0)
+            turn_me(turn)
             scale_x(turn)
             if shared:
                 empty_out(leave, 2, 4, nc.vector.tensor_copy)
             if 0 <= leave:
                 store(leave, 0, G)
-            turn_me(turn)
             quant_in(turn)
             quant_gated(mix, 0, GT)
 

@@ -49,6 +49,7 @@ def tile_lstmcell_pa_t_w8_kernel(
         ctx.enter_context(tc.manual_schedule())
 
         ident = keep.tile([P, P], F32, name="ident")
+        ident_bf = keep.tile([P, P], BF16, name="ident_bf")
         ones = keep.tile([P, 1], F32, name="ones")
         warm = keep.tile([P, 1], F32, name="warm")
         s4 = keep.tile([P, PACK], F32, name="s4")
@@ -101,28 +102,46 @@ def tile_lstmcell_pa_t_w8_kernel(
             nc.scalar.copy(out=t[:], in_=xb[g][:, first * K :].bitcast(FP8))
             words = t[:].bitcast(F32)
             for i in range(G - first):
-                xw[g, first + i] = [words[:, i * HT + u : (i + 1) * HT : 2] for u in range(2)]
+                if g == 0:
+                    xw[g, first + i] = [words[:, i * HT + u : (i + 1) * HT : 2] for u in range(2)]
+                else:
+                    xw[g, i] = [t[:, i * K + j : (i + 1) * K : PACK] for j in range(PACK)]
 
         def turn_x(g, banks=(0, 1)):
             t = turnp.tile([P, 2 * GT * PACK], BF16, name="turned", align_bytes=64)
             turned[g] = t
             for b in banks:
                 pt, name = take_bank()
-                bank = pt[:].rearrange("p (u i r) -> p u i r", u=2, i=2)
-                for i in range(2):
-                    for u in range(2):
-                        nc.tensor.transpose(bank[:, u, i, :], xw[g, 2 * b + i][u], ident[:])
+                if g == 0:
+                    bank = pt[:].rearrange("p (u i r) -> p u i r", u=2, i=2)
+                    for i in range(2):
+                        for u in range(2):
+                            nc.tensor.transpose(bank[:, u, i, :], xw[g, 2 * b + i][u], ident[:])
+                else:
+                    bank = pt[:].bitcast(BF16).rearrange("p (i c j r) -> p i j c r", i=2, j=PACK, r=2)
+                    for i in range(2):
+                        for j in range(PACK):
+                            nc.tensor.matmul(bank[:, i, j, :, :], lhsT=xw[g, 2 * b + i][j], rhs=ident_bf[:], start=True, stop=True)
                 xbank[g, b] = (pt, name)
 
         def scale_x(g, banks=(0, 1)):
             for b in banks:
                 lo = (GT + b * HT) * PACK
-                nc.vector.tensor_tensor(
-                    out=turned[g][:, lo : lo + HT * PACK].rearrange("p (m u e) -> p m u e", u=2, e=2),
-                    in0=xbank[g, b][0][:].bitcast(BF16).rearrange("p (u m e) -> p m u e", u=2, e=2),
-                    in1=s4[:].rearrange("p (u e) -> p u e", u=2).unsqueeze(1).to_broadcast([P, HT, 2, 2]),
-                    op=MULT,
-                )
+                dst, src = turned[g][:, lo : lo + HT * PACK], xbank[g, b][0][:].bitcast(BF16)
+                if g == 0:
+                    nc.vector.tensor_tensor(
+                        out=dst.rearrange("p (m u e) -> p m u e", u=2, e=2),
+                        in0=src.rearrange("p (u m e) -> p m u e", u=2, e=2),
+                        in1=s4[:].rearrange("p (u e) -> p u e", u=2).unsqueeze(1).to_broadcast([P, HT, 2, 2]),
+                        op=MULT,
+                    )
+                else:
+                    nc.vector.tensor_tensor(
+                        out=dst.rearrange("p (c r j) -> p c r j", r=2, j=PACK),
+                        in0=src.rearrange("p (c j r) -> p c r j", r=2, j=PACK),
+                        in1=s4[:].unsqueeze(1).unsqueeze(1).to_broadcast([P, HT // 2, 2, PACK]),
+                        op=MULT,
+                    )
                 free_banks.append(xbank[g, b][1])
 
         def turn_me(g):
@@ -263,6 +282,7 @@ def tile_lstmcell_pa_t_w8_kernel(
         widen_vector(0, 0, 1)
         widen_vector(0, 1, 1)
         nc.vector.memset(wts[:].bitcast(I32), 0)
+        nc.vector.tensor_copy(out=ident_bf[:], in_=ident[:])
         widen_scalar(0, 2)
         turn_x(0)
         widen_scalar(1, 0)
@@ -288,15 +308,15 @@ def tile_lstmcell_pa_t_w8_kernel(
             gates(mix)
             gate(nc.gpsimd, mix, share, GT, False)
             gate(nc.vector, mix, 0, share, True)
-            turn_x(turn)
-            if cast < GROUPS:
-                widen_scalar(cast, 0)
             if 0 <= leave:
                 read_out(leave, 0, 2)
                 empty_out(leave, 0, 2, nc.scalar.copy)
                 read_out(leave, 2, 4, shared)
                 if not shared:
                     empty_out(leave, 2, 4, nc.scalar.copy)
+            turn_x(turn)
+            if cast < GROUPS:
+                widen_scalar(cast, 0)
             turn_me(turn)
             scale_x(turn)
             if shared:

@@ -24,8 +24,10 @@ GROUPS = TILES // G
 GT = G * P
 HT = GT // 2
 AHEAD = 3
-VECTOR_TOKENS = 144
-NARROW_TOKENS = 192
+VECTOR_TOKENS = 136
+NARROW_TOKENS = 184
+LAST_TOKENS = 112
+REST_TOKENS = 96
 
 
 def tile_lstmcell_pa_t_w8_kernel(
@@ -64,7 +66,7 @@ def tile_lstmcell_pa_t_w8_kernel(
         wts = keep.tile([P, N_OUT], U8, name="wts", align_bytes=64)
 
         xb, me, xw, xbank, mbank, turned, q = {}, {}, {}, {}, {}, {}, {}
-        sig, gated, gq, res, obank = {}, {}, {}, {}, {}
+        sig, gq, res, obank = {}, {}, {}, {}
 
         free_banks = ["bank%d" % i for i in range(5)]
 
@@ -108,8 +110,9 @@ def tile_lstmcell_pa_t_w8_kernel(
                     xw[g, i] = [t[:, i * K + j : (i + 1) * K : PACK] for j in range(PACK)]
 
         def turn_x(g, banks=(0, 1)):
-            t = turnp.tile([P, 2 * GT * PACK], BF16, name="turned", align_bytes=64)
-            turned[g] = t
+            if g not in turned:
+                t = turnp.tile([P, 2 * GT * PACK], BF16, name="turned", align_bytes=64)
+                turned[g] = t
             for b in banks:
                 pt, name = take_bank()
                 if g == 0:
@@ -146,7 +149,7 @@ def tile_lstmcell_pa_t_w8_kernel(
 
         def turn_me(g):
             words = me[g].bitcast(F32)
-            for b, run in ((1, P), (0, 2)):
+            for b, run in ((1, 2 if g == GROUPS - 1 else P), (0, 2)):
                 dst = turned[g][:, b * HT * PACK : (b + 1) * HT * PACK].bitcast(F32)
                 if b == 1:
                     pt, name = take_bank()
@@ -161,15 +164,18 @@ def tile_lstmcell_pa_t_w8_kernel(
                         base = (2 * b + i) * (K // 2)
                         nc.tensor.transpose(bank[:, u, per * i : per * (i + 1), :], words[:, base + u : base + K // 2 : 2], ident[:])
                 nc.scalar.copy(out=dst.rearrange("p (c i u) -> p c i u", i=run, u=2), in_=bank.rearrange("p u c i -> p c i u"))
-                if b == 0:
-                    mbank[g] = pt
-                else:
+                mbank[g, b] = pt
+                if b == 1 and g < GROUPS - 1:
                     free_banks.append(name)
 
-        def quant_in(g):
+        def quant_in(g, pieces):
             codes = work.tile([P, 2 * GT], U32, name="qc", align_bytes=64)
             scales = work.tile([P, 2 * GT], U8, name="qs", align_bytes=64)
-            nc.vector.quantize_mx(out=codes[:].bitcast(FP8X4), scales=scales[:], in_=turned[g][:])
+            n = 2 * GT // pieces
+            for lo in range(0, 2 * GT, n):
+                nc.vector.quantize_mx(
+                    out=codes[:, lo : lo + n].bitcast(FP8X4), scales=scales[:, lo : lo + n], in_=turned[g][:, lo * PACK : (lo + n) * PACK]
+                )
             q[g] = (codes, scales)
 
         def gates(g, ts=range(PACK)):
@@ -191,17 +197,23 @@ def tile_lstmcell_pa_t_w8_kernel(
                 nc.scalar.activation(out=s[:, t, :], in_=pm[:], func=ACT.Sigmoid, bias=bias[:, t : t + 1])
                 free_banks.append(name)
 
+        def gated(g, lo, hi):
+            if g < GROUPS - 1:
+                return turned[g + 1][:, (GT + lo) * PACK : (GT + hi) * PACK]
+            if lo < HT:
+                return turned[g - 1][:, lo * PACK : hi * PACK]
+            return turned[g][:, (HT + lo) * PACK : (HT + hi) * PACK]
+
         def gate(engine, g, lo, hi, from_psum):
-            gated[g] = turned[g - 1][:, : GT * PACK] if g == GROUPS - 1 else turned[g + 1][:, GT * PACK :]
             cols = slice(lo * PACK, hi * PACK)
             if from_psum:
                 run = 2
-                me_turned = mbank[g][:].bitcast(BF16)[:, cols].rearrange("p (c u i e) -> p c u e i", u=2, i=run, e=2)
+                me_turned = mbank[g, lo // HT][:].bitcast(BF16)[:, lo % HT * PACK : (lo % HT + hi - lo) * PACK].rearrange("p (c u i e) -> p c u e i", u=2, i=run, e=2)
             else:
                 run = 4
                 me_turned = turned[g][:, cols].rearrange("p (c i u e) -> p c u e i", i=run, u=2, e=2)
             engine.tensor_tensor(
-                out=gated[g][:, cols].rearrange("p (c i u e) -> p c u e i", i=run, u=2, e=2),
+                out=gated(g, lo, hi).rearrange("p (c i u e) -> p c u e i", i=run, u=2, e=2),
                 in0=me_turned,
                 in1=sig[g][:, :, lo:hi].rearrange("p (u e) (c i) -> p c u e i", i=run, u=2),
                 op=MULT,
@@ -214,7 +226,7 @@ def tile_lstmcell_pa_t_w8_kernel(
                 gq[g] = (codes, scales)
             codes, scales = gq[g]
             nc.vector.quantize_mx(
-                out=codes[:, lo:hi].bitcast(FP8X4), scales=scales[:, lo:hi], in_=gated[g][:, lo * PACK : hi * PACK]
+                out=codes[:, lo:hi].bitcast(FP8X4), scales=scales[:, lo:hi], in_=gated(g, lo, hi)
             )
 
         def read_out(g, i0, i1, late=False):
@@ -291,12 +303,13 @@ def tile_lstmcell_pa_t_w8_kernel(
         permute(nc.vector.tensor_copy, ws[:], ws_raw[:])
         permute(nc.scalar.copy, wi[:], wi_raw[:])
         permute(nc.scalar.copy, wh[:], wh_raw[:])
-        turn_x(1)
+        turn_x(1, (0,))
         widen_scalar(2, 0)
-        quant_in(0)
-        scale_x(1)
         turn_me(1)
-        quant_in(1)
+        turn_x(1, (1,))
+        quant_in(0, 1)
+        scale_x(1)
+        quant_in(1, 2)
         load_words(wt, wt_words)
         load_scale_rows(nc.sync, wts, 0, wt_scales, range(4))
 
@@ -323,7 +336,7 @@ def tile_lstmcell_pa_t_w8_kernel(
                 empty_out(leave, 2, 4, nc.vector.tensor_copy)
             if 0 <= leave:
                 store(leave, 0, G)
-            quant_in(turn)
+            quant_in(turn, 1 if shared else 2)
             quant_gated(mix, 0, GT)
 
         def leave_by_scalar(g):
@@ -333,7 +346,7 @@ def tile_lstmcell_pa_t_w8_kernel(
             store(g, 0, G)
 
         gates(last - 1)
-        gate(nc.gpsimd, last - 1, 3 * P, GT, False)
+        gate(nc.gpsimd, last - 1, HT + REST_TOKENS, GT, False)
         gate(nc.vector, last - 1, 0, HT, True)
         read_out(last - 3, 0, 2)
         empty_out(last - 3, 0, 2, nc.scalar.copy)
@@ -341,13 +354,14 @@ def tile_lstmcell_pa_t_w8_kernel(
         empty_out(last - 3, 2, 4, nc.vector.tensor_copy)
         store(last - 3, 0, G)
         gates(last)
-        gate(nc.vector, last - 1, HT, 3 * P, False)
-        quant_gated(last - 1, 0, GT)
+        gate(nc.vector, last - 1, HT, HT + REST_TOKENS, False)
+        quant_gated(last - 1, 0, HT)
+        quant_gated(last - 1, HT, GT)
         leave_by_scalar(last - 2)
-        gate(nc.gpsimd, last, HT, 3 * P, False)
+        gate(nc.gpsimd, last, HT, GT - LAST_TOKENS, False)
         gate(nc.vector, last, 0, HT, True)
+        gate(nc.vector, last, GT - LAST_TOKENS, GT, True)
         leave_by_scalar(last - 1)
-        gate(nc.vector, last, 3 * P, GT, False)
         for lo, hi in ((0, 2 * P), (2 * P, 4 * P)):
             quant_gated(last, lo, hi)
         for i in range(G):

@@ -291,6 +291,9 @@ def tile_lstmcell_pa_t_w8_kernel(
         loads(0)
         loads(1)
         loads(2)
+        idle = plate.tile([P, GT], F32, name="late")
+        for i in range(G):
+            nc.tensor.matmul(idle[:, i * P : (i + 1) * P], lhsT=ident[:], rhs=ident[:], start=True, stop=True)
         widen_vector(0, 0, 1)
         widen_vector(0, 1, 1)
         nc.vector.memset(wts[:].bitcast(I32), 0)

@@ -99,15 +99,19 @@ def tile_lstmcell_pa_t_w8_kernel(
             for i in range(slabs):
                 xw[g, first + i] = [words[:, u * n + i * P : u * n + (i + 1) * P] for u in range(2)]
 
-        def widen_scalar(g, first):
-            t = work.tile([P, (G - first) * K], BF16, name="xw_scalar")
-            nc.scalar.copy(out=t[:], in_=xb[g][:, first * K :].bitcast(FP8))
-            words = t[:].bitcast(F32)
-            for i in range(G - first):
+        def widen_plain(g, first, copy, slabs=None, into=None):
+            slabs = slabs or G - first
+            if into is None:
+                fresh = work.tile([P, slabs * K], BF16, name="xw_plain")
+                into = fresh[:]
+            t = into
+            copy(out=t, in_=xb[g][:, first * K : (first + slabs) * K].bitcast(FP8))
+            words = t.bitcast(F32)
+            for i in range(slabs):
                 if g == 0:
                     xw[g, first + i] = [words[:, i * HT + u : (i + 1) * HT : 2] for u in range(2)]
                 else:
-                    xw[g, i] = [t[:, i * K + j : (i + 1) * K : PACK] for j in range(PACK)]
+                    xw[g, first + i] = [t[:, i * K + j : (i + 1) * K : PACK] for j in range(PACK)]
 
         def turn_x(g, banks=(0, 1)):
             if g not in turned:
@@ -272,7 +276,10 @@ def tile_lstmcell_pa_t_w8_kernel(
         nc.sync.dma_start(out=s4[:], in_=x_scale.rearrange("o (p t) -> p (o t)", t=PACK))
         load_me(0, 1)
         load_x(1)
-        load_scale_rows(nc.sync, ws_raw, 0, wi_scales, range(4))
+        load_scale_rows(nc.sync, ws_raw, 0, wi_scales, (0,))
+        load_scale_rows(nc.sync, ws_raw, 0, wi_scales, (1,))
+        load_scale_rows(nc.sync, ws_raw, 0, wi_scales, (2,))
+        load_scale_rows(nc.sync, ws_raw, 0, wi_scales, (3,))
         load_scale_rows(nc.sync, ws_raw, 4, wh_scales, (3,))
         load_me(1, 1)
         load_words(wi_raw, wi_words)
@@ -298,19 +305,19 @@ def tile_lstmcell_pa_t_w8_kernel(
         widen_vector(0, 1, 1)
         nc.vector.memset(wts[:].bitcast(I32), 0)
         nc.vector.tensor_copy(out=ident_bf[:], in_=ident[:])
-        widen_scalar(0, 2)
+        widen_plain(0, 2, nc.scalar.copy)
         turn_x(0)
-        widen_scalar(1, 0)
+        widen_plain(1, 0, nc.scalar.copy)
         scale_x(0)
         turn_me(0)
         permute(nc.vector.tensor_copy, ws[:], ws_raw[:])
         permute(nc.scalar.copy, wi[:], wi_raw[:])
         permute(nc.scalar.copy, wh[:], wh_raw[:])
         turn_x(1, (0,))
-        widen_scalar(2, 0)
         turn_me(1)
         turn_x(1, (1,))
         quant_in(0, 1)
+        widen_plain(2, 0, nc.gpsimd.tensor_copy, 2, turned[0][:, GT * PACK : GT * PACK + 2 * K])
         scale_x(1)
         quant_in(1, 2)
         load_words(wt, wt_words)
@@ -330,10 +337,17 @@ def tile_lstmcell_pa_t_w8_kernel(
                 read_out(leave, 2, 4, shared)
                 if not shared:
                     empty_out(leave, 2, 4, nc.scalar.copy)
-            turn_x(turn)
-            if cast < GROUPS:
-                widen_scalar(cast, 0)
-            turn_me(turn)
+            if s == 3:
+                widen_plain(turn, 2, nc.scalar.copy)
+                turn_x(turn, (0,))
+                turn_me(turn)
+                turn_x(turn, (1,))
+                widen_plain(cast, 0, nc.scalar.copy)
+            else:
+                turn_x(turn)
+                if cast < GROUPS:
+                    widen_plain(cast, 0, nc.scalar.copy)
+                turn_me(turn)
             scale_x(turn)
             if shared:
                 empty_out(leave, 2, 4, nc.vector.tensor_copy)

@@ -85,20 +85,6 @@ def tile_lstmcell_pa_t_w8_kernel(
             for j in range(n):
                 me[g + j] = t[:, j * G * K : (j + 1) * G * K]
 
-        def widen_vector(g, first, slabs):
-            n = slabs * P
-            t = work.tile([P, slabs * K], BF16, name="xw_vector")
-            nc.vector.tensor_scalar(
-                out=t[:].rearrange("p (u m e) -> p m u e", u=2, e=2),
-                in0=xb[g][:, first * K : (first + slabs) * K].bitcast(FP8).rearrange("p (m u e) -> p m u e", u=2, e=2),
-                scalar1=ones[:],
-                scalar2=None,
-                op0=MULT,
-            )
-            words = t[:].bitcast(F32)
-            for i in range(slabs):
-                xw[g, first + i] = [words[:, u * n + i * P : u * n + (i + 1) * P] for u in range(2)]
-
         def widen_plain(g, first, copy, slabs=None, into=None):
             slabs = slabs or G - first
             if into is None:
@@ -108,7 +94,7 @@ def tile_lstmcell_pa_t_w8_kernel(
             copy(out=t, in_=xb[g][:, first * K : (first + slabs) * K].bitcast(FP8))
             words = t.bitcast(F32)
             for i in range(slabs):
-                if g == 0:
+                if (g, first) == (0, 2):
                     xw[g, first + i] = [words[:, i * HT + u : (i + 1) * HT : 2] for u in range(2)]
                 else:
                     xw[g, first + i] = [t[:, i * K + j : (i + 1) * K : PACK] for j in range(PACK)]
@@ -119,7 +105,7 @@ def tile_lstmcell_pa_t_w8_kernel(
                 turned[g] = t
             for b in banks:
                 pt, name = take_bank()
-                if g == 0:
+                if (g, b) == (0, 1):
                     bank = pt[:].rearrange("p (u i r) -> p u i r", u=2, i=2)
                     for i in range(2):
                         for u in range(2):
@@ -135,7 +121,7 @@ def tile_lstmcell_pa_t_w8_kernel(
             for b in banks:
                 lo = (GT + b * HT) * PACK
                 dst, src = turned[g][:, lo : lo + HT * PACK], xbank[g, b][0][:].bitcast(BF16)
-                if g == 0:
+                if (g, b) == (0, 1):
                     nc.vector.tensor_tensor(
                         out=dst.rearrange("p (m u e) -> p m u e", u=2, e=2),
                         in0=src.rearrange("p (u m e) -> p m u e", u=2, e=2),
@@ -301,10 +287,9 @@ def tile_lstmcell_pa_t_w8_kernel(
         idle = plate.tile([P, GT], F32, name="late")
         for i in range(G):
             nc.tensor.matmul(idle[:, i * P : (i + 1) * P], lhsT=ident[:], rhs=ident[:], start=True, stop=True)
-        widen_vector(0, 0, 1)
-        widen_vector(0, 1, 1)
-        nc.vector.memset(wts[:].bitcast(I32), 0)
-        nc.vector.tensor_copy(out=ident_bf[:], in_=ident[:])
+        nc.scalar.copy(out=ident_bf[:], in_=ident[:])
+        nc.gpsimd.memset(wts[:].bitcast(I32), 0)
+        widen_plain(0, 0, nc.scalar.copy, 2)
         widen_plain(0, 2, nc.scalar.copy)
         turn_x(0)
         widen_plain(1, 0, nc.scalar.copy)
@@ -379,7 +364,7 @@ def tile_lstmcell_pa_t_w8_kernel(
         gate(nc.vector, last, 0, HT, True)
         gate(nc.vector, last, GT - LAST_TOKENS, GT, True)
         leave_by_scalar(last - 1)
-        for lo, hi in ((0, 2 * P), (2 * P, 4 * P)):
+        for lo, hi in ((0, P), (P, HT), (HT, GT)):
             quant_gated(last, lo, hi)
         for i in range(G):
             read_out(last, i, i + 1)

@@ -18,25 +18,26 @@ ACT = mybir.ActivationFunctionType
 
 P = 128
 PACK = 4
-TILES = TOKENS // P
+SLABS = TOKENS // P
 G = 4
-GROUPS = TILES // G
+GROUPS = SLABS // G
 GT = G * P
 HT = GT // 2
-AHEAD = 3
-VECTOR_TOKENS = 136
+WIDE_TOKENS = 136
 NARROW_TOKENS = 184
-LAST_TOKENS = 112
-REST_TOKENS = 96
+REST_TOKENS = 48
+LAST_TOKENS = 192
+WARM_UPS = 3
 
 
 def tile_lstmcell_pa_t_w8_kernel(
     tc, x_bytes, x_scale, me_output, wi_words, wi_scales, wh_words, wh_scales, wt_words, wt_scales, mem_bias, out
 ):
     nc = tc.nc
-    x_hbm = x_bytes.rearrange("(p i) k -> p i k", i=TILES)
-    me_hbm = me_output.rearrange("(p i) k -> p i k", i=TILES)
-    out_hbm = out.rearrange("(p i) n -> p i n", i=TILES)
+    x_hbm = x_bytes.rearrange("(p i) k -> p i k", i=SLABS)
+    me_hbm = me_output.rearrange("(p i) k -> p i k", i=SLABS)
+    out_hbm = out.rearrange("(p i) n -> p i n", i=SLABS)
+    last = GROUPS - 1
 
     with ExitStack() as ctx:
         keep = ctx.enter_context(tc.tile_pool(name="keep", bufs=1))
@@ -45,14 +46,12 @@ def tile_lstmcell_pa_t_w8_kernel(
         work = ctx.enter_context(tc.tile_pool(name="work", bufs=3))
         turnp = ctx.enter_context(tc.tile_pool(name="turnp", bufs=5))
         outp = ctx.enter_context(tc.tile_pool(name="outp", bufs=4))
-        pkeep = ctx.enter_context(tc.psum_pool(name="pkeep", bufs=2))
         pmix = ctx.enter_context(tc.psum_pool(name="pmix", bufs=1))
-        plate = ctx.enter_context(tc.psum_pool(name="plate", bufs=1))
         ctx.enter_context(tc.manual_schedule())
 
         ident = keep.tile([P, P], F32, name="ident")
         ident_bf = keep.tile([P, P], BF16, name="ident_bf")
-        ones = keep.tile([P, 1], F32, name="ones")
+        zeros = keep.tile([P, P], F32, name="zeros")
         warm = keep.tile([P, 1], F32, name="warm")
         s4 = keep.tile([P, PACK], F32, name="s4")
         bias = keep.tile([P, PACK], BF16, name="bias")
@@ -66,142 +65,160 @@ def tile_lstmcell_pa_t_w8_kernel(
         wts = keep.tile([P, N_OUT], U8, name="wts", align_bytes=64)
 
         xb, me, xw, xbank, mbank, turned, q = {}, {}, {}, {}, {}, {}, {}
-        sig, gq, res, obank = {}, {}, {}, {}
+        sig, gq, res, obank, gbank = {}, {}, {}, {}, []
 
-        free_banks = ["bank%d" % i for i in range(5)]
+        free_banks = ["bank%d" % i for i in range(8)]
 
         def take_bank():
             name = free_banks.pop(0)
             return pmix.tile([P, GT], F32, name=name), name
 
-        def load_x(g):
+        def load_x(g, halves=(0, 1), name="xb"):
+            n = len(halves) * 2
+            t = xin.tile([P, n * K], U8, name=name)
+            i0 = g * G + 2 * halves[0]
+            nc.sync.dma_start(out=t[:].rearrange("p (i k) -> p i k", k=K), in_=x_hbm[:, i0 : i0 + n, :])
+            for j, h in enumerate(halves):
+                xb[g, h] = t[:, j * 2 * K : (j + 1) * 2 * K]
+
+        def load_me(g, first, count, name="me"):
+            t = mein.tile([P, count * 2 * K], BF16, name=name)
+            i0 = g * G + 2 * first
+            nc.sync.dma_start(out=t[:].rearrange("p (i k) -> p i k", k=K), in_=me_hbm[:, i0 : i0 + 2 * count, :])
+            for j in range(count):
+                me[g + (first + j) // 2, (first + j) % 2] = t[:, j * 2 * K : (j + 1) * 2 * K]
+
+        def cast(copy, g, h):
+            fresh = work.tile([P, 2 * K], BF16, name="xw%d" % h)
+            copy(out=fresh[:], in_=xb[g, h].bitcast(FP8))
+            xw[g, h] = fresh[:]
+
+        def cast_both(g):
+            fresh = work.tile([P, G * K], BF16, name="xw")
+            nc.scalar.copy(out=fresh[:], in_=xall[g].bitcast(FP8))
+            for h in range(2):
+                xw[g, h] = fresh[:, h * 2 * K : (h + 1) * 2 * K]
+
+        xall = {}
+
+        def load_x_group(g):
             t = xin.tile([P, G * K], U8, name="xb")
-            nc.sync.dma_start(out=t[:].rearrange("p (i k) -> p i k", i=G), in_=x_hbm[:, g * G : (g + 1) * G, :])
-            xb[g] = t
+            nc.sync.dma_start(out=t[:].rearrange("p (i k) -> p i k", k=K), in_=x_hbm[:, g * G : (g + 1) * G, :])
+            xall[g] = t[:]
+            for h in range(2):
+                xb[g, h] = t[:, h * 2 * K : (h + 1) * 2 * K]
 
-        def load_me(g, n):
-            t = mein.tile([P, n * G * K], BF16, name="me")
-            nc.sync.dma_start(out=t[:].rearrange("p (i k) -> p i k", k=K), in_=me_hbm[:, g * G : (g + n) * G, :])
-            for j in range(n):
-                me[g + j] = t[:, j * G * K : (j + 1) * G * K]
-
-        def widen_plain(g, first, copy, slabs=None, into=None):
-            slabs = slabs or G - first
-            if into is None:
-                fresh = work.tile([P, slabs * K], BF16, name="xw_plain")
-                into = fresh[:]
-            t = into
-            copy(out=t, in_=xb[g][:, first * K : (first + slabs) * K].bitcast(FP8))
-            words = t.bitcast(F32)
-            for i in range(slabs):
-                if (g, first) == (0, 2):
-                    xw[g, first + i] = [words[:, i * HT + u : (i + 1) * HT : 2] for u in range(2)]
-                else:
-                    xw[g, first + i] = [t[:, i * K + j : (i + 1) * K : PACK] for j in range(PACK)]
-
-        def turn_x(g, banks=(0, 1)):
+        def turned_tile(g):
             if g not in turned:
-                t = turnp.tile([P, 2 * GT * PACK], BF16, name="turned", align_bytes=64)
-                turned[g] = t
-            for b in banks:
-                pt, name = take_bank()
-                if (g, b) == (0, 1):
-                    bank = pt[:].rearrange("p (u i r) -> p u i r", u=2, i=2)
-                    for i in range(2):
-                        for u in range(2):
-                            nc.tensor.transpose(bank[:, u, i, :], xw[g, 2 * b + i][u], ident[:])
-                else:
-                    bank = pt[:].bitcast(BF16).rearrange("p (i c j r) -> p i j c r", i=2, j=PACK, r=2)
-                    for i in range(2):
-                        for j in range(PACK):
-                            nc.tensor.matmul(bank[:, i, j, :, :], lhsT=xw[g, 2 * b + i][j], rhs=ident_bf[:], start=True, stop=True)
-                xbank[g, b] = (pt, name)
+                fresh = turnp.tile([P, 2 * GT * PACK], BF16, name="turned", align_bytes=64)
+                turned[g] = fresh
+            return turned[g]
 
-        def scale_x(g, banks=(0, 1)):
-            for b in banks:
-                lo = (GT + b * HT) * PACK
-                dst, src = turned[g][:, lo : lo + HT * PACK], xbank[g, b][0][:].bitcast(BF16)
-                if (g, b) == (0, 1):
-                    nc.vector.tensor_tensor(
-                        out=dst.rearrange("p (m u e) -> p m u e", u=2, e=2),
-                        in0=src.rearrange("p (u m e) -> p m u e", u=2, e=2),
-                        in1=s4[:].rearrange("p (u e) -> p u e", u=2).unsqueeze(1).to_broadcast([P, HT, 2, 2]),
-                        op=MULT,
-                    )
-                else:
-                    nc.vector.tensor_tensor(
-                        out=dst.rearrange("p (c r j) -> p c r j", r=2, j=PACK),
-                        in0=src.rearrange("p (c j r) -> p c r j", r=2, j=PACK),
-                        in1=s4[:].unsqueeze(1).unsqueeze(1).to_broadcast([P, HT // 2, 2, PACK]),
-                        op=MULT,
-                    )
-                free_banks.append(xbank[g, b][1])
+        def turn_words(bank, words):
+            for i in range(2):
+                for u in range(2):
+                    nc.tensor.transpose(bank[u][i], words[:, i * HT + u : (i + 1) * HT : 2], ident[:])
 
-        def turn_me(g):
-            words = me[g].bitcast(F32)
-            for b, run in ((1, 2 if g == GROUPS - 1 else P), (0, 2)):
-                dst = turned[g][:, b * HT * PACK : (b + 1) * HT * PACK].bitcast(F32)
-                if b == 1:
-                    pt, name = take_bank()
-                elif g == 2:
-                    pt = plate.tile([P, GT], F32, name="late")
-                else:
-                    pt = pkeep.tile([P, GT], F32, name="kept")
-                bank = pt[:].rearrange("p (c u i) -> p u c i", u=2, i=run)
-                per = P // run
+        def turn_x(g, h, as_words=False):
+            pt, name = take_bank()
+            if as_words:
+                bank = pt[:].rearrange("p (u i r) -> p u i r", u=2, i=2)
+                turn_words([[bank[:, u, i, :] for i in range(2)] for u in range(2)], xw[g, h].bitcast(F32))
+            else:
+                bank = pt[:].bitcast(BF16).rearrange("p (i c j r) -> p i j c r", i=2, j=PACK, r=2)
                 for i in range(2):
-                    for u in range(2):
-                        base = (2 * b + i) * (K // 2)
-                        nc.tensor.transpose(bank[:, u, per * i : per * (i + 1), :], words[:, base + u : base + K // 2 : 2], ident[:])
-                nc.scalar.copy(out=dst.rearrange("p (c i u) -> p c i u", i=run, u=2), in_=bank.rearrange("p u c i -> p c i u"))
-                mbank[g, b] = pt
-                if b == 1 and g < GROUPS - 1:
-                    free_banks.append(name)
+                    for j in range(PACK):
+                        nc.tensor.matmul(
+                            bank[:, i, j, :, :], lhsT=xw[g, h][:, i * K + j : (i + 1) * K : PACK], rhs=ident_bf[:], start=True, stop=True
+                        )
+            xbank[g, h] = (pt, name, as_words)
 
-        def quant_in(g, pieces):
-            codes = work.tile([P, 2 * GT], U32, name="qc", align_bytes=64)
-            scales = work.tile([P, 2 * GT], U8, name="qs", align_bytes=64)
-            n = 2 * GT // pieces
-            for lo in range(0, 2 * GT, n):
-                nc.vector.quantize_mx(
-                    out=codes[:, lo : lo + n].bitcast(FP8X4), scales=scales[:, lo : lo + n], in_=turned[g][:, lo * PACK : (lo + n) * PACK]
+        def scale_x(g, h):
+            pt, name, as_words = xbank[g, h]
+            lo = (GT + h * HT) * PACK
+            dst, src = turned_tile(g)[:, lo : lo + HT * PACK], pt[:].bitcast(BF16)
+            if as_words:
+                nc.vector.tensor_tensor(
+                    out=dst.rearrange("p (m u e) -> p m u e", u=2, e=2),
+                    in0=src.rearrange("p (u m e) -> p m u e", u=2, e=2),
+                    in1=s4[:].rearrange("p (u e) -> p u e", u=2).unsqueeze(1).to_broadcast([P, HT, 2, 2]),
+                    op=MULT,
                 )
-            q[g] = (codes, scales)
+            else:
+                nc.vector.tensor_tensor(
+                    out=dst.rearrange("p (c r j) -> p c r j", r=2, j=PACK),
+                    in0=src.rearrange("p (c j r) -> p c r j", r=2, j=PACK),
+                    in1=s4[:].unsqueeze(1).unsqueeze(1).to_broadcast([P, HT // 2, 2, PACK]),
+                    op=MULT,
+                )
+            free_banks.append(name)
 
-        def gates(g, ts=range(PACK)):
+        def turn_me(g, h):
+            stays = h == 0 or g == last
+            run = 2 if stays else P
+            pt, name = take_bank()
+            bank = pt[:].rearrange("p (c u i) -> p u c i", u=2, i=run)
+            per = P // run
+            turn_words([[bank[:, u, per * i : per * (i + 1), :] for i in range(2)] for u in range(2)], me[g, h].bitcast(F32))
+            dst = turned_tile(g)[:, h * HT * PACK : (h + 1) * HT * PACK].bitcast(F32)
+            nc.scalar.copy(out=dst.rearrange("p (c i u) -> p c i u", i=run, u=2), in_=bank.rearrange("p u c i -> p c i u"))
+            mbank[g, h] = (pt, name)
+            if not stays:
+                free_banks.append(name)
+
+        def quant_in(g, parts):
+            if g not in q:
+                codes = work.tile([P, 2 * GT], U32, name="qc", align_bytes=64)
+                scales = work.tile([P, 2 * GT], U8, name="qs", align_bytes=64)
+                q[g] = (codes, scales)
+            codes, scales = q[g]
+            for lo, hi in parts:
+                nc.vector.quantize_mx(
+                    out=codes[:, lo:hi].bitcast(FP8X4), scales=scales[:, lo:hi], in_=turned[g][:, lo * PACK : hi * PACK]
+                )
+
+        BOTH, ME, X = (0, 2 * GT), (0, GT), (GT, 2 * GT)
+
+        def gates(g, ts, lo=0, hi=GT):
             if g not in sig:
                 fresh = work.tile([P, PACK, GT], F32, name="sig")
                 sig[g] = fresh
-            s = sig[g]
+            n = hi - lo
+            codes, scales = q[g]
             for t in ts:
                 cols = slice(t * P, (t + 1) * P)
                 pm, name = take_bank()
                 nc.tensor.matmul_mx(
-                    out=pm[:], lhsT=wi[:, cols].bitcast(FP8X4), lhsT_scale=ws[:, cols],
-                    rhs=q[g][0][:, GT:].bitcast(FP8X4), rhs_scale=q[g][1][:, GT:], start=True, stop=False,
+                    out=pm[:, 0:n], lhsT=wi[:, cols].bitcast(FP8X4), lhsT_scale=ws[:, cols],
+                    rhs=codes[:, GT + lo : GT + hi].bitcast(FP8X4), rhs_scale=scales[:, GT + lo : GT + hi], start=True, stop=False,
                 )
                 nc.tensor.matmul_mx(
-                    out=pm[:], lhsT=wh[:, cols].bitcast(FP8X4), lhsT_scale=ws[4:, cols],
-                    rhs=q[g][0][:, 0:GT].bitcast(FP8X4), rhs_scale=q[g][1][:, 0:GT], start=False, stop=True,
+                    out=pm[:, 0:n], lhsT=wh[:, cols].bitcast(FP8X4), lhsT_scale=ws[4:, cols],
+                    rhs=codes[:, lo:hi].bitcast(FP8X4), rhs_scale=scales[:, lo:hi], start=False, stop=True,
                 )
-                nc.scalar.activation(out=s[:, t, :], in_=pm[:], func=ACT.Sigmoid, bias=bias[:, t : t + 1])
-                free_banks.append(name)
+                nc.scalar.activation(out=sig[g][:, t, lo:hi], in_=pm[:, 0:n], func=ACT.Sigmoid, bias=bias[:, t : t + 1])
+                gbank.append(name)
+
+        def free_gate_banks(n):
+            for i in range(n):
+                free_banks.append(gbank.pop(0))
 
         def gated(g, lo, hi):
-            if g < GROUPS - 1:
+            if g < last:
                 return turned[g + 1][:, (GT + lo) * PACK : (GT + hi) * PACK]
             if lo < HT:
-                return turned[g - 1][:, lo * PACK : hi * PACK]
-            return turned[g][:, (HT + lo) * PACK : (HT + hi) * PACK]
+                return turned[g][:, (GT + lo) * PACK : (GT + hi) * PACK]
+            return turned[g - 1][:, lo * PACK : hi * PACK]
 
         def gate(engine, g, lo, hi, from_psum):
-            cols = slice(lo * PACK, hi * PACK)
             if from_psum:
                 run = 2
-                me_turned = mbank[g, lo // HT][:].bitcast(BF16)[:, lo % HT * PACK : (lo % HT + hi - lo) * PACK].rearrange("p (c u i e) -> p c u e i", u=2, i=run, e=2)
+                me_turned = mbank[g, lo // HT][0][:].bitcast(BF16)[:, lo % HT * PACK : (lo % HT + hi - lo) * PACK].rearrange(
+                    "p (c u i e) -> p c u e i", u=2, i=run, e=2
+                )
             else:
                 run = 4
-                me_turned = turned[g][:, cols].rearrange("p (c i u e) -> p c u e i", i=run, u=2, e=2)
+                me_turned = turned[g][:, lo * PACK : hi * PACK].rearrange("p (c i u e) -> p c u e i", i=run, u=2, e=2)
             engine.tensor_tensor(
                 out=gated(g, lo, hi).rearrange("p (c i u e) -> p c u e i", i=run, u=2, e=2),
                 in0=me_turned,
@@ -209,21 +226,23 @@ def tile_lstmcell_pa_t_w8_kernel(
                 op=MULT,
             )
 
+        def gate_kept(g, share):
+            gate(nc.vector, g, 0, share, True)
+            free_banks.append(mbank[g, 0][1])
+
         def quant_gated(g, lo, hi):
             if g not in gq:
                 codes = work.tile([P, GT], U32, name="gc", align_bytes=64)
                 scales = work.tile([P, GT], U8, name="gs", align_bytes=64)
                 gq[g] = (codes, scales)
             codes, scales = gq[g]
-            nc.vector.quantize_mx(
-                out=codes[:, lo:hi].bitcast(FP8X4), scales=scales[:, lo:hi], in_=gated(g, lo, hi)
-            )
+            nc.vector.quantize_mx(out=codes[:, lo:hi].bitcast(FP8X4), scales=scales[:, lo:hi], in_=gated(g, lo, hi))
 
-        def read_out(g, i0, i1, late=False):
+        def read_out(g, i0, i1):
             if g not in res:
                 fresh = outp.tile([P, G, N_OUT], F32, name="res")
                 res[g] = fresh
-            po, name = (plate.tile([P, GT], F32, name="late"), None) if late else take_bank()
+            po, name = take_bank()
             for i in range(i0, i1):
                 cols = slice(i * P, (i + 1) * P)
                 nc.tensor.matmul_mx(
@@ -232,19 +251,18 @@ def tile_lstmcell_pa_t_w8_kernel(
                 )
             obank[g, i0] = (po[:, 0 : (i1 - i0) * N_OUT], name)
 
-        def empty_out(g, i0, i1, copy):
+        def empty_out(copy, g, i0, i1):
             copy(out=res[g][:, i0:i1, :].rearrange("p i n -> p (i n)"), in_=obank[g, i0][0])
-            if obank[g, i0][1]:
-                free_banks.append(obank[g, i0][1])
+            free_banks.append(obank[g, i0][1])
 
         def store(g, i0, i1):
             nc.sync.dma_start(out=out_hbm[:, g * G + i0 : g * G + i1, :], in_=res[g][:, i0:i1, :])
 
         def permute(copy, dst, src):
-            copy(out=dst.rearrange("p (t m) -> p t m", t=PACK), in_=src.rearrange("p (m t) -> p t m", t=PACK))
+            copy(out=dst.rearrange("p (t c i) -> p c t i", t=PACK, i=4), in_=src.rearrange("p (c i t) -> p c t i", t=PACK, i=4))
 
-        def load_scale_rows(queue, tile, row0, hbm, quadrants):
-            for h in quadrants:
+        def load_scale_rows(queue, tile, row0, hbm):
+            for h in range(4):
                 queue.dma_start(
                     out=tile[32 * h + row0 : 32 * h + row0 + 4, :].bitcast(I32), in_=hbm[0, 4 * h : 4 * h + 4, :].bitcast(I32)
                 )
@@ -252,121 +270,131 @@ def tile_lstmcell_pa_t_w8_kernel(
         def load_words(tile, hbm):
             nc.sync.dma_start(out=tile[:].bitcast(I32), in_=hbm[0].rearrange("p n t -> p (n t)").bitcast(I32))
 
-        nc.gpsimd.memset(ones[:], 1.0)
-        nc.scalar.activation(out=warm[:], in_=ones[:], func=ACT.Sigmoid)
-        nc.gpsimd.memset(ws_raw[:].bitcast(I32), 0)
+        nc.vector.memset(zeros[:], 0.0)
+        nc.vector.memset(ws_raw[:].bitcast(I32), 0)
+        nc.vector.memset(wts[:].bitcast(I32), 0)
+        nc.scalar.activation(out=warm[:], in_=zeros[:, 0:1], func=ACT.Sigmoid)
         make_identity(nc, ident[:])
-        load_scale_rows(nc.gpsimd, ws_raw, 4, wh_scales, range(3))
+        nc.vector.tensor_copy(out=ident_bf[:], in_=ident[:])
+        idle, name = take_bank()
+        for i in range(WARM_UPS):
+            nc.tensor.matmul(idle[:, i * P : (i + 1) * P], lhsT=zeros[:], rhs=zeros[:], start=True, stop=True)
+        free_banks.append(name)
 
-        load_x(0)
+        load_x(0, (0,), "xb0")
+        load_me(0, 0, 1, "me0")
         nc.sync.dma_start(out=s4[:], in_=x_scale.rearrange("o (p t) -> p (o t)", t=PACK))
-        load_me(0, 1)
-        load_x(1)
-        load_scale_rows(nc.sync, ws_raw, 0, wi_scales, (0,))
-        load_scale_rows(nc.sync, ws_raw, 0, wi_scales, (1,))
-        load_scale_rows(nc.sync, ws_raw, 0, wi_scales, (2,))
-        load_scale_rows(nc.sync, ws_raw, 0, wi_scales, (3,))
-        load_scale_rows(nc.sync, ws_raw, 4, wh_scales, (3,))
-        load_me(1, 1)
+        load_x(0, (1,), "xb0")
+        load_me(0, 1, 1, "me0")
+        load_x_group(1)
         load_words(wi_raw, wi_words)
         load_words(wh_raw, wh_words)
-        load_x(2)
+        load_scale_rows(nc.sync, ws_raw, 0, wi_scales)
+        load_scale_rows(nc.gpsimd, ws_raw, 4, wh_scales)
+        load_me(1, 0, 2, "me1")
         nc.sync.dma_start(out=bias[:], in_=mem_bias.rearrange("(p t) -> p t", t=PACK))
+        load_x_group(2)
+        load_x_group(3)
+        load_me(2, 0, 4)
+        load_x_group(4)
 
-        def loads(s):
-            if s + AHEAD < GROUPS:
-                load_x(s + AHEAD)
-            if s % 2 == 0 and s + 2 < GROUPS:
-                load_me(s + 2, 2)
-
-        last = GROUPS - 1
-
-        loads(0)
-        loads(1)
-        loads(2)
-        idle = plate.tile([P, GT], F32, name="late")
-        for i in range(G):
-            nc.tensor.matmul(idle[:, i * P : (i + 1) * P], lhsT=ident[:], rhs=ident[:], start=True, stop=True)
-        nc.scalar.copy(out=ident_bf[:], in_=ident[:])
-        nc.gpsimd.memset(wts[:].bitcast(I32), 0)
-        widen_plain(0, 0, nc.scalar.copy, 2)
-        widen_plain(0, 2, nc.scalar.copy)
-        turn_x(0)
-        widen_plain(1, 0, nc.scalar.copy)
-        scale_x(0)
-        turn_me(0)
-        permute(nc.vector.tensor_copy, ws[:], ws_raw[:])
-        permute(nc.scalar.copy, wi[:], wi_raw[:])
-        permute(nc.scalar.copy, wh[:], wh_raw[:])
-        turn_x(1, (0,))
-        turn_me(1)
-        turn_x(1, (1,))
-        quant_in(0, 1)
-        widen_plain(2, 0, nc.gpsimd.tensor_copy, 2, turned[0][:, GT * PACK : GT * PACK + 2 * K])
-        scale_x(1)
-        quant_in(1, 2)
+        cast(nc.scalar.copy, 0, 0)
+        cast(nc.scalar.copy, 0, 1)
+        turn_me(0, 0)
+        turn_x(0, 0)
+        turn_x(0, 1)
+        cast(nc.scalar.copy, 1, 0)
+        cast(nc.scalar.copy, 1, 1)
+        turn_me(0, 1)
+        scale_x(0, 0)
+        scale_x(0, 1)
+        permute(nc.gpsimd.tensor_copy, wi[:], wi_raw[:])
+        permute(nc.gpsimd.tensor_copy, wh[:], wh_raw[:])
+        quant_in(0, (ME, X))
+        turn_x(1, 0)
+        turn_x(1, 1)
+        turn_me(1, 0)
+        turn_me(1, 1)
+        nc.vector.tensor_copy(out=ws[:].rearrange("p (t m) -> p t m", t=PACK), in_=ws_raw[:].rearrange("p (m t) -> p t m", t=PACK))
+        spent = turned[0][:, GT * PACK : 2 * GT * PACK]
+        nc.gpsimd.tensor_copy(out=spent[:, 0 : 3 * K], in_=xall[2][:, 0 : 3 * K].bitcast(FP8))
+        nc.scalar.copy(out=spent[:, 3 * K :], in_=xall[2][:, 3 * K :].bitcast(FP8))
+        for h in range(2):
+            xw[2, h] = spent[:, h * 2 * K : (h + 1) * 2 * K]
+        gates(0, range(PACK))
+        free_gate_banks(3)
+        scale_x(1, 0)
+        scale_x(1, 1)
+        quant_in(1, (ME, X))
         load_words(wt, wt_words)
-        load_scale_rows(nc.sync, wts, 0, wt_scales, range(4))
+        load_scale_rows(nc.sync, wts, 0, wt_scales)
 
-        for s in range(3, GROUPS + 1):
-            cast, turn, mix, leave = s, s - 1, s - 3, s - 5
-            loads(s)
-            shared = 1 <= leave and cast < GROUPS
-            share = VECTOR_TOKENS if shared else NARROW_TOKENS
-            gates(mix)
+        for t in range(2, GROUPS):
+            mix, leave = t - 2, t - 4
+            if t + 3 < GROUPS:
+                load_x_group(t + 3)
+            if t % 2 == 0 and t + 2 < GROUPS:
+                load_me(t + 2, 0, 4)
+            share = WIDE_TOKENS if leave >= 0 else NARROW_TOKENS
+            turn_x(t, 0)
+            free_gate_banks(1)
+            turn_x(t, 1, t == last)
+            if leave >= 0:
+                empty_out(nc.scalar.copy, leave, 0, 2)
+            if t + 1 < GROUPS:
+                cast_both(t + 1)
             gate(nc.gpsimd, mix, share, GT, False)
-            gate(nc.vector, mix, 0, share, True)
-            if 0 <= leave:
-                read_out(leave, 0, 2)
-                empty_out(leave, 0, 2, nc.scalar.copy)
-                read_out(leave, 2, 4, shared)
-                if not shared:
-                    empty_out(leave, 2, 4, nc.scalar.copy)
-            if s == 3:
-                widen_plain(turn, 2, nc.scalar.copy)
-                turn_x(turn, (0,))
-                turn_me(turn)
-                turn_x(turn, (1,))
-                widen_plain(cast, 0, nc.scalar.copy)
-            else:
-                turn_x(turn)
-                if cast < GROUPS:
-                    widen_plain(cast, 0, nc.scalar.copy)
-                turn_me(turn)
-            scale_x(turn)
-            if shared:
-                empty_out(leave, 2, 4, nc.vector.tensor_copy)
-            if 0 <= leave:
+            if mix > 0:
+                gate_kept(mix, share)
+            turn_me(t, 1)
+            turn_me(t, 0)
+            scale_x(t, 0)
+            gates(mix + 1, (0, 1, 2))
+            scale_x(t, 1)
+            free_gate_banks(1)
+            gates(mix + 1, (3,))
+            if mix == 0:
+                gate_kept(mix, share)
+            if leave >= 0:
+                empty_out(nc.vector.tensor_copy, leave, 2, 4)
                 store(leave, 0, G)
-            quant_in(turn, 1 if shared else 2)
+            free_gate_banks(1)
+            if leave + 1 >= 0:
+                read_out(leave + 1, 0, 2)
+                read_out(leave + 1, 2, 4)
+            free_gate_banks(1)
+            quant_in(t, (ME, X) if mix == 1 else (BOTH,))
             quant_gated(mix, 0, GT)
 
         def leave_by_scalar(g):
             for i in (0, 2):
                 read_out(g, i, i + 2)
-                empty_out(g, i, i + 2, nc.scalar.copy)
-            store(g, 0, G)
+                empty_out(nc.scalar.copy, g, i, i + 2)
+                store(g, i, i + 2)
 
-        gates(last - 1)
+        free_gate_banks(1)
+        empty_out(nc.scalar.copy, last - 3, 0, 2)
+        store(last - 3, 0, 2)
         gate(nc.gpsimd, last - 1, HT + REST_TOKENS, GT, False)
         gate(nc.vector, last - 1, 0, HT, True)
-        read_out(last - 3, 0, 2)
-        empty_out(last - 3, 0, 2, nc.scalar.copy)
-        read_out(last - 3, 2, 4, True)
-        empty_out(last - 3, 2, 4, nc.vector.tensor_copy)
-        store(last - 3, 0, G)
-        gates(last)
+        gates(last, range(PACK), 0, HT)
+        free_gate_banks(4)
+        gates(last, range(PACK), HT, GT)
+        free_banks.append(mbank[last - 1, 0][1])
+        empty_out(nc.vector.tensor_copy, last - 3, 2, 4)
+        store(last - 3, 2, 4)
+        free_gate_banks(4)
         gate(nc.vector, last - 1, HT, HT + REST_TOKENS, False)
         quant_gated(last - 1, 0, HT)
         quant_gated(last - 1, HT, GT)
         leave_by_scalar(last - 2)
-        gate(nc.gpsimd, last, HT, GT - LAST_TOKENS, False)
-        gate(nc.vector, last, 0, HT, True)
-        gate(nc.vector, last, GT - LAST_TOKENS, GT, True)
+        gate(nc.gpsimd, last, 0, LAST_TOKENS, False)
+        gate(nc.vector, last, LAST_TOKENS, HT, True)
+        gate(nc.vector, last, HT, GT, True)
         leave_by_scalar(last - 1)
-        for lo, hi in ((0, P), (P, HT), (HT, GT)):
+        for lo, hi in ((0, HT), (HT, HT + P), (HT + P, GT)):
             quant_gated(last, lo, hi)
         for i in range(G):
             read_out(last, i, i + 1)
-            empty_out(last, i, i + 1, nc.vector.tensor_copy if i % 2 else nc.scalar.copy)
+            empty_out(nc.vector.tensor_copy if i % 2 else nc.scalar.copy, last, i, i + 1)
             store(last, i, i + 1)

@@ -25,8 +25,8 @@ GT = G * P
 HT = GT // 2
 WIDE_TOKENS = 136
 NARROW_TOKENS = 184
-REST_TOKENS = 48
-LAST_TOKENS = 192
+REST_TOKENS = 96
+LAST_TOKENS = 112
 WARM_UPS = 3
 
 
@@ -46,7 +46,9 @@ def tile_lstmcell_pa_t_w8_kernel(
         work = ctx.enter_context(tc.tile_pool(name="work", bufs=3))
         turnp = ctx.enter_context(tc.tile_pool(name="turnp", bufs=5))
         outp = ctx.enter_context(tc.tile_pool(name="outp", bufs=4))
+        pkeep = ctx.enter_context(tc.psum_pool(name="pkeep", bufs=2))
         pmix = ctx.enter_context(tc.psum_pool(name="pmix", bufs=1))
+        plate = ctx.enter_context(tc.psum_pool(name="plate", bufs=1))
         ctx.enter_context(tc.manual_schedule())
 
         ident = keep.tile([P, P], F32, name="ident")
@@ -65,9 +67,9 @@ def tile_lstmcell_pa_t_w8_kernel(
         wts = keep.tile([P, N_OUT], U8, name="wts", align_bytes=64)
 
         xb, me, xw, xbank, mbank, turned, q = {}, {}, {}, {}, {}, {}, {}
-        sig, gq, res, obank, gbank = {}, {}, {}, {}, []
+        sig, gq, res, obank = {}, {}, {}, {}
 
-        free_banks = ["bank%d" % i for i in range(8)]
+        free_banks = ["bank%d" % i for i in range(5)]
 
         def take_bank():
             name = free_banks.pop(0)
@@ -156,13 +158,18 @@ def tile_lstmcell_pa_t_w8_kernel(
         def turn_me(g, h):
             stays = h == 0 or g == last
             run = 2 if stays else P
-            pt, name = take_bank()
+            if h == 1:
+                pt, name = take_bank()
+            elif g == 2:
+                pt = plate.tile([P, GT], F32, name="late")
+            else:
+                pt = pkeep.tile([P, GT], F32, name="kept")
             bank = pt[:].rearrange("p (c u i) -> p u c i", u=2, i=run)
             per = P // run
             turn_words([[bank[:, u, per * i : per * (i + 1), :] for i in range(2)] for u in range(2)], me[g, h].bitcast(F32))
             dst = turned_tile(g)[:, h * HT * PACK : (h + 1) * HT * PACK].bitcast(F32)
             nc.scalar.copy(out=dst.rearrange("p (c i u) -> p c i u", i=run, u=2), in_=bank.rearrange("p u c i -> p c i u"))
-            mbank[g, h] = (pt, name)
+            mbank[g, h] = pt
             if not stays:
                 free_banks.append(name)
 
@@ -179,41 +186,36 @@ def tile_lstmcell_pa_t_w8_kernel(
 
         BOTH, ME, X = (0, 2 * GT), (0, GT), (GT, 2 * GT)
 
-        def gates(g, ts, lo=0, hi=GT):
+        def gates(g):
             if g not in sig:
                 fresh = work.tile([P, PACK, GT], F32, name="sig")
                 sig[g] = fresh
-            n = hi - lo
             codes, scales = q[g]
-            for t in ts:
+            for t in range(PACK):
                 cols = slice(t * P, (t + 1) * P)
                 pm, name = take_bank()
                 nc.tensor.matmul_mx(
-                    out=pm[:, 0:n], lhsT=wi[:, cols].bitcast(FP8X4), lhsT_scale=ws[:, cols],
-                    rhs=codes[:, GT + lo : GT + hi].bitcast(FP8X4), rhs_scale=scales[:, GT + lo : GT + hi], start=True, stop=False,
+                    out=pm[:], lhsT=wi[:, cols].bitcast(FP8X4), lhsT_scale=ws[:, cols],
+                    rhs=codes[:, GT:].bitcast(FP8X4), rhs_scale=scales[:, GT:], start=True, stop=False,
                 )
                 nc.tensor.matmul_mx(
-                    out=pm[:, 0:n], lhsT=wh[:, cols].bitcast(FP8X4), lhsT_scale=ws[4:, cols],
-                    rhs=codes[:, lo:hi].bitcast(FP8X4), rhs_scale=scales[:, lo:hi], start=False, stop=True,
+                    out=pm[:], lhsT=wh[:, cols].bitcast(FP8X4), lhsT_scale=ws[4:, cols],
+                    rhs=codes[:, 0:GT].bitcast(FP8X4), rhs_scale=scales[:, 0:GT], start=False, stop=True,
                 )
-                nc.scalar.activation(out=sig[g][:, t, lo:hi], in_=pm[:, 0:n], func=ACT.Sigmoid, bias=bias[:, t : t + 1])
-                gbank.append(name)
-
-        def free_gate_banks(n):
-            for i in range(n):
-                free_banks.append(gbank.pop(0))
+                nc.scalar.activation(out=sig[g][:, t, :], in_=pm[:], func=ACT.Sigmoid, bias=bias[:, t : t + 1])
+                free_banks.append(name)
 
         def gated(g, lo, hi):
             if g < last:
                 return turned[g + 1][:, (GT + lo) * PACK : (GT + hi) * PACK]
             if lo < HT:
-                return turned[g][:, (GT + lo) * PACK : (GT + hi) * PACK]
-            return turned[g - 1][:, lo * PACK : hi * PACK]
+                return turned[g - 1][:, lo * PACK : hi * PACK]
+            return turned[g][:, (HT + lo) * PACK : (HT + hi) * PACK]
 
         def gate(engine, g, lo, hi, from_psum):
             if from_psum:
                 run = 2
-                me_turned = mbank[g, lo // HT][0][:].bitcast(BF16)[:, lo % HT * PACK : (lo % HT + hi - lo) * PACK].rearrange(
+                me_turned = mbank[g, lo // HT][:].bitcast(BF16)[:, lo % HT * PACK : (lo % HT + hi - lo) * PACK].rearrange(
                     "p (c u i e) -> p c u e i", u=2, i=run, e=2
                 )
             else:
@@ -226,10 +228,6 @@ def tile_lstmcell_pa_t_w8_kernel(
                 op=MULT,
             )
 
-        def gate_kept(g, share):
-            gate(nc.vector, g, 0, share, True)
-            free_banks.append(mbank[g, 0][1])
-
         def quant_gated(g, lo, hi):
             if g not in gq:
                 codes = work.tile([P, GT], U32, name="gc", align_bytes=64)
@@ -238,11 +236,11 @@ def tile_lstmcell_pa_t_w8_kernel(
             codes, scales = gq[g]
             nc.vector.quantize_mx(out=codes[:, lo:hi].bitcast(FP8X4), scales=scales[:, lo:hi], in_=gated(g, lo, hi))
 
-        def read_out(g, i0, i1):
+        def read_out(g, i0, i1, late=False):
             if g not in res:
                 fresh = outp.tile([P, G, N_OUT], F32, name="res")
                 res[g] = fresh
-            po, name = take_bank()
+            po, name = (plate.tile([P, GT], F32, name="late"), None) if late else take_bank()
             for i in range(i0, i1):
                 cols = slice(i * P, (i + 1) * P)
                 nc.tensor.matmul_mx(
@@ -253,7 +251,8 @@ def tile_lstmcell_pa_t_w8_kernel(
 
         def empty_out(copy, g, i0, i1):
             copy(out=res[g][:, i0:i1, :].rearrange("p i n -> p (i n)"), in_=obank[g, i0][0])
-            free_banks.append(obank[g, i0][1])
+            if obank[g, i0][1]:
+                free_banks.append(obank[g, i0][1])
 
         def store(g, i0, i1):
             nc.sync.dma_start(out=out_hbm[:, g * G + i0 : g * G + i1, :], in_=res[g][:, i0:i1, :])
@@ -276,10 +275,9 @@ def tile_lstmcell_pa_t_w8_kernel(
         nc.scalar.activation(out=warm[:], in_=zeros[:, 0:1], func=ACT.Sigmoid)
         make_identity(nc, ident[:])
         nc.vector.tensor_copy(out=ident_bf[:], in_=ident[:])
-        idle, name = take_bank()
+        idle = plate.tile([P, GT], F32, name="late")
         for i in range(WARM_UPS):
             nc.tensor.matmul(idle[:, i * P : (i + 1) * P], lhsT=zeros[:], rhs=zeros[:], start=True, stop=True)
-        free_banks.append(name)
 
         load_x(0, (0,), "xb0")
         load_me(0, 0, 1, "me0")
@@ -321,8 +319,6 @@ def tile_lstmcell_pa_t_w8_kernel(
         nc.scalar.copy(out=spent[:, 3 * K :], in_=xall[2][:, 3 * K :].bitcast(FP8))
         for h in range(2):
             xw[2, h] = spent[:, h * 2 * K : (h + 1) * 2 * K]
-        gates(0, range(PACK))
-        free_gate_banks(3)
         scale_x(1, 0)
         scale_x(1, 1)
         quant_in(1, (ME, X))
@@ -335,64 +331,59 @@ def tile_lstmcell_pa_t_w8_kernel(
                 load_x_group(t + 3)
             if t % 2 == 0 and t + 2 < GROUPS:
                 load_me(t + 2, 0, 4)
-            share = WIDE_TOKENS if leave >= 0 else NARROW_TOKENS
-            turn_x(t, 0)
-            free_gate_banks(1)
-            turn_x(t, 1, t == last)
-            if leave >= 0:
-                empty_out(nc.scalar.copy, leave, 0, 2)
-            if t + 1 < GROUPS:
-                cast_both(t + 1)
+            shared = 1 <= leave and t < last
+            share = WIDE_TOKENS if shared else NARROW_TOKENS
+            gates(mix)
             gate(nc.gpsimd, mix, share, GT, False)
             if mix > 0:
-                gate_kept(mix, share)
+                gate(nc.vector, mix, 0, share, True)
+            if 0 <= leave:
+                read_out(leave, 0, 2)
+                empty_out(nc.scalar.copy, leave, 0, 2)
+                read_out(leave, 2, 4, shared)
+                if not shared:
+                    empty_out(nc.scalar.copy, leave, 2, 4)
+            turn_x(t, 0)
+            turn_x(t, 1, t == last)
+            if t < last:
+                cast_both(t + 1)
             turn_me(t, 1)
             turn_me(t, 0)
             scale_x(t, 0)
-            gates(mix + 1, (0, 1, 2))
             scale_x(t, 1)
-            free_gate_banks(1)
-            gates(mix + 1, (3,))
             if mix == 0:
-                gate_kept(mix, share)
-            if leave >= 0:
+                gate(nc.vector, mix, 0, share, True)
+            if shared:
                 empty_out(nc.vector.tensor_copy, leave, 2, 4)
+            if 0 <= leave:
                 store(leave, 0, G)
-            free_gate_banks(1)
-            if leave + 1 >= 0:
-                read_out(leave + 1, 0, 2)
-                read_out(leave + 1, 2, 4)
-            free_gate_banks(1)
-            quant_in(t, (ME, X) if mix == 1 else (BOTH,))
+            quant_in(t, (BOTH,) if shared or mix == 0 else (ME, X))
             quant_gated(mix, 0, GT)
 
         def leave_by_scalar(g):
             for i in (0, 2):
                 read_out(g, i, i + 2)
                 empty_out(nc.scalar.copy, g, i, i + 2)
-                store(g, i, i + 2)
+            store(g, 0, G)
 
-        free_gate_banks(1)
-        empty_out(nc.scalar.copy, last - 3, 0, 2)
-        store(last - 3, 0, 2)
+        gates(last - 1)
         gate(nc.gpsimd, last - 1, HT + REST_TOKENS, GT, False)
         gate(nc.vector, last - 1, 0, HT, True)
-        gates(last, range(PACK), 0, HT)
-        free_gate_banks(4)
-        gates(last, range(PACK), HT, GT)
-        free_banks.append(mbank[last - 1, 0][1])
+        read_out(last - 3, 0, 2)
+        empty_out(nc.scalar.copy, last - 3, 0, 2)
+        read_out(last - 3, 2, 4, True)
         empty_out(nc.vector.tensor_copy, last - 3, 2, 4)
-        store(last - 3, 2, 4)
-        free_gate_banks(4)
+        store(last - 3, 0, G)
+        gates(last)
         gate(nc.vector, last - 1, HT, HT + REST_TOKENS, False)
         quant_gated(last - 1, 0, HT)
         quant_gated(last - 1, HT, GT)
         leave_by_scalar(last - 2)
-        gate(nc.gpsimd, last, 0, LAST_TOKENS, False)
-        gate(nc.vector, last, LAST_TOKENS, HT, True)
-        gate(nc.vector, last, HT, GT, True)
+        gate(nc.gpsimd, last, HT, GT - LAST_TOKENS, False)
+        gate(nc.vector, last, 0, HT, True)
+        gate(nc.vector, last, GT - LAST_TOKENS, GT, True)
         leave_by_scalar(last - 1)
-        for lo, hi in ((0, HT), (HT, HT + P), (HT + P, GT)):
+        for lo, hi in ((0, P), (P, HT), (HT, GT)):
             quant_gated(last, lo, hi)
         for i in range(G):
             read_out(last, i, i + 1)

@@ -25,9 +25,9 @@ GT = G * P
 HT = GT // 2
 WIDE_TOKENS = 136
 NARROW_TOKENS = 184
-REST_TOKENS = 96
-LAST_TOKENS = 112
-WARM_UPS = 3
+REST_TOKENS = 80
+LAST_TOKENS = 80
+WARM_UPS = 4
 
 
 def tile_lstmcell_pa_t_w8_kernel(
@@ -160,7 +160,7 @@ def tile_lstmcell_pa_t_w8_kernel(
             run = 2 if stays else P
             if h == 1:
                 pt, name = take_bank()
-            elif g == 2:
+            elif g in (2, last):
                 pt = plate.tile([P, GT], F32, name="late")
             else:
                 pt = pkeep.tile([P, GT], F32, name="kept")
@@ -236,11 +236,11 @@ def tile_lstmcell_pa_t_w8_kernel(
             codes, scales = gq[g]
             nc.vector.quantize_mx(out=codes[:, lo:hi].bitcast(FP8X4), scales=scales[:, lo:hi], in_=gated(g, lo, hi))
 
-        def read_out(g, i0, i1, late=False):
+        def read_out(g, i0, i1, pool=None):
             if g not in res:
                 fresh = outp.tile([P, G, N_OUT], F32, name="res")
                 res[g] = fresh
-            po, name = (plate.tile([P, GT], F32, name="late"), None) if late else take_bank()
+            po, name = (pool[0].tile([P, GT], F32, name=pool[1]), None) if pool else take_bank()
             for i in range(i0, i1):
                 cols = slice(i * P, (i + 1) * P)
                 nc.tensor.matmul_mx(
@@ -315,8 +315,8 @@ def tile_lstmcell_pa_t_w8_kernel(
         turn_me(1, 1)
         nc.vector.tensor_copy(out=ws[:].rearrange("p (t m) -> p t m", t=PACK), in_=ws_raw[:].rearrange("p (m t) -> p t m", t=PACK))
         spent = turned[0][:, GT * PACK : 2 * GT * PACK]
-        nc.gpsimd.tensor_copy(out=spent[:, 0 : 3 * K], in_=xall[2][:, 0 : 3 * K].bitcast(FP8))
-        nc.scalar.copy(out=spent[:, 3 * K :], in_=xall[2][:, 3 * K :].bitcast(FP8))
+        nc.gpsimd.tensor_copy(out=spent[:, 0 : 2 * K], in_=xall[2][:, 0 : 2 * K].bitcast(FP8))
+        nc.scalar.copy(out=spent[:, 2 * K :], in_=xall[2][:, 2 * K :].bitcast(FP8))
         for h in range(2):
             xw[2, h] = spent[:, h * 2 * K : (h + 1) * 2 * K]
         scale_x(1, 0)
@@ -340,7 +340,7 @@ def tile_lstmcell_pa_t_w8_kernel(
             if 0 <= leave:
                 read_out(leave, 0, 2)
                 empty_out(nc.scalar.copy, leave, 0, 2)
-                read_out(leave, 2, 4, shared)
+                read_out(leave, 2, 4, (plate, "late") if shared else None)
                 if not shared:
                     empty_out(nc.scalar.copy, leave, 2, 4)
             turn_x(t, 0)
@@ -364,16 +364,17 @@ def tile_lstmcell_pa_t_w8_kernel(
             for i in (0, 2):
                 read_out(g, i, i + 2)
                 empty_out(nc.scalar.copy, g, i, i + 2)
-            store(g, 0, G)
+                store(g, i, i + 2)
 
         gates(last - 1)
         gate(nc.gpsimd, last - 1, HT + REST_TOKENS, GT, False)
+        read_out(last - 3, 0, 2, (pkeep, "kept"))
+        empty_out(nc.vector.tensor_copy, last - 3, 0, 2)
+        store(last - 3, 0, 2)
+        read_out(last - 3, 2, 4)
+        empty_out(nc.scalar.copy, last - 3, 2, 4)
+        store(last - 3, 2, 4)
         gate(nc.vector, last - 1, 0, HT, True)
-        read_out(last - 3, 0, 2)
-        empty_out(nc.scalar.copy, last - 3, 0, 2)
-        read_out(last - 3, 2, 4, True)
-        empty_out(nc.vector.tensor_copy, last - 3, 2, 4)
-        store(last - 3, 0, G)
         gates(last)
         gate(nc.vector, last - 1, HT, HT + REST_TOKENS, False)
         quant_gated(last - 1, 0, HT)

@@ -25,6 +25,7 @@ GT = G * P
 HT = GT // 2
 WIDE_TOKENS = 136
 NARROW_TOKENS = 184
+FIRST_TOKENS = 212
 REST_TOKENS = 80
 LAST_TOKENS = 80
 WARM_UPS = 4
@@ -46,9 +47,8 @@ def tile_lstmcell_pa_t_w8_kernel(
         work = ctx.enter_context(tc.tile_pool(name="work", bufs=3))
         turnp = ctx.enter_context(tc.tile_pool(name="turnp", bufs=5))
         outp = ctx.enter_context(tc.tile_pool(name="outp", bufs=4))
-        pkeep = ctx.enter_context(tc.psum_pool(name="pkeep", bufs=2))
+        pkeep = ctx.enter_context(tc.psum_pool(name="pkeep", bufs=1))
         pmix = ctx.enter_context(tc.psum_pool(name="pmix", bufs=1))
-        plate = ctx.enter_context(tc.psum_pool(name="plate", bufs=1))
         ctx.enter_context(tc.manual_schedule())
 
         ident = keep.tile([P, P], F32, name="ident")
@@ -155,15 +155,18 @@ def tile_lstmcell_pa_t_w8_kernel(
                 )
             free_banks.append(name)
 
+        def kept_name(g):
+            if g in (2, last):
+                return "spare"
+            return "kept%d" % ((g if g < 2 else g + 1) % 2)
+
         def turn_me(g, h):
             stays = h == 0 or g == last
             run = 2 if stays else P
             if h == 1:
                 pt, name = take_bank()
-            elif g in (2, last):
-                pt = plate.tile([P, GT], F32, name="late")
             else:
-                pt = pkeep.tile([P, GT], F32, name="kept")
+                pt = pkeep.tile([P, GT], F32, name=kept_name(g))
             bank = pt[:].rearrange("p (c u i) -> p u c i", u=2, i=run)
             per = P // run
             turn_words([[bank[:, u, per * i : per * (i + 1), :] for i in range(2)] for u in range(2)], me[g, h].bitcast(F32))
@@ -236,11 +239,11 @@ def tile_lstmcell_pa_t_w8_kernel(
             codes, scales = gq[g]
             nc.vector.quantize_mx(out=codes[:, lo:hi].bitcast(FP8X4), scales=scales[:, lo:hi], in_=gated(g, lo, hi))
 
-        def read_out(g, i0, i1, pool=None):
+        def read_out(g, i0, i1, bank=None):
             if g not in res:
                 fresh = outp.tile([P, G, N_OUT], F32, name="res")
                 res[g] = fresh
-            po, name = (pool[0].tile([P, GT], F32, name=pool[1]), None) if pool else take_bank()
+            po, name = (pkeep.tile([P, GT], F32, name=bank), None) if bank else take_bank()
             for i in range(i0, i1):
                 cols = slice(i * P, (i + 1) * P)
                 nc.tensor.matmul_mx(
@@ -275,7 +278,7 @@ def tile_lstmcell_pa_t_w8_kernel(
         nc.scalar.activation(out=warm[:], in_=zeros[:, 0:1], func=ACT.Sigmoid)
         make_identity(nc, ident[:])
         nc.vector.tensor_copy(out=ident_bf[:], in_=ident[:])
-        idle = plate.tile([P, GT], F32, name="late")
+        idle = pkeep.tile([P, GT], F32, name="spare")
         for i in range(WARM_UPS):
             nc.tensor.matmul(idle[:, i * P : (i + 1) * P], lhsT=zeros[:], rhs=zeros[:], start=True, stop=True)
 
@@ -286,10 +289,11 @@ def tile_lstmcell_pa_t_w8_kernel(
         load_me(0, 1, 1, "me0")
         load_x_group(1)
         load_words(wi_raw, wi_words)
+        load_me(1, 0, 1, "me0")
         load_words(wh_raw, wh_words)
         load_scale_rows(nc.sync, ws_raw, 0, wi_scales)
+        load_me(1, 1, 1, "me0")
         load_scale_rows(nc.gpsimd, ws_raw, 4, wh_scales)
-        load_me(1, 0, 2, "me1")
         nc.sync.dma_start(out=bias[:], in_=mem_bias.rearrange("(p t) -> p t", t=PACK))
         load_x_group(2)
         load_x_group(3)
@@ -307,7 +311,7 @@ def tile_lstmcell_pa_t_w8_kernel(
         scale_x(0, 0)
         scale_x(0, 1)
         permute(nc.gpsimd.tensor_copy, wi[:], wi_raw[:])
-        permute(nc.gpsimd.tensor_copy, wh[:], wh_raw[:])
+        permute(nc.scalar.copy, wh[:], wh_raw[:])
         quant_in(0, (ME, X))
         turn_x(1, 0)
         turn_x(1, 1)
@@ -331,18 +335,20 @@ def tile_lstmcell_pa_t_w8_kernel(
                 load_x_group(t + 3)
             if t % 2 == 0 and t + 2 < GROUPS:
                 load_me(t + 2, 0, 4)
-            shared = 1 <= leave and t < last
-            share = WIDE_TOKENS if shared else NARROW_TOKENS
+            shared = 0 <= leave and t < last
+            share = WIDE_TOKENS if shared else NARROW_TOKENS if mix > 0 else FIRST_TOKENS
             gates(mix)
             gate(nc.gpsimd, mix, share, GT, False)
-            if mix > 0:
-                gate(nc.vector, mix, 0, share, True)
             if 0 <= leave:
                 read_out(leave, 0, 2)
                 empty_out(nc.scalar.copy, leave, 0, 2)
-                read_out(leave, 2, 4, (plate, "late") if shared else None)
+                read_out(leave, 2, 4, None if not shared else "spare" if leave else kept_name(1))
                 if not shared:
                     empty_out(nc.scalar.copy, leave, 2, 4)
+                if leave == 0:
+                    empty_out(nc.vector.tensor_copy, leave, 2, 4)
+            if mix > 0:
+                gate(nc.vector, mix, 0, share, True)
             turn_x(t, 0)
             turn_x(t, 1, t == last)
             if t < last:
@@ -353,11 +359,11 @@ def tile_lstmcell_pa_t_w8_kernel(
             scale_x(t, 1)
             if mix == 0:
                 gate(nc.vector, mix, 0, share, True)
-            if shared:
+            if shared and leave:
                 empty_out(nc.vector.tensor_copy, leave, 2, 4)
             if 0 <= leave:
                 store(leave, 0, G)
-            quant_in(t, (BOTH,) if shared or mix == 0 else (ME, X))
+            quant_in(t, (BOTH,) if shared and leave or mix == 0 else (ME, X))
             quant_gated(mix, 0, GT)
 
         def leave_by_scalar(g):
@@ -368,7 +374,7 @@ def tile_lstmcell_pa_t_w8_kernel(
 
         gates(last - 1)
         gate(nc.gpsimd, last - 1, HT + REST_TOKENS, GT, False)
-        read_out(last - 3, 0, 2, (pkeep, "kept"))
+        read_out(last - 3, 0, 2, kept_name(last - 2))
         empty_out(nc.vector.tensor_copy, last - 3, 0, 2)
         store(last - 3, 0, 2)
         read_out(last - 3, 2, 4)

@@ -23,12 +23,15 @@ G = 4
 GROUPS = SLABS // G
 GT = G * P
 HT = GT // 2
+HK = 2 * K
+ROTATING = 5
+
 WIDE_TOKENS = 136
 NARROW_TOKENS = 184
 FIRST_TOKENS = 212
 REST_TOKENS = 80
 LAST_TOKENS = 80
-WARM_UPS = 4
+WARM_UPS = 5
 
 
 def tile_lstmcell_pa_t_w8_kernel(
@@ -66,49 +69,67 @@ def tile_lstmcell_pa_t_w8_kernel(
         ws = keep.tile([P, CH], U8, name="ws", align_bytes=64)
         wts = keep.tile([P, N_OUT], U8, name="wts", align_bytes=64)
 
-        xb, me, xw, xbank, mbank, turned, q = {}, {}, {}, {}, {}, {}, {}
-        sig, gq, res, obank = {}, {}, {}, {}
+        x_group, x_half, me, wide, x_bank, me_bank, turned, coded = {}, {}, {}, {}, {}, {}, {}, {}
+        sig, gated_coded, res, out_bank = {}, {}, {}, {}
 
-        free_banks = ["bank%d" % i for i in range(5)]
+        free_banks = ["bank%d" % i for i in range(ROTATING)]
 
         def take_bank():
             name = free_banks.pop(0)
             return pmix.tile([P, GT], F32, name=name), name
 
-        def load_x(g, halves=(0, 1), name="xb"):
-            n = len(halves) * 2
-            t = xin.tile([P, n * K], U8, name=name)
-            i0 = g * G + 2 * halves[0]
-            nc.sync.dma_start(out=t[:].rearrange("p (i k) -> p i k", k=K), in_=x_hbm[:, i0 : i0 + n, :])
-            for j, h in enumerate(halves):
-                xb[g, h] = t[:, j * 2 * K : (j + 1) * 2 * K]
+        def kept_name(g):
+            if g in (2, last):
+                return "spare"
+            return "kept%d" % ((g if g < 2 else g + 1) % 2)
 
-        def load_me(g, first, count, name="me"):
-            t = mein.tile([P, count * 2 * K], BF16, name=name)
-            i0 = g * G + 2 * first
-            nc.sync.dma_start(out=t[:].rearrange("p (i k) -> p i k", k=K), in_=me_hbm[:, i0 : i0 + 2 * count, :])
-            for j in range(count):
-                me[g + (first + j) // 2, (first + j) % 2] = t[:, j * 2 * K : (j + 1) * 2 * K]
+        def load_x_half(g, h):
+            t = xin.tile([P, HK], U8, name="x_first")
+            i0 = g * G + 2 * h
+            nc.sync.dma_start(out=t[:].rearrange("p (i k) -> p i k", k=K), in_=x_hbm[:, i0 : i0 + 2, :])
+            x_half[g, h] = t[:]
 
-        def cast(copy, g, h):
-            fresh = work.tile([P, 2 * K], BF16, name="xw%d" % h)
-            copy(out=fresh[:], in_=xb[g, h].bitcast(FP8))
-            xw[g, h] = fresh[:]
-
-        def cast_both(g):
-            fresh = work.tile([P, G * K], BF16, name="xw")
-            nc.scalar.copy(out=fresh[:], in_=xall[g].bitcast(FP8))
-            for h in range(2):
-                xw[g, h] = fresh[:, h * 2 * K : (h + 1) * 2 * K]
-
-        xall = {}
-
-        def load_x_group(g):
-            t = xin.tile([P, G * K], U8, name="xb")
+        def load_x(g):
+            t = xin.tile([P, G * K], U8, name="x_group")
             nc.sync.dma_start(out=t[:].rearrange("p (i k) -> p i k", k=K), in_=x_hbm[:, g * G : (g + 1) * G, :])
-            xall[g] = t[:]
+            x_group[g] = t[:]
             for h in range(2):
-                xb[g, h] = t[:, h * 2 * K : (h + 1) * 2 * K]
+                x_half[g, h] = t[:, h * HK : (h + 1) * HK]
+
+        def load_me_half(g, h):
+            t = mein.tile([P, HK], BF16, name="me_first")
+            i0 = g * G + 2 * h
+            nc.sync.dma_start(out=t[:].rearrange("p (i k) -> p i k", k=K), in_=me_hbm[:, i0 : i0 + 2, :])
+            me[g, h] = t[:]
+
+        def load_me_pair(g):
+            t = mein.tile([P, 4 * HK], BF16, name="me_pair")
+            nc.sync.dma_start(out=t[:].rearrange("p (i k) -> p i k", k=K), in_=me_hbm[:, g * G : (g + 2) * G, :])
+            for j in range(4):
+                me[g + j // 2, j % 2] = t[:, j * HK : (j + 1) * HK]
+
+        def load_words(tile, hbm):
+            nc.sync.dma_start(out=tile[:].bitcast(I32), in_=hbm[0].rearrange("p n t -> p (n t)").bitcast(I32))
+
+        def load_scale_rows(queue, tile, row0, hbm, quadrants):
+            for h in quadrants:
+                queue.dma_start(
+                    out=tile[32 * h + row0 : 32 * h + row0 + 4, :].bitcast(I32), in_=hbm[0, 4 * h : 4 * h + 4, :].bitcast(I32)
+                )
+
+        def permute_words(copy, dst, src):
+            copy(out=dst.rearrange("p (t c i) -> p c t i", t=PACK, i=4), in_=src.rearrange("p (c i t) -> p c t i", t=PACK, i=4))
+
+        def widen_half(g, h):
+            fresh = work.tile([P, HK], BF16, name="wide%d" % h)
+            nc.scalar.copy(out=fresh[:], in_=x_half[g, h].bitcast(FP8))
+            wide[g, h] = fresh[:]
+
+        def widen(g):
+            fresh = work.tile([P, G * K], BF16, name="wide")
+            nc.scalar.copy(out=fresh[:], in_=x_group[g].bitcast(FP8))
+            for h in range(2):
+                wide[g, h] = fresh[:, h * HK : (h + 1) * HK]
 
         def turned_tile(g):
             if g not in turned:
@@ -125,18 +146,18 @@ def tile_lstmcell_pa_t_w8_kernel(
             pt, name = take_bank()
             if as_words:
                 bank = pt[:].rearrange("p (u i r) -> p u i r", u=2, i=2)
-                turn_words([[bank[:, u, i, :] for i in range(2)] for u in range(2)], xw[g, h].bitcast(F32))
+                turn_words([[bank[:, u, i, :] for i in range(2)] for u in range(2)], wide[g, h].bitcast(F32))
             else:
-                bank = pt[:].bitcast(BF16).rearrange("p (i c j r) -> p i j c r", i=2, j=PACK, r=2)
+                bank = pt[:].bitcast(BF16).rearrange("p (i c t r) -> p i t c r", i=2, t=PACK, r=2)
                 for i in range(2):
-                    for j in range(PACK):
+                    for t in range(PACK):
                         nc.tensor.matmul(
-                            bank[:, i, j, :, :], lhsT=xw[g, h][:, i * K + j : (i + 1) * K : PACK], rhs=ident_bf[:], start=True, stop=True
+                            bank[:, i, t, :, :], lhsT=wide[g, h][:, i * K + t : (i + 1) * K : PACK], rhs=ident_bf[:], start=True, stop=True
                         )
-            xbank[g, h] = (pt, name, as_words)
+            x_bank[g, h] = (pt, name, as_words)
 
         def scale_x(g, h):
-            pt, name, as_words = xbank[g, h]
+            pt, name, as_words = x_bank[g, h]
             lo = (GT + h * HT) * PACK
             dst, src = turned_tile(g)[:, lo : lo + HT * PACK], pt[:].bitcast(BF16)
             if as_words:
@@ -148,17 +169,12 @@ def tile_lstmcell_pa_t_w8_kernel(
                 )
             else:
                 nc.vector.tensor_tensor(
-                    out=dst.rearrange("p (c r j) -> p c r j", r=2, j=PACK),
-                    in0=src.rearrange("p (c j r) -> p c r j", r=2, j=PACK),
+                    out=dst.rearrange("p (c r t) -> p c r t", r=2, t=PACK),
+                    in0=src.rearrange("p (c t r) -> p c r t", r=2, t=PACK),
                     in1=s4[:].unsqueeze(1).unsqueeze(1).to_broadcast([P, HT // 2, 2, PACK]),
                     op=MULT,
                 )
             free_banks.append(name)
-
-        def kept_name(g):
-            if g in (2, last):
-                return "spare"
-            return "kept%d" % ((g if g < 2 else g + 1) % 2)
 
         def turn_me(g, h):
             stays = h == 0 or g == last
@@ -172,28 +188,24 @@ def tile_lstmcell_pa_t_w8_kernel(
             turn_words([[bank[:, u, per * i : per * (i + 1), :] for i in range(2)] for u in range(2)], me[g, h].bitcast(F32))
             dst = turned_tile(g)[:, h * HT * PACK : (h + 1) * HT * PACK].bitcast(F32)
             nc.scalar.copy(out=dst.rearrange("p (c i u) -> p c i u", i=run, u=2), in_=bank.rearrange("p u c i -> p c i u"))
-            mbank[g, h] = pt
+            me_bank[g, h] = pt
             if not stays:
                 free_banks.append(name)
 
-        def quant_in(g, parts):
-            if g not in q:
-                codes = work.tile([P, 2 * GT], U32, name="qc", align_bytes=64)
-                scales = work.tile([P, 2 * GT], U8, name="qs", align_bytes=64)
-                q[g] = (codes, scales)
-            codes, scales = q[g]
-            for lo, hi in parts:
+        def quantise_inputs(g, pieces):
+            codes = work.tile([P, 2 * GT], U32, name="codes", align_bytes=64)
+            scales = work.tile([P, 2 * GT], U8, name="scales", align_bytes=64)
+            coded[g] = (codes, scales)
+            n = 2 * GT // pieces
+            for lo in range(0, 2 * GT, n):
                 nc.vector.quantize_mx(
-                    out=codes[:, lo:hi].bitcast(FP8X4), scales=scales[:, lo:hi], in_=turned[g][:, lo * PACK : hi * PACK]
+                    out=codes[:, lo : lo + n].bitcast(FP8X4), scales=scales[:, lo : lo + n], in_=turned[g][:, lo * PACK : (lo + n) * PACK]
                 )
 
-        BOTH, ME, X = (0, 2 * GT), (0, GT), (GT, 2 * GT)
-
-        def gates(g):
-            if g not in sig:
-                fresh = work.tile([P, PACK, GT], F32, name="sig")
-                sig[g] = fresh
-            codes, scales = q[g]
+        def sigmoids(g):
+            fresh = work.tile([P, PACK, GT], F32, name="sig")
+            sig[g] = fresh
+            codes, scales = coded[g]
             for t in range(PACK):
                 cols = slice(t * P, (t + 1) * P)
                 pm, name = take_bank()
@@ -205,7 +217,7 @@ def tile_lstmcell_pa_t_w8_kernel(
                     out=pm[:], lhsT=wh[:, cols].bitcast(FP8X4), lhsT_scale=ws[4:, cols],
                     rhs=codes[:, 0:GT].bitcast(FP8X4), rhs_scale=scales[:, 0:GT], start=False, stop=True,
                 )
-                nc.scalar.activation(out=sig[g][:, t, :], in_=pm[:], func=ACT.Sigmoid, bias=bias[:, t : t + 1])
+                nc.scalar.activation(out=fresh[:, t, :], in_=pm[:], func=ACT.Sigmoid, bias=bias[:, t : t + 1])
                 free_banks.append(name)
 
         def gated(g, lo, hi):
@@ -218,7 +230,7 @@ def tile_lstmcell_pa_t_w8_kernel(
         def gate(engine, g, lo, hi, from_psum):
             if from_psum:
                 run = 2
-                me_turned = mbank[g, lo // HT][:].bitcast(BF16)[:, lo % HT * PACK : (lo % HT + hi - lo) * PACK].rearrange(
+                me_turned = me_bank[g, lo // HT][:].bitcast(BF16)[:, lo % HT * PACK : (lo % HT + hi - lo) * PACK].rearrange(
                     "p (c u i e) -> p c u e i", u=2, i=run, e=2
                 )
             else:
@@ -231,12 +243,12 @@ def tile_lstmcell_pa_t_w8_kernel(
                 op=MULT,
             )
 
-        def quant_gated(g, lo, hi):
-            if g not in gq:
-                codes = work.tile([P, GT], U32, name="gc", align_bytes=64)
-                scales = work.tile([P, GT], U8, name="gs", align_bytes=64)
-                gq[g] = (codes, scales)
-            codes, scales = gq[g]
+        def quantise_gated(g, lo, hi):
+            if g not in gated_coded:
+                codes = work.tile([P, GT], U32, name="gated_codes", align_bytes=64)
+                scales = work.tile([P, GT], U8, name="gated_scales", align_bytes=64)
+                gated_coded[g] = (codes, scales)
+            codes, scales = gated_coded[g]
             nc.vector.quantize_mx(out=codes[:, lo:hi].bitcast(FP8X4), scales=scales[:, lo:hi], in_=gated(g, lo, hi))
 
         def read_out(g, i0, i1, bank=None):
@@ -244,33 +256,23 @@ def tile_lstmcell_pa_t_w8_kernel(
                 fresh = outp.tile([P, G, N_OUT], F32, name="res")
                 res[g] = fresh
             po, name = (pkeep.tile([P, GT], F32, name=bank), None) if bank else take_bank()
+            codes, scales = gated_coded[g]
             for i in range(i0, i1):
                 cols = slice(i * P, (i + 1) * P)
                 nc.tensor.matmul_mx(
-                    out=po[:, (i - i0) * N_OUT : (i - i0 + 1) * N_OUT], lhsT=gq[g][0][:, cols].bitcast(FP8X4), lhsT_scale=gq[g][1][:, cols],
+                    out=po[:, (i - i0) * N_OUT : (i - i0 + 1) * N_OUT], lhsT=codes[:, cols].bitcast(FP8X4), lhsT_scale=scales[:, cols],
                     rhs=wt[:].bitcast(FP8X4), rhs_scale=wts[:], start=True, stop=True,
                 )
-            obank[g, i0] = (po[:, 0 : (i1 - i0) * N_OUT], name)
+            out_bank[g, i0] = (po[:, 0 : (i1 - i0) * N_OUT], name)
 
         def empty_out(copy, g, i0, i1):
-            copy(out=res[g][:, i0:i1, :].rearrange("p i n -> p (i n)"), in_=obank[g, i0][0])
-            if obank[g, i0][1]:
-                free_banks.append(obank[g, i0][1])
+            src, name = out_bank[g, i0]
+            copy(out=res[g][:, i0:i1, :].rearrange("p i n -> p (i n)"), in_=src)
+            if name:
+                free_banks.append(name)
 
         def store(g, i0, i1):
             nc.sync.dma_start(out=out_hbm[:, g * G + i0 : g * G + i1, :], in_=res[g][:, i0:i1, :])
-
-        def permute(copy, dst, src):
-            copy(out=dst.rearrange("p (t c i) -> p c t i", t=PACK, i=4), in_=src.rearrange("p (c i t) -> p c t i", t=PACK, i=4))
-
-        def load_scale_rows(queue, tile, row0, hbm):
-            for h in range(4):
-                queue.dma_start(
-                    out=tile[32 * h + row0 : 32 * h + row0 + 4, :].bitcast(I32), in_=hbm[0, 4 * h : 4 * h + 4, :].bitcast(I32)
-                )
-
-        def load_words(tile, hbm):
-            nc.sync.dma_start(out=tile[:].bitcast(I32), in_=hbm[0].rearrange("p n t -> p (n t)").bitcast(I32))
 
         nc.vector.memset(zeros[:], 0.0)
         nc.vector.memset(ws_raw[:].bitcast(I32), 0)
@@ -280,91 +282,92 @@ def tile_lstmcell_pa_t_w8_kernel(
         nc.vector.tensor_copy(out=ident_bf[:], in_=ident[:])
         idle = pkeep.tile([P, GT], F32, name="spare")
         for i in range(WARM_UPS):
-            nc.tensor.matmul(idle[:, i * P : (i + 1) * P], lhsT=zeros[:], rhs=zeros[:], start=True, stop=True)
+            nc.tensor.matmul(idle[:, i % G * P : (i % G + 1) * P], lhsT=zeros[:], rhs=zeros[:], start=True, stop=True)
 
-        load_x(0, (0,), "xb0")
-        load_me(0, 0, 1, "me0")
+        load_x_half(0, 0)
+        load_me_half(0, 0)
         nc.sync.dma_start(out=s4[:], in_=x_scale.rearrange("o (p t) -> p (o t)", t=PACK))
-        load_x(0, (1,), "xb0")
-        load_me(0, 1, 1, "me0")
-        load_x_group(1)
+        load_x_half(0, 1)
+        load_me_half(0, 1)
+        load_x(1)
         load_words(wi_raw, wi_words)
-        load_me(1, 0, 1, "me0")
+        load_me_half(1, 0)
         load_words(wh_raw, wh_words)
-        load_scale_rows(nc.sync, ws_raw, 0, wi_scales)
-        load_me(1, 1, 1, "me0")
-        load_scale_rows(nc.gpsimd, ws_raw, 4, wh_scales)
+        load_scale_rows(nc.sync, ws_raw, 0, wi_scales, range(4))
+        load_scale_rows(nc.gpsimd, ws_raw, 4, wh_scales, range(3))
+        load_scale_rows(nc.sync, ws_raw, 4, wh_scales, (3,))
+        load_me_half(1, 1)
         nc.sync.dma_start(out=bias[:], in_=mem_bias.rearrange("(p t) -> p t", t=PACK))
-        load_x_group(2)
-        load_x_group(3)
-        load_me(2, 0, 4)
-        load_x_group(4)
+        load_x(2)
+        load_x(3)
+        load_me_pair(2)
+        load_x(4)
 
-        cast(nc.scalar.copy, 0, 0)
-        cast(nc.scalar.copy, 0, 1)
+        widen_half(0, 0)
+        widen_half(0, 1)
         turn_me(0, 0)
         turn_x(0, 0)
-        turn_x(0, 1)
-        cast(nc.scalar.copy, 1, 0)
-        cast(nc.scalar.copy, 1, 1)
+        turn_x(0, 1, as_words=True)
+        widen_half(1, 0)
+        widen_half(1, 1)
         turn_me(0, 1)
         scale_x(0, 0)
         scale_x(0, 1)
-        permute(nc.gpsimd.tensor_copy, wi[:], wi_raw[:])
-        permute(nc.scalar.copy, wh[:], wh_raw[:])
-        quant_in(0, (ME, X))
-        turn_x(1, 0)
-        turn_x(1, 1)
-        turn_me(1, 0)
-        turn_me(1, 1)
-        nc.vector.tensor_copy(out=ws[:].rearrange("p (t m) -> p t m", t=PACK), in_=ws_raw[:].rearrange("p (m t) -> p t m", t=PACK))
-        spent = turned[0][:, GT * PACK : 2 * GT * PACK]
-        nc.gpsimd.tensor_copy(out=spent[:, 0 : 2 * K], in_=xall[2][:, 0 : 2 * K].bitcast(FP8))
-        nc.scalar.copy(out=spent[:, 2 * K :], in_=xall[2][:, 2 * K :].bitcast(FP8))
+        permute_words(nc.gpsimd.tensor_copy, wi[:], wi_raw[:])
+        permute_words(nc.scalar.copy, wh[:], wh_raw[:])
+        quantise_inputs(0, 2)
         for h in range(2):
-            xw[2, h] = spent[:, h * 2 * K : (h + 1) * 2 * K]
+            turn_x(1, h)
+            turn_me(1, h)
+        nc.vector.tensor_copy(out=ws[:].rearrange("p (t m) -> p t m", t=PACK), in_=ws_raw[:].rearrange("p (m t) -> p t m", t=PACK))
+        for h, copy in enumerate((nc.gpsimd.tensor_copy, nc.scalar.copy)):
+            wide[2, h] = turned[0][:, GT * PACK + h * HK : GT * PACK + (h + 1) * HK]
+            copy(out=wide[2, h], in_=x_half[2, h].bitcast(FP8))
         scale_x(1, 0)
         scale_x(1, 1)
-        quant_in(1, (ME, X))
+        quantise_inputs(1, 2)
         load_words(wt, wt_words)
-        load_scale_rows(nc.sync, wts, 0, wt_scales)
+        load_scale_rows(nc.sync, wts, 0, wt_scales, range(4))
 
-        for t in range(2, GROUPS):
-            mix, leave = t - 2, t - 4
-            if t + 3 < GROUPS:
-                load_x_group(t + 3)
-            if t % 2 == 0 and t + 2 < GROUPS:
-                load_me(t + 2, 0, 4)
-            shared = 0 <= leave and t < last
+        for s in range(2, GROUPS):
+            mix, leave = s - 2, s - 4
+            if s + 3 < GROUPS:
+                load_x(s + 3)
+            if s % 2 == 0 and s + 2 < GROUPS:
+                load_me_pair(s + 2)
+            shared = 0 <= leave and s < last
             share = WIDE_TOKENS if shared else NARROW_TOKENS if mix > 0 else FIRST_TOKENS
-            gates(mix)
+            sigmoids(mix)
             gate(nc.gpsimd, mix, share, GT, False)
             if 0 <= leave:
                 read_out(leave, 0, 2)
                 empty_out(nc.scalar.copy, leave, 0, 2)
-                read_out(leave, 2, 4, None if not shared else "spare" if leave else kept_name(1))
-                if not shared:
-                    empty_out(nc.scalar.copy, leave, 2, 4)
-                if leave == 0:
-                    empty_out(nc.vector.tensor_copy, leave, 2, 4)
+            if leave == 0:
+                read_out(leave, 2, 4, kept_name(s))
+                empty_out(nc.vector.tensor_copy, leave, 2, 4)
+            elif shared:
+                read_out(leave, 2, 4, "spare")
+            elif s == last:
+                read_out(leave, 2, 4)
+                empty_out(nc.scalar.copy, leave, 2, 4)
             if mix > 0:
                 gate(nc.vector, mix, 0, share, True)
-            turn_x(t, 0)
-            turn_x(t, 1, t == last)
-            if t < last:
-                cast_both(t + 1)
-            turn_me(t, 1)
-            turn_me(t, 0)
-            scale_x(t, 0)
-            scale_x(t, 1)
+            turn_x(s, 0)
+            turn_x(s, 1)
+            if s < last:
+                widen(s + 1)
+            turn_me(s, 1)
+            turn_me(s, 0)
+            scale_x(s, 0)
+            scale_x(s, 1)
             if mix == 0:
                 gate(nc.vector, mix, 0, share, True)
-            if shared and leave:
+            if shared and leave > 0:
                 empty_out(nc.vector.tensor_copy, leave, 2, 4)
             if 0 <= leave:
                 store(leave, 0, G)
-            quant_in(t, (BOTH,) if shared and leave or mix == 0 else (ME, X))
-            quant_gated(mix, 0, GT)
+            quantise_inputs(s, 1 if shared and leave > 0 or mix == 0 else 2)
+            quantise_gated(mix, 0, GT)
 
         def leave_by_scalar(g):
             for i in (0, 2):
@@ -372,7 +375,7 @@ def tile_lstmcell_pa_t_w8_kernel(
                 empty_out(nc.scalar.copy, g, i, i + 2)
                 store(g, i, i + 2)
 
-        gates(last - 1)
+        sigmoids(last - 1)
         gate(nc.gpsimd, last - 1, HT + REST_TOKENS, GT, False)
         read_out(last - 3, 0, 2, kept_name(last - 2))
         empty_out(nc.vector.tensor_copy, last - 3, 0, 2)
@@ -381,17 +384,17 @@ def tile_lstmcell_pa_t_w8_kernel(
         empty_out(nc.scalar.copy, last - 3, 2, 4)
         store(last - 3, 2, 4)
         gate(nc.vector, last - 1, 0, HT, True)
-        gates(last)
+        sigmoids(last)
         gate(nc.vector, last - 1, HT, HT + REST_TOKENS, False)
-        quant_gated(last - 1, 0, HT)
-        quant_gated(last - 1, HT, GT)
+        quantise_gated(last - 1, 0, HT)
+        quantise_gated(last - 1, HT, GT)
         leave_by_scalar(last - 2)
         gate(nc.gpsimd, last, HT, GT - LAST_TOKENS, False)
         gate(nc.vector, last, 0, HT, True)
         gate(nc.vector, last, GT - LAST_TOKENS, GT, True)
         leave_by_scalar(last - 1)
         for lo, hi in ((0, P), (P, HT), (HT, GT)):
-            quant_gated(last, lo, hi)
+            quantise_gated(last, lo, hi)
         for i in range(G):
             read_out(last, i, i + 1)
             empty_out(nc.vector.tensor_copy if i % 2 else nc.scalar.copy, last, i, i + 1)

@@ -24,7 +24,7 @@ GROUPS = SLABS // G
 GT = G * P
 HT = GT // 2
 HK = 2 * K
-ROTATING = 5
+ROTATING = 6
 
 WIDE_TOKENS = 136
 NARROW_TOKENS = 184
@@ -70,7 +70,7 @@ def tile_lstmcell_pa_t_w8_kernel(
         wts = keep.tile([P, N_OUT], U8, name="wts", align_bytes=64)
 
         x_group, x_half, me, wide, x_bank, me_bank, turned, coded = {}, {}, {}, {}, {}, {}, {}, {}
-        sig, gated_coded, res, out_bank = {}, {}, {}, {}
+        sig, gated_coded, res, out_bank, lent = {}, {}, {}, {}, {}
 
         free_banks = ["bank%d" % i for i in range(ROTATING)]
 
@@ -79,8 +79,6 @@ def tile_lstmcell_pa_t_w8_kernel(
             return pmix.tile([P, GT], F32, name=name), name
 
         def kept_name(g):
-            if g in (2, last):
-                return "spare"
             return "kept%d" % ((g if g < 2 else g + 1) % 2)
 
         def load_x_half(g, h):
@@ -125,11 +123,24 @@ def tile_lstmcell_pa_t_w8_kernel(
             nc.scalar.copy(out=fresh[:], in_=x_half[g, h].bitcast(FP8))
             wide[g, h] = fresh[:]
 
+        def widen_sorted(copy, dst, codes, by_read):
+            walk = "p u m e" if by_read else "p m u e"
+            copy(out=dst.rearrange("p (u m e) -> " + walk, u=2, e=2), in_=codes.bitcast(FP8).rearrange("p (m u e) -> " + walk, u=2, e=2))
+            return dst.bitcast(F32).rearrange("p (u m) -> p u m", u=2)
+
         def widen(g):
             fresh = work.tile([P, G * K], BF16, name="wide")
-            nc.scalar.copy(out=fresh[:], in_=x_group[g].bitcast(FP8))
+            words = widen_sorted(nc.scalar.copy, fresh[:], x_group[g], g % 3 != 0)
             for h in range(2):
-                wide[g, h] = fresh[:, h * HK : (h + 1) * HK]
+                wide[g, h] = words[:, :, h * HT : (h + 1) * HT]
+
+        def turn_x_sorted(g, h):
+            pt, name = take_bank()
+            bank = pt[:].rearrange("p (c u r) -> p u c r", u=2, r=2)
+            for i in range(2):
+                for u in range(2):
+                    nc.tensor.transpose(bank[:, u, 64 * i : 64 * (i + 1), :], wide[g, h][:, u, i * P : (i + 1) * P], ident[:])
+            x_bank[g, h] = (pt, name, "sorted")
 
         def turned_tile(g):
             if g not in turned:
@@ -160,7 +171,14 @@ def tile_lstmcell_pa_t_w8_kernel(
             pt, name, as_words = x_bank[g, h]
             lo = (GT + h * HT) * PACK
             dst, src = turned_tile(g)[:, lo : lo + HT * PACK], pt[:].bitcast(BF16)
-            if as_words:
+            if as_words == "sorted":
+                nc.vector.tensor_tensor(
+                    out=dst.rearrange("p (c r t) -> p c t r", r=2, t=PACK),
+                    in0=src.rearrange("p (c u r e) -> p c u e r", u=2, r=2, e=2),
+                    in1=s4[:].unsqueeze(1).unsqueeze(3).to_broadcast([P, HT // 2, PACK, 2]),
+                    op=MULT,
+                )
+            elif as_words:
                 nc.vector.tensor_tensor(
                     out=dst.rearrange("p (m u e) -> p m u e", u=2, e=2),
                     in0=src.rearrange("p (u m e) -> p m u e", u=2, e=2),
@@ -179,8 +197,9 @@ def tile_lstmcell_pa_t_w8_kernel(
         def turn_me(g, h):
             stays = h == 0 or g == last
             run = 2 if stays else P
-            if h == 1:
+            if h == 1 or g in (2, last):
                 pt, name = take_bank()
+                lent[g] = name
             else:
                 pt = pkeep.tile([P, GT], F32, name=kept_name(g))
             bank = pt[:].rearrange("p (c u i) -> p u c i", u=2, i=run)
@@ -202,11 +221,13 @@ def tile_lstmcell_pa_t_w8_kernel(
                     out=codes[:, lo : lo + n].bitcast(FP8X4), scales=scales[:, lo : lo + n], in_=turned[g][:, lo * PACK : (lo + n) * PACK]
                 )
 
-        def sigmoids(g):
-            fresh = work.tile([P, PACK, GT], F32, name="sig")
-            sig[g] = fresh
+        def sigmoids(g, planes=range(PACK)):
+            if g not in sig:
+                first = work.tile([P, PACK, GT], F32, name="sig")
+                sig[g] = first
+            fresh = sig[g]
             codes, scales = coded[g]
-            for t in range(PACK):
+            for t in planes:
                 cols = slice(t * P, (t + 1) * P)
                 pm, name = take_bank()
                 nc.tensor.matmul_mx(
@@ -280,7 +301,7 @@ def tile_lstmcell_pa_t_w8_kernel(
         nc.scalar.activation(out=warm[:], in_=zeros[:, 0:1], func=ACT.Sigmoid)
         make_identity(nc, ident[:])
         nc.vector.tensor_copy(out=ident_bf[:], in_=ident[:])
-        idle = pkeep.tile([P, GT], F32, name="spare")
+        idle = pmix.tile([P, GT], F32, name="bank5")
         for i in range(WARM_UPS):
             nc.tensor.matmul(idle[:, i % G * P : (i % G + 1) * P], lhsT=zeros[:], rhs=zeros[:], start=True, stop=True)
 
@@ -321,14 +342,14 @@ def tile_lstmcell_pa_t_w8_kernel(
             turn_me(1, h)
         nc.vector.tensor_copy(out=ws[:].rearrange("p (t m) -> p t m", t=PACK), in_=ws_raw[:].rearrange("p (m t) -> p t m", t=PACK))
         for h, copy in enumerate((nc.gpsimd.tensor_copy, nc.scalar.copy)):
-            wide[2, h] = turned[0][:, GT * PACK + h * HK : GT * PACK + (h + 1) * HK]
-            copy(out=wide[2, h], in_=x_half[2, h].bitcast(FP8))
+            wide[2, h] = widen_sorted(copy, turned[0][:, GT * PACK + h * HK : GT * PACK + (h + 1) * HK], x_half[2, h], False)
         scale_x(1, 0)
         scale_x(1, 1)
         quantise_inputs(1, 2)
         load_words(wt, wt_words)
         load_scale_rows(nc.sync, wts, 0, wt_scales, range(4))
 
+        sigmoids(0, (0,))
         for s in range(2, GROUPS):
             mix, leave = s - 2, s - 4
             if s + 3 < GROUPS:
@@ -337,36 +358,34 @@ def tile_lstmcell_pa_t_w8_kernel(
                 load_me_pair(s + 2)
             shared = 0 <= leave and s < last
             share = WIDE_TOKENS if shared else NARROW_TOKENS if mix > 0 else FIRST_TOKENS
-            sigmoids(mix)
+            sigmoids(mix, (1, 2, 3))
             gate(nc.gpsimd, mix, share, GT, False)
+            if mix > 0:
+                gate(nc.vector, mix, 0, share, True)
+            if mix == 2:
+                free_banks.append(lent[2])
+            turn_x_sorted(s, 0)
+            turn_x_sorted(s, 1)
+            if s < last:
+                widen(s + 1)
             if 0 <= leave:
                 read_out(leave, 0, 2)
                 empty_out(nc.scalar.copy, leave, 0, 2)
-            if leave == 0:
-                read_out(leave, 2, 4, kept_name(s))
-                empty_out(nc.vector.tensor_copy, leave, 2, 4)
-            elif shared:
-                read_out(leave, 2, 4, "spare")
-            elif s == last:
                 read_out(leave, 2, 4)
-                empty_out(nc.scalar.copy, leave, 2, 4)
-            if mix > 0:
-                gate(nc.vector, mix, 0, share, True)
-            turn_x(s, 0)
-            turn_x(s, 1)
-            if s < last:
-                widen(s + 1)
+                if not shared:
+                    empty_out(nc.scalar.copy, leave, 2, 4)
+            sigmoids(mix + 1, (0,))
+            scale_x(s, 0)
             turn_me(s, 1)
             turn_me(s, 0)
-            scale_x(s, 0)
             scale_x(s, 1)
             if mix == 0:
                 gate(nc.vector, mix, 0, share, True)
-            if shared and leave > 0:
+            if shared:
                 empty_out(nc.vector.tensor_copy, leave, 2, 4)
             if 0 <= leave:
                 store(leave, 0, G)
-            quantise_inputs(s, 1 if shared and leave > 0 or mix == 0 else 2)
+            quantise_inputs(s, 1 if shared or mix == 0 else 2)
             quantise_gated(mix, 0, GT)
 
         def leave_by_scalar(g):
@@ -375,9 +394,9 @@ def tile_lstmcell_pa_t_w8_kernel(
                 empty_out(nc.scalar.copy, g, i, i + 2)
                 store(g, i, i + 2)
 
-        sigmoids(last - 1)
+        sigmoids(last - 1, (1, 2, 3))
         gate(nc.gpsimd, last - 1, HT + REST_TOKENS, GT, False)
-        read_out(last - 3, 0, 2, kept_name(last - 2))
+        read_out(last - 3, 0, 2)
         empty_out(nc.vector.tensor_copy, last - 3, 0, 2)
         store(last - 3, 0, 2)
         read_out(last - 3, 2, 4)

@@ -19,19 +19,16 @@ ACT = mybir.ActivationFunctionType
 P = 128
 PACK = 4
 SLABS = TOKENS // P
-G = 4
-GROUPS = SLABS // G
-GT = G * P
-HT = GT // 2
-HK = 2 * K
-ROTATING = 6
-
+BANK = 512
+SIZES = [4] * 16
+FIRST = 196
+SECOND = 212
+NARROW = 184
+T15 = 144
 WIDE_TOKENS = 136
-NARROW_TOKENS = 184
-FIRST_TOKENS = 212
-REST_TOKENS = 80
-LAST_TOKENS = 80
-WARM_UPS = 5
+EXTRA = 0
+WARM_UPS = 4
+PLAIN = 8
 
 
 def tile_lstmcell_pa_t_w8_kernel(
@@ -41,17 +38,19 @@ def tile_lstmcell_pa_t_w8_kernel(
     x_hbm = x_bytes.rearrange("(p i) k -> p i k", i=SLABS)
     me_hbm = me_output.rearrange("(p i) k -> p i k", i=SLABS)
     out_hbm = out.rearrange("(p i) n -> p i n", i=SLABS)
-    last = GROUPS - 1
+    groups = len(SIZES)
+    first = [sum(SIZES[:g]) for g in range(groups)]
+    last = groups - 1
+    toks = [n * P for n in SIZES]
 
     with ExitStack() as ctx:
         keep = ctx.enter_context(tc.tile_pool(name="keep", bufs=1))
         xin = ctx.enter_context(tc.tile_pool(name="xin", bufs=5))
-        mein = ctx.enter_context(tc.tile_pool(name="mein", bufs=4))
+        mein = ctx.enter_context(tc.tile_pool(name="mein", bufs=5))
         work = ctx.enter_context(tc.tile_pool(name="work", bufs=3))
         turnp = ctx.enter_context(tc.tile_pool(name="turnp", bufs=5))
         outp = ctx.enter_context(tc.tile_pool(name="outp", bufs=4))
-        pkeep = ctx.enter_context(tc.psum_pool(name="pkeep", bufs=1))
-        pmix = ctx.enter_context(tc.psum_pool(name="pmix", bufs=1))
+        psum = ctx.enter_context(tc.psum_pool(name="psum", bufs=1))
         ctx.enter_context(tc.manual_schedule())
 
         ident = keep.tile([P, P], F32, name="ident")
@@ -65,200 +64,168 @@ def tile_lstmcell_pa_t_w8_kernel(
         wi = keep.tile([P, CH], U32, name="wi", align_bytes=64)
         wh = keep.tile([P, CH], U32, name="wh", align_bytes=64)
         wt = keep.tile([P, N_OUT], U32, name="wt", align_bytes=64)
-        ws_raw = keep.tile([P, CH], U8, name="ws_raw", align_bytes=64)
+        ws_raw = keep.tile([P, 4, CH], U8, name="ws_raw", align_bytes=64)
         ws = keep.tile([P, CH], U8, name="ws", align_bytes=64)
         wts = keep.tile([P, N_OUT], U8, name="wts", align_bytes=64)
 
-        x_group, x_half, me, wide, x_bank, me_bank, turned, coded = {}, {}, {}, {}, {}, {}, {}, {}
-        sig, gated_coded, res, out_bank, lent = {}, {}, {}, {}, {}
-
-        free_banks = ["bank%d" % i for i in range(ROTATING)]
+        xs, me, wide, x_bank, me_bank, turned, coded = {}, {}, {}, {}, {}, {}, {}
+        sig, gated_coded, res, out_bank, words = {}, {}, {}, {}, {}
+        free_banks = ["bank%d" % i for i in range(8)]
 
         def take_bank():
             name = free_banks.pop(0)
-            return pmix.tile([P, GT], F32, name=name), name
+            return psum.tile([P, BANK], F32, name=name), name
 
-        def kept_name(g):
-            return "kept%d" % ((g if g < 2 else g + 1) % 2)
+        def load_x(g, i0=0, i1=4):
+            t = xin.tile([P, (i1 - i0) * K], U8, name="x%d" % (i1 - i0))
+            nc.sync.dma_start(out=t[:].rearrange("p (i k) -> p i k", k=K), in_=x_hbm[:, first[g] + i0 : first[g] + i1, :])
+            xs[g, i0] = t
 
-        def load_x_half(g, h):
-            t = xin.tile([P, HK], U8, name="x_first")
-            i0 = g * G + 2 * h
-            nc.sync.dma_start(out=t[:].rearrange("p (i k) -> p i k", k=K), in_=x_hbm[:, i0 : i0 + 2, :])
-            x_half[g, h] = t[:]
-
-        def load_x(g):
-            t = xin.tile([P, G * K], U8, name="x_group")
-            nc.sync.dma_start(out=t[:].rearrange("p (i k) -> p i k", k=K), in_=x_hbm[:, g * G : (g + 1) * G, :])
-            x_group[g] = t[:]
-            for h in range(2):
-                x_half[g, h] = t[:, h * HK : (h + 1) * HK]
-
-        def load_me_half(g, h):
-            t = mein.tile([P, HK], BF16, name="me_first")
-            i0 = g * G + 2 * h
-            nc.sync.dma_start(out=t[:].rearrange("p (i k) -> p i k", k=K), in_=me_hbm[:, i0 : i0 + 2, :])
-            me[g, h] = t[:]
-
-        def load_me_pair(g):
-            t = mein.tile([P, 4 * HK], BF16, name="me_pair")
-            nc.sync.dma_start(out=t[:].rearrange("p (i k) -> p i k", k=K), in_=me_hbm[:, g * G : (g + 2) * G, :])
-            for j in range(4):
-                me[g + j // 2, j % 2] = t[:, j * HK : (j + 1) * HK]
+        def load_me(g, i0=0, i1=4):
+            t = mein.tile([P, (i1 - i0) * K], BF16, name="me%d" % (i1 - i0))
+            nc.sync.dma_start(out=t[:].rearrange("p (i k) -> p i k", k=K), in_=me_hbm[:, first[g] + i0 : first[g] + i1, :])
+            for i in range(i0, i1):
+                me[g, i] = t[:, (i - i0) * K : (i - i0 + 1) * K]
 
         def load_words(tile, hbm):
             nc.sync.dma_start(out=tile[:].bitcast(I32), in_=hbm[0].rearrange("p n t -> p (n t)").bitcast(I32))
 
-        def load_scale_rows(queue, tile, row0, hbm, quadrants):
-            for h in quadrants:
-                queue.dma_start(
-                    out=tile[32 * h + row0 : 32 * h + row0 + 4, :].bitcast(I32), in_=hbm[0, 4 * h : 4 * h + 4, :].bitcast(I32)
-                )
-
         def permute_words(copy, dst, src):
             copy(out=dst.rearrange("p (t c i) -> p c t i", t=PACK, i=4), in_=src.rearrange("p (c i t) -> p c t i", t=PACK, i=4))
 
-        def widen_half(g, h):
-            fresh = work.tile([P, HK], BF16, name="wide%d" % h)
-            nc.scalar.copy(out=fresh[:], in_=x_half[g, h].bitcast(FP8))
-            wide[g, h] = fresh[:]
-
-        def widen_sorted(copy, dst, codes, by_read):
-            walk = "p u m e" if by_read else "p m u e"
-            copy(out=dst.rearrange("p (u m e) -> " + walk, u=2, e=2), in_=codes.bitcast(FP8).rearrange("p (m u e) -> " + walk, u=2, e=2))
-            return dst.bitcast(F32).rearrange("p (u m) -> p u m", u=2)
-
-        def widen(g):
-            fresh = work.tile([P, G * K], BF16, name="wide")
-            words = widen_sorted(nc.scalar.copy, fresh[:], x_group[g], g % 3 != 0)
-            for h in range(2):
-                wide[g, h] = words[:, :, h * HT : (h + 1) * HT]
-
-        def turn_x_sorted(g, h):
-            pt, name = take_bank()
-            bank = pt[:].rearrange("p (c u r) -> p u c r", u=2, r=2)
-            for i in range(2):
-                for u in range(2):
-                    nc.tensor.transpose(bank[:, u, 64 * i : 64 * (i + 1), :], wide[g, h][:, u, i * P : (i + 1) * P], ident[:])
-            x_bank[g, h] = (pt, name, "sorted")
+        def widen(g, i0=0, i1=4, by_pool=False):
+            if g not in wide:
+                fresh = work.tile([P, SIZES[g] * K], BF16, name="wide")
+                wide[g] = fresh
+            j0 = max(j for j in range(i0 + 1) if (g, j) in xs)
+            dst, codes = wide[g][:, i0 * K : i1 * K], xs[g, j0][:, (i0 - j0) * K : (i1 - j0) * K].bitcast(FP8)
+            if by_pool:
+                dst = turned[0][:, 1, i0 * K : i1 * K]
+            if g * 4 + i0 < PLAIN:
+                nc.scalar.copy(out=dst, in_=codes)
+            elif by_pool:
+                nc.gpsimd.tensor_copy(out=dst.rearrange("p (u m e) -> p m u e", u=2, e=2), in_=codes.rearrange("p (m u e) -> p m u e", u=2, e=2))
+            else:
+                nc.scalar.copy(out=dst.rearrange("p (u m e) -> p u m e", u=2, e=2), in_=codes.rearrange("p (m u e) -> p u m e", u=2, e=2))
+            if g * 4 + i0 >= PLAIN:
+                for i in range(i0, i1):
+                    words[g, i] = dst.bitcast(F32).rearrange("p (u i m) -> p i u m", u=2, m=P)[:, i - i0, :, :]
 
         def turned_tile(g):
             if g not in turned:
-                fresh = turnp.tile([P, 2 * GT * PACK], BF16, name="turned", align_bytes=64)
+                fresh = turnp.tile([P, 2, toks[g] * PACK], BF16, name="turned", align_bytes=64)
                 turned[g] = fresh
             return turned[g]
 
-        def turn_words(bank, words):
-            for i in range(2):
-                for u in range(2):
-                    nc.tensor.transpose(bank[u][i], words[:, i * HT + u : (i + 1) * HT : 2], ident[:])
-
-        def turn_x(g, h, as_words=False):
+        def turn_x(g, i0, i1):
             pt, name = take_bank()
-            if as_words:
-                bank = pt[:].rearrange("p (u i r) -> p u i r", u=2, i=2)
-                turn_words([[bank[:, u, i, :] for i in range(2)] for u in range(2)], wide[g, h].bitcast(F32))
-            else:
+            if g * 4 + i0 < PLAIN:
                 bank = pt[:].bitcast(BF16).rearrange("p (i c t r) -> p i t c r", i=2, t=PACK, r=2)
-                for i in range(2):
+                for i in range(i0, i1):
                     for t in range(PACK):
                         nc.tensor.matmul(
-                            bank[:, i, t, :, :], lhsT=wide[g, h][:, i * K + t : (i + 1) * K : PACK], rhs=ident_bf[:], start=True, stop=True
+                            bank[:, i - i0, t, :, :], lhsT=wide[g][:, i * K + t : (i + 1) * K : PACK], rhs=ident_bf[:], start=True, stop=True
                         )
-            x_bank[g, h] = (pt, name, as_words)
-
-        def scale_x(g, h):
-            pt, name, as_words = x_bank[g, h]
-            lo = (GT + h * HT) * PACK
-            dst, src = turned_tile(g)[:, lo : lo + HT * PACK], pt[:].bitcast(BF16)
-            if as_words == "sorted":
-                nc.vector.tensor_tensor(
-                    out=dst.rearrange("p (c r t) -> p c t r", r=2, t=PACK),
-                    in0=src.rearrange("p (c u r e) -> p c u e r", u=2, r=2, e=2),
-                    in1=s4[:].unsqueeze(1).unsqueeze(3).to_broadcast([P, HT // 2, PACK, 2]),
-                    op=MULT,
-                )
-            elif as_words:
-                nc.vector.tensor_tensor(
-                    out=dst.rearrange("p (m u e) -> p m u e", u=2, e=2),
-                    in0=src.rearrange("p (u m e) -> p m u e", u=2, e=2),
-                    in1=s4[:].rearrange("p (u e) -> p u e", u=2).unsqueeze(1).to_broadcast([P, HT, 2, 2]),
-                    op=MULT,
-                )
             else:
+                bank = pt[:].rearrange("p (i c u r) -> p i u c r", i=2, u=2, r=2)
+                for i in range(i0, i1):
+                    for u in range(2):
+                        nc.tensor.transpose(bank[:, i - i0, u, :, :], words[g, i][:, u, :], ident[:])
+            x_bank[g, i0] = (pt, name)
+
+        def scale_x(g, i0, i1):
+            pt, name = x_bank[g, i0]
+            n = (i1 - i0) * K
+            dst, src = turned_tile(g)[:, 1, i0 * K : i1 * K], pt[:].bitcast(BF16)[:, 0:n]
+            if g * 4 + i0 < PLAIN:
                 nc.vector.tensor_tensor(
                     out=dst.rearrange("p (c r t) -> p c r t", r=2, t=PACK),
                     in0=src.rearrange("p (c t r) -> p c r t", r=2, t=PACK),
-                    in1=s4[:].unsqueeze(1).unsqueeze(1).to_broadcast([P, HT // 2, 2, PACK]),
+                    in1=s4[:].unsqueeze(1).unsqueeze(1).to_broadcast([P, n // 8, 2, PACK]),
+                    op=MULT,
+                )
+            else:
+                nc.vector.tensor_tensor(
+                    out=dst.rearrange("p (c r t) -> p c t r", r=2, t=PACK),
+                    in0=src.rearrange("p (c u r e) -> p c u e r", u=2, r=2, e=2),
+                    in1=s4[:].unsqueeze(1).unsqueeze(3).to_broadcast([P, n // 8, PACK, 2]),
                     op=MULT,
                 )
             free_banks.append(name)
 
-        def turn_me(g, h):
-            stays = h == 0 or g == last
-            run = 2 if stays else P
-            if h == 1 or g in (2, last):
-                pt, name = take_bank()
-                lent[g] = name
-            else:
-                pt = pkeep.tile([P, GT], F32, name=kept_name(g))
-            bank = pt[:].rearrange("p (c u i) -> p u c i", u=2, i=run)
-            per = P // run
-            turn_words([[bank[:, u, per * i : per * (i + 1), :] for i in range(2)] for u in range(2)], me[g, h].bitcast(F32))
-            dst = turned_tile(g)[:, h * HT * PACK : (h + 1) * HT * PACK].bitcast(F32)
-            nc.scalar.copy(out=dst.rearrange("p (c i u) -> p c i u", i=run, u=2), in_=bank.rearrange("p u c i -> p c i u"))
-            me_bank[g, h] = pt
+        def turn_me(g, i0, i1, stays):
+            pt, name = take_bank()
+            bank = pt[:].rearrange("p (i c u r) -> p i u c r", i=2, u=2, r=2)
+            for i in range(i0, i1):
+                for u in range(2):
+                    nc.tensor.transpose(bank[:, i - i0, u, :, :], me[g, i].bitcast(F32)[:, u::2], ident[:])
+            dst = turned_tile(g)[:, 0, i0 * K : i1 * K].bitcast(F32)
+            nc.scalar.copy(
+                out=dst.rearrange("p (c r u) -> p c r u", r=2, u=2), in_=pt[:, 0 : (i1 - i0) * 2 * P].rearrange("p (c u r) -> p c r u", r=2, u=2)
+            )
+            me_bank[g, i0] = (pt, name)
             if not stays:
                 free_banks.append(name)
 
-        def quantise_inputs(g, pieces):
-            codes = work.tile([P, 2 * GT], U32, name="codes", align_bytes=64)
-            scales = work.tile([P, 2 * GT], U8, name="scales", align_bytes=64)
-            coded[g] = (codes, scales)
-            n = 2 * GT // pieces
-            for lo in range(0, 2 * GT, n):
-                nc.vector.quantize_mx(
-                    out=codes[:, lo : lo + n].bitcast(FP8X4), scales=scales[:, lo : lo + n], in_=turned[g][:, lo * PACK : (lo + n) * PACK]
-                )
-
-        def sigmoids(g, planes=range(PACK)):
-            if g not in sig:
-                first = work.tile([P, PACK, GT], F32, name="sig")
-                sig[g] = first
-            fresh = sig[g]
+        def quantise_inputs(g, parts=None, i0=0, i1=4):
+            if g not in coded:
+                codes = work.tile([P, 2, toks[g]], U32, name="codes", align_bytes=64)
+                scales = work.tile([P, 2, toks[g]], U8, name="scales", align_bytes=64)
+                coded[g] = (codes, scales)
             codes, scales = coded[g]
-            for t in planes:
-                cols = slice(t * P, (t + 1) * P)
+            if parts is None:
+                flat = "p a n -> p (a n)"
+                nc.vector.quantize_mx(out=codes[:].rearrange(flat).bitcast(FP8X4), scales=scales[:].rearrange(flat), in_=turned[g][:].rearrange(flat))
+            else:
+                for a in parts:
+                    nc.vector.quantize_mx(
+                        out=codes[:, a, i0 * P : i1 * P].bitcast(FP8X4), scales=scales[:, a, i0 * P : i1 * P], in_=turned[g][:, a, i0 * K : i1 * K]
+                    )
+
+        def sigmoids(g, b0, b1, i0=0, i1=4):
+            if g not in sig:
+                fresh = work.tile([P, PACK, toks[g]], F32, name="sig")
+                sig[g] = fresh
+            codes, scales = coded[g]
+            per, n, rows = PACK // (i1 - i0), (i1 - i0) * P, slice(i0 * P, i1 * P)
+            for b in range(b0, b1):
                 pm, name = take_bank()
-                nc.tensor.matmul_mx(
-                    out=pm[:], lhsT=wi[:, cols].bitcast(FP8X4), lhsT_scale=ws[:, cols],
-                    rhs=codes[:, GT:].bitcast(FP8X4), rhs_scale=scales[:, GT:], start=True, stop=False,
-                )
-                nc.tensor.matmul_mx(
-                    out=pm[:], lhsT=wh[:, cols].bitcast(FP8X4), lhsT_scale=ws[4:, cols],
-                    rhs=codes[:, 0:GT].bitcast(FP8X4), rhs_scale=scales[:, 0:GT], start=False, stop=True,
-                )
-                nc.scalar.activation(out=fresh[:, t, :], in_=pm[:], func=ACT.Sigmoid, bias=bias[:, t : t + 1])
+                for j in range(per):
+                    cols = slice((b * per + j) * P, (b * per + j + 1) * P)
+                    dst = pm[:, j * n : (j + 1) * n]
+                    nc.tensor.matmul_mx(
+                        out=dst, lhsT=wi[:, cols].bitcast(FP8X4), lhsT_scale=ws[:, cols],
+                        rhs=codes[:, 1, rows].bitcast(FP8X4), rhs_scale=scales[:, 1, rows], start=True, stop=False,
+                    )
+                    nc.tensor.matmul_mx(
+                        out=dst, lhsT=wh[:, cols].bitcast(FP8X4), lhsT_scale=ws[4:, cols],
+                        rhs=codes[:, 0, rows].bitcast(FP8X4), rhs_scale=scales[:, 0, rows], start=False, stop=True,
+                    )
+                for j in range(per):
+                    t = b * per + j
+                    nc.scalar.activation(out=sig[g][:, t, rows], in_=pm[:, j * n : (j + 1) * n], func=ACT.Sigmoid, bias=bias[:, t : t + 1])
                 free_banks.append(name)
 
-        def gated(g, lo, hi):
+        def place(g, lo, hi):
             if g < last:
-                return turned[g + 1][:, (GT + lo) * PACK : (GT + hi) * PACK]
-            if lo < HT:
-                return turned[g - 1][:, lo * PACK : hi * PACK]
-            return turned[g][:, (HT + lo) * PACK : (HT + hi) * PACK]
+                return turned[g + 1][:, 1, lo * PACK : hi * PACK]
+            if lo < 256:
+                return turned[g][:, 1, lo * PACK : hi * PACK]
+            return turned[g - 1][:, 0, lo * PACK : hi * PACK]
 
         def gate(engine, g, lo, hi, from_psum):
+            if hi <= lo:
+                return
             if from_psum:
                 run = 2
-                me_turned = me_bank[g, lo // HT][:].bitcast(BF16)[:, lo % HT * PACK : (lo % HT + hi - lo) * PACK].rearrange(
-                    "p (c u i e) -> p c u e i", u=2, i=run, e=2
-                )
+                i0 = lo // (2 * P) * 2
+                a = (lo - i0 * P) * PACK
+                me_turned = me_bank[g, i0][0][:].bitcast(BF16)[:, a : a + (hi - lo) * PACK].rearrange("p (c u i e) -> p c u e i", u=2, i=run, e=2)
             else:
                 run = 4
-                me_turned = turned[g][:, lo * PACK : hi * PACK].rearrange("p (c i u e) -> p c u e i", i=run, u=2, e=2)
+                me_turned = turned[g][:, 0, lo * PACK : hi * PACK].rearrange("p (c i u e) -> p c u e i", i=run, u=2, e=2)
             engine.tensor_tensor(
-                out=gated(g, lo, hi).rearrange("p (c i u e) -> p c u e i", i=run, u=2, e=2),
+                out=place(g, lo, hi).rearrange("p (c i u e) -> p c u e i", i=run, u=2, e=2),
                 in0=me_turned,
                 in1=sig[g][:, :, lo:hi].rearrange("p (u e) (c i) -> p c u e i", i=run, u=2),
                 op=MULT,
@@ -266,17 +233,17 @@ def tile_lstmcell_pa_t_w8_kernel(
 
         def quantise_gated(g, lo, hi):
             if g not in gated_coded:
-                codes = work.tile([P, GT], U32, name="gated_codes", align_bytes=64)
-                scales = work.tile([P, GT], U8, name="gated_scales", align_bytes=64)
+                codes = work.tile([P, toks[g]], U32, name="gated_codes", align_bytes=64)
+                scales = work.tile([P, toks[g]], U8, name="gated_scales", align_bytes=64)
                 gated_coded[g] = (codes, scales)
             codes, scales = gated_coded[g]
-            nc.vector.quantize_mx(out=codes[:, lo:hi].bitcast(FP8X4), scales=scales[:, lo:hi], in_=gated(g, lo, hi))
+            nc.vector.quantize_mx(out=codes[:, lo:hi].bitcast(FP8X4), scales=scales[:, lo:hi], in_=place(g, lo, hi))
 
-        def read_out(g, i0, i1, bank=None):
+        def read_out(g, i0, i1):
             if g not in res:
-                fresh = outp.tile([P, G, N_OUT], F32, name="res")
+                fresh = outp.tile([P, SIZES[g] * N_OUT], F32, name="res")
                 res[g] = fresh
-            po, name = (pkeep.tile([P, GT], F32, name=bank), None) if bank else take_bank()
+            po, name = take_bank()
             codes, scales = gated_coded[g]
             for i in range(i0, i1):
                 cols = slice(i * P, (i + 1) * P)
@@ -284,137 +251,163 @@ def tile_lstmcell_pa_t_w8_kernel(
                     out=po[:, (i - i0) * N_OUT : (i - i0 + 1) * N_OUT], lhsT=codes[:, cols].bitcast(FP8X4), lhsT_scale=scales[:, cols],
                     rhs=wt[:].bitcast(FP8X4), rhs_scale=wts[:], start=True, stop=True,
                 )
-            out_bank[g, i0] = (po[:, 0 : (i1 - i0) * N_OUT], name)
+            out_bank[g, i0] = (po, name)
 
-        def empty_out(copy, g, i0, i1):
-            src, name = out_bank[g, i0]
-            copy(out=res[g][:, i0:i1, :].rearrange("p i n -> p (i n)"), in_=src)
-            if name:
+        def empty_out(copy, g, i0, lo, hi, done=True):
+            po, name = out_bank[g, i0]
+            if hi > lo:
+                copy(out=res[g][:, i0 * N_OUT + lo : i0 * N_OUT + hi], in_=po[:, lo:hi])
+            if done:
                 free_banks.append(name)
 
         def store(g, i0, i1):
-            nc.sync.dma_start(out=out_hbm[:, g * G + i0 : g * G + i1, :], in_=res[g][:, i0:i1, :])
+            nc.sync.dma_start(
+                out=out_hbm[:, first[g] + i0 : first[g] + i1, :], in_=res[g][:, i0 * N_OUT : i1 * N_OUT].rearrange("p (i n) -> p i n", n=N_OUT)
+            )
 
-        nc.vector.memset(zeros[:], 0.0)
-        nc.vector.memset(ws_raw[:].bitcast(I32), 0)
-        nc.vector.memset(wts[:].bitcast(I32), 0)
+        nc.gpsimd.memset(zeros[:], 0.0)
         nc.scalar.activation(out=warm[:], in_=zeros[:, 0:1], func=ACT.Sigmoid)
+        nc.vector.memset(ws_raw[:].rearrange("p h n -> p (h n)").bitcast(I32), 0)
+        nc.vector.memset(wts[:].bitcast(I32), 0)
         make_identity(nc, ident[:])
         nc.vector.tensor_copy(out=ident_bf[:], in_=ident[:])
-        idle = pmix.tile([P, GT], F32, name="bank5")
+        idle, name = take_bank()
         for i in range(WARM_UPS):
-            nc.tensor.matmul(idle[:, i % G * P : (i % G + 1) * P], lhsT=zeros[:], rhs=zeros[:], start=True, stop=True)
+            nc.tensor.matmul(idle[:, i % 4 * P : (i % 4 + 1) * P], lhsT=zeros[:], rhs=zeros[:], start=True, stop=True)
+        free_banks.append(name)
 
-        load_x_half(0, 0)
-        load_me_half(0, 0)
+        load_x(0, 0, 2)
         nc.sync.dma_start(out=s4[:], in_=x_scale.rearrange("o (p t) -> p (o t)", t=PACK))
-        load_x_half(0, 1)
-        load_me_half(0, 1)
+        load_me(0, 0, 2)
+        load_x(0, 2, 4)
+        for row0, hbm in ((0, wi_scales), (4, wh_scales)):
+            nc.sync.dma_start(out=ws_raw[row0 : row0 + 4, :, :].bitcast(I32), in_=hbm[0].rearrange("(h r) n -> r h n", r=4).bitcast(I32))
         load_x(1)
         load_words(wi_raw, wi_words)
-        load_me_half(1, 0)
         load_words(wh_raw, wh_words)
-        load_scale_rows(nc.sync, ws_raw, 0, wi_scales, range(4))
-        load_scale_rows(nc.gpsimd, ws_raw, 4, wh_scales, range(3))
-        load_scale_rows(nc.sync, ws_raw, 4, wh_scales, (3,))
-        load_me_half(1, 1)
-        nc.sync.dma_start(out=bias[:], in_=mem_bias.rearrange("(p t) -> p t", t=PACK))
+        load_me(0, 2, 4)
         load_x(2)
+        nc.sync.dma_start(out=bias[:], in_=mem_bias.rearrange("(p t) -> p t", t=PACK))
+        load_me(1, 0, 2)
+        load_me(1, 2, 4)
         load_x(3)
-        load_me_pair(2)
+        load_me(2)
+        load_words(wt, wt_words)
+        for h in range(4):
+            nc.sync.dma_start(out=wts[32 * h : 32 * h + 4, :].bitcast(I32), in_=wt_scales[0, 4 * h : 4 * h + 4, :].bitcast(I32))
+        load_me(3)
         load_x(4)
 
-        widen_half(0, 0)
-        widen_half(0, 1)
-        turn_me(0, 0)
-        turn_x(0, 0)
-        turn_x(0, 1, as_words=True)
-        widen_half(1, 0)
-        widen_half(1, 1)
-        turn_me(0, 1)
-        scale_x(0, 0)
-        scale_x(0, 1)
-        permute_words(nc.gpsimd.tensor_copy, wi[:], wi_raw[:])
-        permute_words(nc.scalar.copy, wh[:], wh_raw[:])
-        quantise_inputs(0, 2)
-        for h in range(2):
-            turn_x(1, h)
-            turn_me(1, h)
-        nc.vector.tensor_copy(out=ws[:].rearrange("p (t m) -> p t m", t=PACK), in_=ws_raw[:].rearrange("p (m t) -> p t m", t=PACK))
-        for h, copy in enumerate((nc.gpsimd.tensor_copy, nc.scalar.copy)):
-            wide[2, h] = widen_sorted(copy, turned[0][:, GT * PACK + h * HK : GT * PACK + (h + 1) * HK], x_half[2, h], False)
-        scale_x(1, 0)
-        scale_x(1, 1)
-        quantise_inputs(1, 2)
-        load_words(wt, wt_words)
-        load_scale_rows(nc.sync, wts, 0, wt_scales, range(4))
+        for h in range(1, 4):
+            nc.vector.tensor_copy(out=ws_raw[32 * h : 32 * h + 32, 0, :].bitcast(I32), in_=ws_raw[0:32, h, :].bitcast(I32))
+        nc.gpsimd.tensor_copy(out=ws[:].rearrange("p (t m) -> p t m", t=PACK), in_=ws_raw[:, 0, :].rearrange("p (m t) -> p t m", t=PACK))
+        for i in range(2):
+            widen(0, i, i + 1)
+            turn_x(0, i, i + 1)
+        widen(0, 2, 4)
+        widen(1, 0, 2)
+        turn_me(0, 0, 2, False)
+        turn_x(0, 2, 4)
+        scale_x(0, 0, 1)
+        scale_x(0, 1, 2)
+        permute_words(nc.vector.tensor_copy, wi[:].bitcast(I32), wi_raw[:].bitcast(I32))
+        permute_words(nc.gpsimd.tensor_copy, wh[:], wh_raw[:])
+        widen(1, 2, 4)
+        turn_x(1, 0, 2)
+        turn_me(0, 2, 4, True)
+        turn_x(1, 2, 4)
+        scale_x(0, 2, 4)
+        quantise_inputs(0, (0,), 0, 2)
+        quantise_inputs(0, (1,))
+        widen(2, 0, 2, True)
+        widen(2, 2, 4)
+        turn_me(1, 0, 2, True)
+        scale_x(1, 0, 2)
+        scale_x(1, 2, 4)
+        quantise_inputs(0, (0,), 2, 4)
+        turn_me(1, 2, 4, False)
+        sigmoids(0, 0, 2, 0, 2)
+        turn_x(2, 0, 2)
+        turn_x(2, 2, 4)
+        widen(3)
+        sigmoids(0, 0, 2, 2, 4)
+        quantise_inputs(1, (0, 1))
 
-        sigmoids(0, (0,))
-        for s in range(2, GROUPS):
+        for s in range(2, groups):
             mix, leave = s - 2, s - 4
-            if s + 3 < GROUPS:
+            if s + 3 < groups:
                 load_x(s + 3)
-            if s % 2 == 0 and s + 2 < GROUPS:
-                load_me_pair(s + 2)
-            shared = 0 <= leave and s < last
-            share = WIDE_TOKENS if shared else NARROW_TOKENS if mix > 0 else FIRST_TOKENS
-            sigmoids(mix, (1, 2, 3))
-            gate(nc.gpsimd, mix, share, GT, False)
-            if mix > 0:
-                gate(nc.vector, mix, 0, share, True)
-            if mix == 2:
-                free_banks.append(lent[2])
-            turn_x_sorted(s, 0)
-            turn_x_sorted(s, 1)
-            if s < last:
-                widen(s + 1)
-            if 0 <= leave:
-                read_out(leave, 0, 2)
-                empty_out(nc.scalar.copy, leave, 0, 2)
-                read_out(leave, 2, 4)
-                if not shared:
-                    empty_out(nc.scalar.copy, leave, 2, 4)
-            sigmoids(mix + 1, (0,))
-            scale_x(s, 0)
-            turn_me(s, 1)
-            turn_me(s, 0)
-            scale_x(s, 1)
+            if s + 2 < groups:
+                load_me(s + 2)
+            by_vector = 0 if s == last or leave < 0 else BANK - EXTRA
             if mix == 0:
+                gate(nc.gpsimd, 0, 0, 256, False)
+                gate(nc.gpsimd, 0, 256, 512 - FIRST, False)
+            else:
+                share = SECOND if mix == 1 else NARROW if s == last else WIDE_TOKENS
+                sigmoids(mix, 1, 4)
+                gate(nc.gpsimd, mix, share, 512, False)
+                if mix > 1:
+                    gate(nc.vector, mix, 0, share, True)
+                    free_banks.append(me_bank[mix, 0][1])
+            if s > 2:
+                turn_x(s, 0, 2)
+                turn_x(s, 2, 4)
+            if 2 < s < last:
+                widen(s + 1)
+            if leave >= 0:
+                read_out(leave, 0, 2)
+                read_out(leave, 2, 4)
+                empty_out(nc.scalar.copy, leave, 0, 0, BANK)
+                empty_out(nc.scalar.copy, leave, 2, 0, BANK - by_vector, by_vector == 0)
+            if s > 2:
+                sigmoids(s - 1, 0, 1)
+            scale_x(s, 0, 2)
+            turn_me(s, 2, 4, s == last)
+            turn_me(s, 0, 2, True)
+            scale_x(s, 2, 4)
+            if mix == 0:
+                sigmoids(1, 0, 1)
+                gate(nc.vector, 0, 512 - FIRST, 512, True)
+                free_banks.append(me_bank[0, 2][1])
+            if mix == 1:
                 gate(nc.vector, mix, 0, share, True)
-            if shared:
-                empty_out(nc.vector.tensor_copy, leave, 2, 4)
-            if 0 <= leave:
-                store(leave, 0, G)
-            quantise_inputs(s, 1 if shared or mix == 0 else 2)
-            quantise_gated(mix, 0, GT)
+                free_banks.append(me_bank[mix, 0][1])
+            if by_vector:
+                empty_out(nc.vector.tensor_copy, leave, 2, BANK - by_vector, BANK)
+            if leave >= 0:
+                store(leave, 0, 4)
+            quantise_inputs(s, None if by_vector or mix < 2 else (0, 1))
+            quantise_gated(mix, 0, 512)
 
-        def leave_by_scalar(g):
-            for i in (0, 2):
-                read_out(g, i, i + 2)
-                empty_out(nc.scalar.copy, g, i, i + 2)
-                store(g, i, i + 2)
+        a, b, c = last - 2, last - 1, last
 
-        sigmoids(last - 1, (1, 2, 3))
-        gate(nc.gpsimd, last - 1, HT + REST_TOKENS, GT, False)
-        read_out(last - 3, 0, 2)
-        empty_out(nc.vector.tensor_copy, last - 3, 0, 2)
-        store(last - 3, 0, 2)
-        read_out(last - 3, 2, 4)
-        empty_out(nc.scalar.copy, last - 3, 2, 4)
-        store(last - 3, 2, 4)
-        gate(nc.vector, last - 1, 0, HT, True)
-        sigmoids(last)
-        gate(nc.vector, last - 1, HT, HT + REST_TOKENS, False)
-        quantise_gated(last - 1, 0, HT)
-        quantise_gated(last - 1, HT, GT)
-        leave_by_scalar(last - 2)
-        gate(nc.gpsimd, last, HT, GT - LAST_TOKENS, False)
-        gate(nc.vector, last, 0, HT, True)
-        gate(nc.vector, last, GT - LAST_TOKENS, GT, True)
-        leave_by_scalar(last - 1)
-        for lo, hi in ((0, P), (P, HT), (HT, GT)):
-            quantise_gated(last, lo, hi)
-        for i in range(G):
-            read_out(last, i, i + 1)
-            empty_out(nc.vector.tensor_copy if i % 2 else nc.scalar.copy, last, i, i + 1)
-            store(last, i, i + 1)
+        def leave_half(copy, g, i):
+            read_out(g, i, i + 2)
+            empty_out(copy, g, i, 0, BANK)
+            store(g, i, i + 2)
+
+        sigmoids(b, 1, 4)
+        leave_half(nc.scalar.copy, last - 3, 0)
+        gate(nc.gpsimd, b, 256, 512, False)
+        gate(nc.vector, b, 0, 256, True)
+        free_banks.append(me_bank[b, 0][1])
+        leave_half(nc.vector.tensor_copy, last - 3, 2)
+        sigmoids(c, 0, 2, 0, 2)
+        leave_half(nc.vector.tensor_copy, a, 0)
+        sigmoids(c, 0, 2, 2, 4)
+        leave_half(nc.scalar.copy, a, 2)
+        quantise_gated(b, 0, 256)
+        quantise_gated(b, 256, 512)
+        gate(nc.gpsimd, c, 0, T15, False)
+        gate(nc.vector, c, T15, 256, True)
+        gate(nc.vector, c, 256, 512, True)
+        leave_half(nc.scalar.copy, b, 0)
+        leave_half(nc.scalar.copy, b, 2)
+        for lo, hi in ((0, 256), (256, 384), (384, 512)):
+            quantise_gated(c, lo, hi)
+        leave_half(nc.scalar.copy, c, 0)
+        for i in (2, 3):
+            read_out(c, i, i + 1)
+            empty_out(nc.vector.tensor_copy if i == 2 else nc.scalar.copy, c, i, 0, N_OUT)
+            store(c, i, i + 1)

@@ -25,8 +25,8 @@ FIRST = 196
 SECOND = 212
 NARROW = 184
 T15 = 144
-WIDE_TOKENS = 136
-EXTRA = 0
+WIDE_TOKENS = 144
+EXTRA = 128
 WARM_UPS = 4
 PLAIN = 8
 

@@ -24,7 +24,6 @@ SIZES = [4] * 16
 FIRST = 196
 SECOND = 212
 NARROW = 184
-T15 = 144
 WIDE_TOKENS = 144
 EXTRA = 128
 WARM_UPS = 4
@@ -90,6 +89,16 @@ def tile_lstmcell_pa_t_w8_kernel(
         def load_words(tile, hbm):
             nc.sync.dma_start(out=tile[:].bitcast(I32), in_=hbm[0].rearrange("p n t -> p (n t)").bitcast(I32))
 
+        def load_scale_rows(row0, hbm):
+            nc.sync.dma_start(out=ws_raw[row0 : row0 + 4, :, :].bitcast(I32), in_=hbm[0].rearrange("(h r) n -> r h n", r=4).bitcast(I32))
+
+        def spread_scale_rows():
+            for h in range(1, 4):
+                nc.vector.tensor_copy(out=ws_raw[32 * h : 32 * h + 32, 0, :].bitcast(I32), in_=ws_raw[0:32, h, :].bitcast(I32))
+
+        def permute_scales(copy):
+            copy(out=ws[:].rearrange("p (t m) -> p t m", t=PACK), in_=ws_raw[:, 0, :].rearrange("p (m t) -> p t m", t=PACK))
+
         def permute_words(copy, dst, src):
             copy(out=dst.rearrange("p (t c i) -> p c t i", t=PACK, i=4), in_=src.rearrange("p (c i t) -> p c t i", t=PACK, i=4))
 
@@ -153,17 +162,20 @@ def tile_lstmcell_pa_t_w8_kernel(
                 )
             free_banks.append(name)
 
-        def turn_me(g, i0, i1, stays):
+        def turn_me(g, i0, i1, stays, later=False):
             pt, name = take_bank()
             bank = pt[:].rearrange("p (i c u r) -> p i u c r", i=2, u=2, r=2)
             for i in range(i0, i1):
                 for u in range(2):
                     nc.tensor.transpose(bank[:, i - i0, u, :, :], me[g, i].bitcast(F32)[:, u::2], ident[:])
-            dst = turned_tile(g)[:, 0, i0 * K : i1 * K].bitcast(F32)
-            nc.scalar.copy(
-                out=dst.rearrange("p (c r u) -> p c r u", r=2, u=2), in_=pt[:, 0 : (i1 - i0) * 2 * P].rearrange("p (c u r) -> p c r u", r=2, u=2)
-            )
             me_bank[g, i0] = (pt, name)
+            if not later:
+                empty_me(nc.scalar.copy, g, i0, i1, stays)
+
+        def empty_me(copy, g, i0, i1, stays):
+            pt, name = me_bank[g, i0]
+            dst = turned_tile(g)[:, 0, i0 * K : i1 * K].bitcast(F32)
+            copy(out=dst.rearrange("p (c r u) -> p c r u", r=2, u=2), in_=pt[:].rearrange("p (c u r) -> p c r u", r=2, u=2))
             if not stays:
                 free_banks.append(name)
 
@@ -280,16 +292,16 @@ def tile_lstmcell_pa_t_w8_kernel(
         nc.sync.dma_start(out=s4[:], in_=x_scale.rearrange("o (p t) -> p (o t)", t=PACK))
         load_me(0, 0, 2)
         load_x(0, 2, 4)
-        for row0, hbm in ((0, wi_scales), (4, wh_scales)):
-            nc.sync.dma_start(out=ws_raw[row0 : row0 + 4, :, :].bitcast(I32), in_=hbm[0].rearrange("(h r) n -> r h n", r=4).bitcast(I32))
+        load_scale_rows(0, wi_scales)
+        load_scale_rows(4, wh_scales)
         load_x(1)
         load_words(wi_raw, wi_words)
-        load_words(wh_raw, wh_words)
         load_me(0, 2, 4)
+        load_words(wh_raw, wh_words)
         load_x(2)
-        nc.sync.dma_start(out=bias[:], in_=mem_bias.rearrange("(p t) -> p t", t=PACK))
         load_me(1, 0, 2)
         load_me(1, 2, 4)
+        nc.sync.dma_start(out=bias[:], in_=mem_bias.rearrange("(p t) -> p t", t=PACK))
         load_x(3)
         load_me(2)
         load_words(wt, wt_words)
@@ -298,34 +310,34 @@ def tile_lstmcell_pa_t_w8_kernel(
         load_me(3)
         load_x(4)
 
-        for h in range(1, 4):
-            nc.vector.tensor_copy(out=ws_raw[32 * h : 32 * h + 32, 0, :].bitcast(I32), in_=ws_raw[0:32, h, :].bitcast(I32))
-        nc.gpsimd.tensor_copy(out=ws[:].rearrange("p (t m) -> p t m", t=PACK), in_=ws_raw[:, 0, :].rearrange("p (m t) -> p t m", t=PACK))
         for i in range(2):
             widen(0, i, i + 1)
             turn_x(0, i, i + 1)
         widen(0, 2, 4)
-        widen(1, 0, 2)
         turn_me(0, 0, 2, False)
+        widen(1, 0, 2)
         turn_x(0, 2, 4)
         scale_x(0, 0, 1)
         scale_x(0, 1, 2)
-        permute_words(nc.vector.tensor_copy, wi[:].bitcast(I32), wi_raw[:].bitcast(I32))
-        permute_words(nc.gpsimd.tensor_copy, wh[:], wh_raw[:])
+        spread_scale_rows()
+        permute_scales(nc.gpsimd.tensor_copy)
         widen(1, 2, 4)
+        scale_x(0, 2, 4)
+        permute_words(nc.scalar.copy, wi[:], wi_raw[:])
         turn_x(1, 0, 2)
         turn_me(0, 2, 4, True)
         turn_x(1, 2, 4)
-        scale_x(0, 2, 4)
         quantise_inputs(0, (0,), 0, 2)
         quantise_inputs(0, (1,))
+        permute_words(nc.scalar.copy, wh[:], wh_raw[:])
         widen(2, 0, 2, True)
         widen(2, 2, 4)
         turn_me(1, 0, 2, True)
         scale_x(1, 0, 2)
         scale_x(1, 2, 4)
+        turn_me(1, 2, 4, False, True)
+        empty_me(nc.vector.tensor_copy, 1, 2, 4, False)
         quantise_inputs(0, (0,), 2, 4)
-        turn_me(1, 2, 4, False)
         sigmoids(0, 0, 2, 0, 2)
         turn_x(2, 0, 2)
         turn_x(2, 2, 4)
@@ -358,7 +370,7 @@ def tile_lstmcell_pa_t_w8_kernel(
             if leave >= 0:
                 read_out(leave, 0, 2)
                 read_out(leave, 2, 4)
-                empty_out(nc.scalar.copy, leave, 0, 0, BANK)
+                empty_out(nc.scalar.copy, leave, 0, 0, min(BANK, 2 * BANK - by_vector), by_vector <= BANK)
                 empty_out(nc.scalar.copy, leave, 2, 0, BANK - by_vector, by_vector == 0)
             if s > 2:
                 sigmoids(s - 1, 0, 1)
@@ -373,8 +385,10 @@ def tile_lstmcell_pa_t_w8_kernel(
             if mix == 1:
                 gate(nc.vector, mix, 0, share, True)
                 free_banks.append(me_bank[mix, 0][1])
+            if by_vector > BANK:
+                empty_out(nc.vector.tensor_copy, leave, 0, 2 * BANK - by_vector, BANK)
             if by_vector:
-                empty_out(nc.vector.tensor_copy, leave, 2, BANK - by_vector, BANK)
+                empty_out(nc.vector.tensor_copy, leave, 2, max(0, BANK - by_vector), BANK)
             if leave >= 0:
                 store(leave, 0, 4)
             quantise_inputs(s, None if by_vector or mix < 2 else (0, 1))
@@ -399,15 +413,22 @@ def tile_lstmcell_pa_t_w8_kernel(
         leave_half(nc.scalar.copy, a, 2)
         quantise_gated(b, 0, 256)
         quantise_gated(b, 256, 512)
-        gate(nc.gpsimd, c, 0, T15, False)
-        gate(nc.vector, c, T15, 256, True)
-        gate(nc.vector, c, 256, 512, True)
+        def leave_slab(copy, i):
+            read_out(c, i, i + 1)
+            empty_out(copy, c, i, 0, N_OUT)
+            store(c, i, i + 1)
+
+        gate(nc.gpsimd, c, 0, P, False)
+        gate(nc.vector, c, P, 2 * P, True)
+        gate(nc.vector, c, 2 * P, 3 * P, True)
         leave_half(nc.scalar.copy, b, 0)
         leave_half(nc.scalar.copy, b, 2)
-        for lo, hi in ((0, 256), (256, 384), (384, 512)):
-            quantise_gated(c, lo, hi)
-        leave_half(nc.scalar.copy, c, 0)
-        for i in (2, 3):
-            read_out(c, i, i + 1)
-            empty_out(nc.vector.tensor_copy if i == 2 else nc.scalar.copy, c, i, 0, N_OUT)
-            store(c, i, i + 1)
+        quantise_gated(c, P, 2 * P)
+        quantise_gated(c, 0, P)
+        gate(nc.vector, c, 3 * P, 4 * P, True)
+        quantise_gated(c, 2 * P, 3 * P)
+        quantise_gated(c, 3 * P, 4 * P)
+        leave_slab(nc.scalar.copy, 1)
+        leave_slab(nc.scalar.copy, 0)
+        leave_slab(nc.vector.tensor_copy, 2)
+        leave_slab(nc.scalar.copy, 3)

@@ -24,8 +24,8 @@ SIZES = [4] * 16
 FIRST = 196
 SECOND = 212
 NARROW = 184
-WIDE_TOKENS = 144
-EXTRA = 128
+WIDE_TOKENS = 152
+EXTRA = 192
 WARM_UPS = 4
 PLAIN = 8
 

@@ -19,15 +19,20 @@ ACT = mybir.ActivationFunctionType
 P = 128
 PACK = 4
 SLABS = TOKENS // P
+G = 4
+GROUPS = SLABS // G
+GT = G * P
+HT = GT // 2
 BANK = 512
-SIZES = [4] * 16
-FIRST = 196
-SECOND = 212
-NARROW = 184
-WIDE_TOKENS = 152
-EXTRA = 192
-WARM_UPS = 4
-PLAIN = 8
+BANKS = 8
+ME, X = 0, 1
+PLAIN_SLABS = 8
+
+STEADY_TOKENS = 152
+FIRST_TOKENS = 196
+SECOND_TOKENS = 212
+LATE_TOKENS = 184
+SCALAR_EXTRA = 192
 
 
 def tile_lstmcell_pa_t_w8_kernel(
@@ -37,10 +42,7 @@ def tile_lstmcell_pa_t_w8_kernel(
     x_hbm = x_bytes.rearrange("(p i) k -> p i k", i=SLABS)
     me_hbm = me_output.rearrange("(p i) k -> p i k", i=SLABS)
     out_hbm = out.rearrange("(p i) n -> p i n", i=SLABS)
-    groups = len(SIZES)
-    first = [sum(SIZES[:g]) for g in range(groups)]
-    last = groups - 1
-    toks = [n * P for n in SIZES]
+    last = GROUPS - 1
 
     with ExitStack() as ctx:
         keep = ctx.enter_context(tc.tile_pool(name="keep", bufs=1))
@@ -67,68 +69,66 @@ def tile_lstmcell_pa_t_w8_kernel(
         ws = keep.tile([P, CH], U8, name="ws", align_bytes=64)
         wts = keep.tile([P, N_OUT], U8, name="wts", align_bytes=64)
 
-        xs, me, wide, x_bank, me_bank, turned, coded = {}, {}, {}, {}, {}, {}, {}
-        sig, gated_coded, res, out_bank, words = {}, {}, {}, {}, {}
-        free_banks = ["bank%d" % i for i in range(8)]
+        x_in, me_in, wide, words, x_bank, me_bank, turned, coded = {}, {}, {}, {}, {}, {}, {}, {}
+        sig, gated_coded, res, out_bank = {}, {}, {}, {}
+
+        free_banks = ["bank%d" % i for i in range(BANKS)]
 
         def take_bank():
             name = free_banks.pop(0)
             return psum.tile([P, BANK], F32, name=name), name
 
-        def load_x(g, i0=0, i1=4):
+        def load_x(g, i0=0, i1=G):
             t = xin.tile([P, (i1 - i0) * K], U8, name="x%d" % (i1 - i0))
-            nc.sync.dma_start(out=t[:].rearrange("p (i k) -> p i k", k=K), in_=x_hbm[:, first[g] + i0 : first[g] + i1, :])
-            xs[g, i0] = t
+            nc.sync.dma_start(out=t[:].rearrange("p (i k) -> p i k", k=K), in_=x_hbm[:, g * G + i0 : g * G + i1, :])
+            x_in[g, i0] = t
 
-        def load_me(g, i0=0, i1=4):
+        def load_me(g, i0=0, i1=G):
             t = mein.tile([P, (i1 - i0) * K], BF16, name="me%d" % (i1 - i0))
-            nc.sync.dma_start(out=t[:].rearrange("p (i k) -> p i k", k=K), in_=me_hbm[:, first[g] + i0 : first[g] + i1, :])
+            nc.sync.dma_start(out=t[:].rearrange("p (i k) -> p i k", k=K), in_=me_hbm[:, g * G + i0 : g * G + i1, :])
             for i in range(i0, i1):
-                me[g, i] = t[:, (i - i0) * K : (i - i0 + 1) * K]
+                me_in[g, i] = t[:, (i - i0) * K : (i - i0 + 1) * K]
 
         def load_words(tile, hbm):
             nc.sync.dma_start(out=tile[:].bitcast(I32), in_=hbm[0].rearrange("p n t -> p (n t)").bitcast(I32))
 
-        def load_scale_rows(row0, hbm):
-            nc.sync.dma_start(out=ws_raw[row0 : row0 + 4, :, :].bitcast(I32), in_=hbm[0].rearrange("(h r) n -> r h n", r=4).bitcast(I32))
-
-        def spread_scale_rows():
-            for h in range(1, 4):
-                nc.vector.tensor_copy(out=ws_raw[32 * h : 32 * h + 32, 0, :].bitcast(I32), in_=ws_raw[0:32, h, :].bitcast(I32))
-
-        def permute_scales(copy):
-            copy(out=ws[:].rearrange("p (t m) -> p t m", t=PACK), in_=ws_raw[:, 0, :].rearrange("p (m t) -> p t m", t=PACK))
-
         def permute_words(copy, dst, src):
             copy(out=dst.rearrange("p (t c i) -> p c t i", t=PACK, i=4), in_=src.rearrange("p (c i t) -> p c t i", t=PACK, i=4))
 
-        def widen(g, i0=0, i1=4, by_pool=False):
+        def plain(g, i):
+            return g * G + i < PLAIN_SLABS
+
+        def widen(g, i0=0, i1=G):
             if g not in wide:
-                fresh = work.tile([P, SIZES[g] * K], BF16, name="wide")
+                fresh = work.tile([P, G * K], BF16, name="wide")
                 wide[g] = fresh
-            j0 = max(j for j in range(i0 + 1) if (g, j) in xs)
-            dst, codes = wide[g][:, i0 * K : i1 * K], xs[g, j0][:, (i0 - j0) * K : (i1 - j0) * K].bitcast(FP8)
-            if by_pool:
-                dst = turned[0][:, 1, i0 * K : i1 * K]
-            if g * 4 + i0 < PLAIN:
+            j0 = max(j for j in range(i0 + 1) if (g, j) in x_in)
+            dst, codes = wide[g][:, i0 * K : i1 * K], x_in[g, j0][:, (i0 - j0) * K : (i1 - j0) * K].bitcast(FP8)
+            if plain(g, i0):
                 nc.scalar.copy(out=dst, in_=codes)
-            elif by_pool:
-                nc.gpsimd.tensor_copy(out=dst.rearrange("p (u m e) -> p m u e", u=2, e=2), in_=codes.rearrange("p (m u e) -> p m u e", u=2, e=2))
             else:
                 nc.scalar.copy(out=dst.rearrange("p (u m e) -> p u m e", u=2, e=2), in_=codes.rearrange("p (m u e) -> p u m e", u=2, e=2))
-            if g * 4 + i0 >= PLAIN:
-                for i in range(i0, i1):
-                    words[g, i] = dst.bitcast(F32).rearrange("p (u i m) -> p i u m", u=2, m=P)[:, i - i0, :, :]
+                note_words(g, i0, i1, dst)
+
+        def note_words(g, i0, i1, values):
+            for i in range(i0, i1):
+                words[g, i] = values.bitcast(F32).rearrange("p (u i m) -> p i u m", u=2, m=P)[:, i - i0, :, :]
 
         def turned_tile(g):
             if g not in turned:
-                fresh = turnp.tile([P, 2, toks[g] * PACK], BF16, name="turned", align_bytes=64)
+                fresh = turnp.tile([P, 2, GT * PACK], BF16, name="turned", align_bytes=64)
                 turned[g] = fresh
             return turned[g]
 
+        def turn_words(pt, i0, i1, source):
+            bank = pt[:].rearrange("p (i c u r) -> p i u c r", i=2, u=2, r=2)
+            for i in range(i0, i1):
+                for u in range(2):
+                    nc.tensor.transpose(bank[:, i - i0, u, :, :], source(i, u), ident[:])
+
         def turn_x(g, i0, i1):
             pt, name = take_bank()
-            if g * 4 + i0 < PLAIN:
+            if plain(g, i0):
                 bank = pt[:].bitcast(BF16).rearrange("p (i c t r) -> p i t c r", i=2, t=PACK, r=2)
                 for i in range(i0, i1):
                     for t in range(PACK):
@@ -136,67 +136,61 @@ def tile_lstmcell_pa_t_w8_kernel(
                             bank[:, i - i0, t, :, :], lhsT=wide[g][:, i * K + t : (i + 1) * K : PACK], rhs=ident_bf[:], start=True, stop=True
                         )
             else:
-                bank = pt[:].rearrange("p (i c u r) -> p i u c r", i=2, u=2, r=2)
-                for i in range(i0, i1):
-                    for u in range(2):
-                        nc.tensor.transpose(bank[:, i - i0, u, :, :], words[g, i][:, u, :], ident[:])
+                turn_words(pt, i0, i1, lambda i, u: words[g, i][:, u, :])
             x_bank[g, i0] = (pt, name)
 
         def scale_x(g, i0, i1):
             pt, name = x_bank[g, i0]
-            n = (i1 - i0) * K
-            dst, src = turned_tile(g)[:, 1, i0 * K : i1 * K], pt[:].bitcast(BF16)[:, 0:n]
-            if g * 4 + i0 < PLAIN:
+            pairs = (i1 - i0) * P // 2
+            dst, src = turned_tile(g)[:, X, i0 * K : i1 * K], pt[:].bitcast(BF16)[:, 0 : (i1 - i0) * K]
+            if plain(g, i0):
                 nc.vector.tensor_tensor(
                     out=dst.rearrange("p (c r t) -> p c r t", r=2, t=PACK),
                     in0=src.rearrange("p (c t r) -> p c r t", r=2, t=PACK),
-                    in1=s4[:].unsqueeze(1).unsqueeze(1).to_broadcast([P, n // 8, 2, PACK]),
+                    in1=s4[:].unsqueeze(1).unsqueeze(1).to_broadcast([P, pairs, 2, PACK]),
                     op=MULT,
                 )
             else:
                 nc.vector.tensor_tensor(
                     out=dst.rearrange("p (c r t) -> p c t r", r=2, t=PACK),
                     in0=src.rearrange("p (c u r e) -> p c u e r", u=2, r=2, e=2),
-                    in1=s4[:].unsqueeze(1).unsqueeze(3).to_broadcast([P, n // 8, PACK, 2]),
+                    in1=s4[:].unsqueeze(1).unsqueeze(3).to_broadcast([P, pairs, PACK, 2]),
                     op=MULT,
                 )
             free_banks.append(name)
 
-        def turn_me(g, i0, i1, stays, later=False):
+        def turn_me(g, i0, stays, copy=nc.scalar.copy):
             pt, name = take_bank()
-            bank = pt[:].rearrange("p (i c u r) -> p i u c r", i=2, u=2, r=2)
-            for i in range(i0, i1):
-                for u in range(2):
-                    nc.tensor.transpose(bank[:, i - i0, u, :, :], me[g, i].bitcast(F32)[:, u::2], ident[:])
-            me_bank[g, i0] = (pt, name)
-            if not later:
-                empty_me(nc.scalar.copy, g, i0, i1, stays)
-
-        def empty_me(copy, g, i0, i1, stays):
-            pt, name = me_bank[g, i0]
-            dst = turned_tile(g)[:, 0, i0 * K : i1 * K].bitcast(F32)
+            turn_words(pt, i0, i0 + 2, lambda i, u: me_in[g, i].bitcast(F32)[:, u::2])
+            dst = turned_tile(g)[:, ME, i0 * K : (i0 + 2) * K].bitcast(F32)
             copy(out=dst.rearrange("p (c r u) -> p c r u", r=2, u=2), in_=pt[:].rearrange("p (c u r) -> p c r u", r=2, u=2))
+            me_bank[g, i0] = (pt, name)
             if not stays:
-                free_banks.append(name)
+                release_me(g, i0)
 
-        def quantise_inputs(g, parts=None, i0=0, i1=4):
+        def release_me(g, i0):
+            free_banks.append(me_bank[g, i0][1])
+
+        def codes_of(g):
             if g not in coded:
-                codes = work.tile([P, 2, toks[g]], U32, name="codes", align_bytes=64)
-                scales = work.tile([P, 2, toks[g]], U8, name="scales", align_bytes=64)
+                codes = work.tile([P, 2, GT], U32, name="codes", align_bytes=64)
+                scales = work.tile([P, 2, GT], U8, name="scales", align_bytes=64)
                 coded[g] = (codes, scales)
-            codes, scales = coded[g]
-            if parts is None:
-                flat = "p a n -> p (a n)"
-                nc.vector.quantize_mx(out=codes[:].rearrange(flat).bitcast(FP8X4), scales=scales[:].rearrange(flat), in_=turned[g][:].rearrange(flat))
-            else:
-                for a in parts:
-                    nc.vector.quantize_mx(
-                        out=codes[:, a, i0 * P : i1 * P].bitcast(FP8X4), scales=scales[:, a, i0 * P : i1 * P], in_=turned[g][:, a, i0 * K : i1 * K]
-                    )
+            return coded[g]
 
-        def sigmoids(g, b0, b1, i0=0, i1=4):
+        def quantise_both(g):
+            codes, scales = codes_of(g)
+            flat = "p a n -> p (a n)"
+            nc.vector.quantize_mx(out=codes[:].rearrange(flat).bitcast(FP8X4), scales=scales[:].rearrange(flat), in_=turned[g][:].rearrange(flat))
+
+        def quantise_part(g, part, i0=0, i1=G):
+            codes, scales = codes_of(g)
+            rows = slice(i0 * P, i1 * P)
+            nc.vector.quantize_mx(out=codes[:, part, rows].bitcast(FP8X4), scales=scales[:, part, rows], in_=turned[g][:, part, i0 * K : i1 * K])
+
+        def sigmoids(g, b0, b1, i0=0, i1=G):
             if g not in sig:
-                fresh = work.tile([P, PACK, toks[g]], F32, name="sig")
+                fresh = work.tile([P, PACK, GT], F32, name="sig")
                 sig[g] = fresh
             codes, scales = coded[g]
             per, n, rows = PACK // (i1 - i0), (i1 - i0) * P, slice(i0 * P, i1 * P)
@@ -207,53 +201,52 @@ def tile_lstmcell_pa_t_w8_kernel(
                     dst = pm[:, j * n : (j + 1) * n]
                     nc.tensor.matmul_mx(
                         out=dst, lhsT=wi[:, cols].bitcast(FP8X4), lhsT_scale=ws[:, cols],
-                        rhs=codes[:, 1, rows].bitcast(FP8X4), rhs_scale=scales[:, 1, rows], start=True, stop=False,
+                        rhs=codes[:, X, rows].bitcast(FP8X4), rhs_scale=scales[:, X, rows], start=True, stop=False,
                     )
                     nc.tensor.matmul_mx(
                         out=dst, lhsT=wh[:, cols].bitcast(FP8X4), lhsT_scale=ws[4:, cols],
-                        rhs=codes[:, 0, rows].bitcast(FP8X4), rhs_scale=scales[:, 0, rows], start=False, stop=True,
+                        rhs=codes[:, ME, rows].bitcast(FP8X4), rhs_scale=scales[:, ME, rows], start=False, stop=True,
                     )
                 for j in range(per):
                     t = b * per + j
                     nc.scalar.activation(out=sig[g][:, t, rows], in_=pm[:, j * n : (j + 1) * n], func=ACT.Sigmoid, bias=bias[:, t : t + 1])
                 free_banks.append(name)
 
-        def place(g, lo, hi):
+        def gated(g, lo, hi):
             if g < last:
-                return turned[g + 1][:, 1, lo * PACK : hi * PACK]
-            if lo < 256:
-                return turned[g][:, 1, lo * PACK : hi * PACK]
-            return turned[g - 1][:, 0, lo * PACK : hi * PACK]
+                return turned[g + 1][:, X, lo * PACK : hi * PACK]
+            if lo < HT:
+                return turned[g][:, X, lo * PACK : hi * PACK]
+            return turned[g - 1][:, ME, lo * PACK : hi * PACK]
 
-        def gate(engine, g, lo, hi, from_psum):
-            if hi <= lo:
-                return
-            if from_psum:
-                run = 2
-                i0 = lo // (2 * P) * 2
-                a = (lo - i0 * P) * PACK
-                me_turned = me_bank[g, i0][0][:].bitcast(BF16)[:, a : a + (hi - lo) * PACK].rearrange("p (c u i e) -> p c u e i", u=2, i=run, e=2)
-            else:
-                run = 4
-                me_turned = turned[g][:, 0, lo * PACK : hi * PACK].rearrange("p (c i u e) -> p c u e i", i=run, u=2, e=2)
+        def gate(engine, g, lo, hi, me_turned, run):
             engine.tensor_tensor(
-                out=place(g, lo, hi).rearrange("p (c i u e) -> p c u e i", i=run, u=2, e=2),
+                out=gated(g, lo, hi).rearrange("p (c i u e) -> p c u e i", i=run, u=2, e=2),
                 in0=me_turned,
                 in1=sig[g][:, :, lo:hi].rearrange("p (u e) (c i) -> p c u e i", i=run, u=2),
                 op=MULT,
             )
 
+        def gate_by_vector(g, lo, hi):
+            i0 = lo // HT * 2
+            values = me_bank[g, i0][0][:].bitcast(BF16)[:, (lo - i0 * P) * PACK : (hi - i0 * P) * PACK]
+            gate(nc.vector, g, lo, hi, values.rearrange("p (c u i e) -> p c u e i", u=2, i=2, e=2), 2)
+
+        def gate_by_gpsimd(g, lo, hi):
+            values = turned[g][:, ME, lo * PACK : hi * PACK]
+            gate(nc.gpsimd, g, lo, hi, values.rearrange("p (c i u e) -> p c u e i", i=4, u=2, e=2), 4)
+
         def quantise_gated(g, lo, hi):
             if g not in gated_coded:
-                codes = work.tile([P, toks[g]], U32, name="gated_codes", align_bytes=64)
-                scales = work.tile([P, toks[g]], U8, name="gated_scales", align_bytes=64)
+                codes = work.tile([P, GT], U32, name="gated_codes", align_bytes=64)
+                scales = work.tile([P, GT], U8, name="gated_scales", align_bytes=64)
                 gated_coded[g] = (codes, scales)
             codes, scales = gated_coded[g]
-            nc.vector.quantize_mx(out=codes[:, lo:hi].bitcast(FP8X4), scales=scales[:, lo:hi], in_=place(g, lo, hi))
+            nc.vector.quantize_mx(out=codes[:, lo:hi].bitcast(FP8X4), scales=scales[:, lo:hi], in_=gated(g, lo, hi))
 
         def read_out(g, i0, i1):
             if g not in res:
-                fresh = outp.tile([P, SIZES[g] * N_OUT], F32, name="res")
+                fresh = outp.tile([P, G * N_OUT], F32, name="res")
                 res[g] = fresh
             po, name = take_bank()
             codes, scales = gated_coded[g]
@@ -265,17 +258,20 @@ def tile_lstmcell_pa_t_w8_kernel(
                 )
             out_bank[g, i0] = (po, name)
 
-        def empty_out(copy, g, i0, lo, hi, done=True):
+        def empty_out(copy, g, i0, lo, hi, release=True):
             po, name = out_bank[g, i0]
-            if hi > lo:
-                copy(out=res[g][:, i0 * N_OUT + lo : i0 * N_OUT + hi], in_=po[:, lo:hi])
-            if done:
+            copy(out=res[g][:, i0 * N_OUT + lo : i0 * N_OUT + hi], in_=po[:, lo:hi])
+            if release:
                 free_banks.append(name)
 
         def store(g, i0, i1):
-            nc.sync.dma_start(
-                out=out_hbm[:, first[g] + i0 : first[g] + i1, :], in_=res[g][:, i0 * N_OUT : i1 * N_OUT].rearrange("p (i n) -> p i n", n=N_OUT)
-            )
+            rows = res[g][:, i0 * N_OUT : i1 * N_OUT].rearrange("p (i n) -> p i n", n=N_OUT)
+            nc.sync.dma_start(out=out_hbm[:, g * G + i0 : g * G + i1, :], in_=rows)
+
+        def leave(copy, g, i0, i1):
+            read_out(g, i0, i1)
+            empty_out(copy, g, i0, 0, (i1 - i0) * N_OUT)
+            store(g, i0, i1)
 
         nc.gpsimd.memset(zeros[:], 0.0)
         nc.scalar.activation(out=warm[:], in_=zeros[:, 0:1], func=ACT.Sigmoid)
@@ -283,17 +279,14 @@ def tile_lstmcell_pa_t_w8_kernel(
         nc.vector.memset(wts[:].bitcast(I32), 0)
         make_identity(nc, ident[:])
         nc.vector.tensor_copy(out=ident_bf[:], in_=ident[:])
-        idle, name = take_bank()
-        for i in range(WARM_UPS):
-            nc.tensor.matmul(idle[:, i % 4 * P : (i % 4 + 1) * P], lhsT=zeros[:], rhs=zeros[:], start=True, stop=True)
-        free_banks.append(name)
+        free_banks.append(free_banks.pop(0))
 
         load_x(0, 0, 2)
         nc.sync.dma_start(out=s4[:], in_=x_scale.rearrange("o (p t) -> p (o t)", t=PACK))
         load_me(0, 0, 2)
         load_x(0, 2, 4)
-        load_scale_rows(0, wi_scales)
-        load_scale_rows(4, wh_scales)
+        for row0, hbm in ((0, wi_scales), (4, wh_scales)):
+            nc.sync.dma_start(out=ws_raw[row0 : row0 + 4, :, :].bitcast(I32), in_=hbm[0].rearrange("(h r) n -> r h n", r=4).bitcast(I32))
         load_x(1)
         load_words(wi_raw, wi_words)
         load_me(0, 2, 4)
@@ -314,121 +307,114 @@ def tile_lstmcell_pa_t_w8_kernel(
             widen(0, i, i + 1)
             turn_x(0, i, i + 1)
         widen(0, 2, 4)
-        turn_me(0, 0, 2, False)
+        turn_me(0, 0, False)
         widen(1, 0, 2)
         turn_x(0, 2, 4)
         scale_x(0, 0, 1)
         scale_x(0, 1, 2)
-        spread_scale_rows()
-        permute_scales(nc.gpsimd.tensor_copy)
+        for h in range(1, 4):
+            nc.vector.tensor_copy(out=ws_raw[32 * h : 32 * h + 32, 0, :].bitcast(I32), in_=ws_raw[0:32, h, :].bitcast(I32))
+        nc.gpsimd.tensor_copy(out=ws[:].rearrange("p (t m) -> p t m", t=PACK), in_=ws_raw[:, 0, :].rearrange("p (m t) -> p t m", t=PACK))
         widen(1, 2, 4)
         scale_x(0, 2, 4)
         permute_words(nc.scalar.copy, wi[:], wi_raw[:])
         turn_x(1, 0, 2)
-        turn_me(0, 2, 4, True)
+        turn_me(0, 2, True)
         turn_x(1, 2, 4)
-        quantise_inputs(0, (0,), 0, 2)
-        quantise_inputs(0, (1,))
+        quantise_part(0, ME, 0, 2)
+        quantise_part(0, X)
         permute_words(nc.scalar.copy, wh[:], wh_raw[:])
-        widen(2, 0, 2, True)
+        spent = turned[0][:, X, 0 : 2 * K]
+        nc.gpsimd.tensor_copy(
+            out=spent.rearrange("p (u m e) -> p m u e", u=2, e=2), in_=x_in[2, 0][:, 0 : 2 * K].bitcast(FP8).rearrange("p (m u e) -> p m u e", u=2, e=2)
+        )
+        note_words(2, 0, 2, spent)
         widen(2, 2, 4)
-        turn_me(1, 0, 2, True)
+        turn_me(1, 0, True)
         scale_x(1, 0, 2)
         scale_x(1, 2, 4)
-        turn_me(1, 2, 4, False, True)
-        empty_me(nc.vector.tensor_copy, 1, 2, 4, False)
-        quantise_inputs(0, (0,), 2, 4)
+        turn_me(1, 2, False, nc.vector.tensor_copy)
+        quantise_part(0, ME, 2, 4)
         sigmoids(0, 0, 2, 0, 2)
         turn_x(2, 0, 2)
         turn_x(2, 2, 4)
         widen(3)
         sigmoids(0, 0, 2, 2, 4)
-        quantise_inputs(1, (0, 1))
+        quantise_part(1, ME)
+        quantise_part(1, X)
 
-        for s in range(2, groups):
-            mix, leave = s - 2, s - 4
-            if s + 3 < groups:
+        for s in range(2, GROUPS):
+            mix, done = s - 2, s - 4
+            if s + 3 < GROUPS:
                 load_x(s + 3)
-            if s + 2 < groups:
+            if s + 2 < GROUPS:
                 load_me(s + 2)
-            by_vector = 0 if s == last or leave < 0 else BANK - EXTRA
+            shared = 0 <= done and s < last
             if mix == 0:
-                gate(nc.gpsimd, 0, 0, 256, False)
-                gate(nc.gpsimd, 0, 256, 512 - FIRST, False)
+                gate_by_gpsimd(mix, 0, HT)
+                gate_by_gpsimd(mix, HT, GT - FIRST_TOKENS)
             else:
-                share = SECOND if mix == 1 else NARROW if s == last else WIDE_TOKENS
-                sigmoids(mix, 1, 4)
-                gate(nc.gpsimd, mix, share, 512, False)
+                share = SECOND_TOKENS if mix == 1 else STEADY_TOKENS if shared else LATE_TOKENS
+                sigmoids(mix, 1, PACK)
+                gate_by_gpsimd(mix, share, GT)
                 if mix > 1:
-                    gate(nc.vector, mix, 0, share, True)
-                    free_banks.append(me_bank[mix, 0][1])
-            if s > 2:
+                    gate_by_vector(mix, 0, share)
+                    release_me(mix, 0)
                 turn_x(s, 0, 2)
                 turn_x(s, 2, 4)
-            if 2 < s < last:
-                widen(s + 1)
-            if leave >= 0:
-                read_out(leave, 0, 2)
-                read_out(leave, 2, 4)
-                empty_out(nc.scalar.copy, leave, 0, 0, min(BANK, 2 * BANK - by_vector), by_vector <= BANK)
-                empty_out(nc.scalar.copy, leave, 2, 0, BANK - by_vector, by_vector == 0)
-            if s > 2:
-                sigmoids(s - 1, 0, 1)
+                if s < last:
+                    widen(s + 1)
+                if 0 <= done:
+                    read_out(done, 0, 2)
+                    read_out(done, 2, 4)
+                    empty_out(nc.scalar.copy, done, 0, 0, BANK)
+                    empty_out(nc.scalar.copy, done, 2, 0, SCALAR_EXTRA if shared else BANK, not shared)
+                sigmoids(mix + 1, 0, 1)
             scale_x(s, 0, 2)
-            turn_me(s, 2, 4, s == last)
-            turn_me(s, 0, 2, True)
+            turn_me(s, 2, s == last)
+            turn_me(s, 0, True)
             scale_x(s, 2, 4)
             if mix == 0:
-                sigmoids(1, 0, 1)
-                gate(nc.vector, 0, 512 - FIRST, 512, True)
-                free_banks.append(me_bank[0, 2][1])
+                sigmoids(mix + 1, 0, 1)
+                gate_by_vector(mix, GT - FIRST_TOKENS, GT)
+                release_me(mix, 2)
             if mix == 1:
-                gate(nc.vector, mix, 0, share, True)
-                free_banks.append(me_bank[mix, 0][1])
-            if by_vector > BANK:
-                empty_out(nc.vector.tensor_copy, leave, 0, 2 * BANK - by_vector, BANK)
-            if by_vector:
-                empty_out(nc.vector.tensor_copy, leave, 2, max(0, BANK - by_vector), BANK)
-            if leave >= 0:
-                store(leave, 0, 4)
-            quantise_inputs(s, None if by_vector or mix < 2 else (0, 1))
-            quantise_gated(mix, 0, 512)
+                gate_by_vector(mix, 0, share)
+                release_me(mix, 0)
+            if shared:
+                empty_out(nc.vector.tensor_copy, done, 2, SCALAR_EXTRA, BANK)
+            if 0 <= done:
+                store(done, 0, G)
+            if s < last:
+                quantise_both(s)
+            else:
+                quantise_part(s, ME)
+                quantise_part(s, X)
+            quantise_gated(mix, 0, GT)
 
-        a, b, c = last - 2, last - 1, last
-
-        def leave_half(copy, g, i):
-            read_out(g, i, i + 2)
-            empty_out(copy, g, i, 0, BANK)
-            store(g, i, i + 2)
-
-        sigmoids(b, 1, 4)
-        leave_half(nc.scalar.copy, last - 3, 0)
-        gate(nc.gpsimd, b, 256, 512, False)
-        gate(nc.vector, b, 0, 256, True)
-        free_banks.append(me_bank[b, 0][1])
-        leave_half(nc.vector.tensor_copy, last - 3, 2)
-        sigmoids(c, 0, 2, 0, 2)
-        leave_half(nc.vector.tensor_copy, a, 0)
-        sigmoids(c, 0, 2, 2, 4)
-        leave_half(nc.scalar.copy, a, 2)
-        quantise_gated(b, 0, 256)
-        quantise_gated(b, 256, 512)
-        def leave_slab(copy, i):
-            read_out(c, i, i + 1)
-            empty_out(copy, c, i, 0, N_OUT)
-            store(c, i, i + 1)
-
-        gate(nc.gpsimd, c, 0, P, False)
-        gate(nc.vector, c, P, 2 * P, True)
-        gate(nc.vector, c, 2 * P, 3 * P, True)
-        leave_half(nc.scalar.copy, b, 0)
-        leave_half(nc.scalar.copy, b, 2)
-        quantise_gated(c, P, 2 * P)
-        quantise_gated(c, 0, P)
-        gate(nc.vector, c, 3 * P, 4 * P, True)
-        quantise_gated(c, 2 * P, 3 * P)
-        quantise_gated(c, 3 * P, 4 * P)
-        leave_slab(nc.scalar.copy, 1)
-        leave_slab(nc.scalar.copy, 0)
-        leave_slab(nc.vector.tensor_copy, 2)
-        leave_slab(nc.scalar.copy, 3)
+        sigmoids(last - 1, 1, PACK)
+        leave(nc.scalar.copy, last - 3, 0, 2)
+        gate_by_gpsimd(last - 1, HT, GT)
+        gate_by_vector(last - 1, 0, HT)
+        release_me(last - 1, 0)
+        leave(nc.vector.tensor_copy, last - 3, 2, 4)
+        sigmoids(last, 0, 2, 0, 2)
+        leave(nc.vector.tensor_copy, last - 2, 0, 2)
+        sigmoids(last, 0, 2, 2, 4)
+        leave(nc.scalar.copy, last - 2, 2, 4)
+        quantise_gated(last - 1, 0, HT)
+        quantise_gated(last - 1, HT, GT)
+        gate_by_gpsimd(last, 0, P)
+        gate_by_vector(last, P, 2 * P)
+        gate_by_vector(last, 2 * P, 3 * P)
+        leave(nc.scalar.copy, last - 1, 0, 2)
+        leave(nc.scalar.copy, last - 1, 2, 4)
+        quantise_gated(last, P, 2 * P)
+        quantise_gated(last, 0, P)
+        gate_by_vector(last, 3 * P, GT)
+        quantise_gated(last, 2 * P, 3 * P)
+        quantise_gated(last, 3 * P, GT)
+        leave(nc.scalar.copy, last, 1, 2)
+        leave(nc.scalar.copy, last, 0, 1)
+        leave(nc.vector.tensor_copy, last, 2, 3)
+        leave(nc.scalar.copy, last, 3, 4)

@@ -28,11 +28,11 @@ BANKS = 8
 ME, X = 0, 1
 PLAIN_SLABS = 8
 
-STEADY_TOKENS = 152
+STEADY_TOKENS = 160
 FIRST_TOKENS = 196
 SECOND_TOKENS = 212
 LATE_TOKENS = 184
-SCALAR_EXTRA = 192
+SCALAR_EXTRA = 128
 
 
 def tile_lstmcell_pa_t_w8_kernel(
@@ -56,7 +56,7 @@ def tile_lstmcell_pa_t_w8_kernel(
 
         ident = keep.tile([P, P], F32, name="ident")
         ident_bf = keep.tile([P, P], BF16, name="ident_bf")
-        zeros = keep.tile([P, P], F32, name="zeros")
+        zeros = keep.tile([P, 1], F32, name="zeros")
         warm = keep.tile([P, 1], F32, name="warm")
         s4 = keep.tile([P, PACK], F32, name="s4")
         bias = keep.tile([P, PACK], BF16, name="bias")
@@ -274,12 +274,11 @@ def tile_lstmcell_pa_t_w8_kernel(
             store(g, i0, i1)
 
         nc.gpsimd.memset(zeros[:], 0.0)
-        nc.scalar.activation(out=warm[:], in_=zeros[:, 0:1], func=ACT.Sigmoid)
+        nc.scalar.activation(out=warm[:], in_=zeros[:], func=ACT.Sigmoid)
         nc.vector.memset(ws_raw[:].rearrange("p h n -> p (h n)").bitcast(I32), 0)
         nc.vector.memset(wts[:].bitcast(I32), 0)
         make_identity(nc, ident[:])
         nc.vector.tensor_copy(out=ident_bf[:], in_=ident[:])
-        free_banks.append(free_banks.pop(0))
 
         load_x(0, 0, 2)
         nc.sync.dma_start(out=s4[:], in_=x_scale.rearrange("o (p t) -> p (o t)", t=PACK))

from contextlib import ExitStack

import concourse.mybir as mybir
from concourse.masks import make_identity

TOKENS, K, CH, N_OUT = 8192, 512, 512, 256
FLOPS = 2 * TOKENS * (K * CH + CH * CH + CH * N_OUT)

F32 = mybir.dt.float32
BF16 = mybir.dt.bfloat16
I32 = mybir.dt.int32
U32 = mybir.dt.uint32
U8 = mybir.dt.uint8
FP8 = mybir.dt.float8_e4m3fn
FP8X4 = mybir.dt.float8_e4m3fn_x4
MULT = mybir.AluOpType.mult
ACT = mybir.ActivationFunctionType

P = 128
PACK = 4
SLABS = TOKENS // P
G = 4
GROUPS = SLABS // G
GT = G * P
HT = GT // 2
BANK = 512
BANKS = 8
ME, X = 0, 1
PLAIN_SLABS = 8

STEADY_TOKENS = 160
FIRST_TOKENS = 196
SECOND_TOKENS = 212
LATE_TOKENS = 184
SCALAR_EXTRA = 128


def tile_lstmcell_pa_t_w8_kernel(
    tc, x_bytes, x_scale, me_output, wi_words, wi_scales, wh_words, wh_scales, wt_words, wt_scales, mem_bias, out
):
    nc = tc.nc
    x_hbm = x_bytes.rearrange("(p i) k -> p i k", i=SLABS)
    me_hbm = me_output.rearrange("(p i) k -> p i k", i=SLABS)
    out_hbm = out.rearrange("(p i) n -> p i n", i=SLABS)
    last = GROUPS - 1

    with ExitStack() as ctx:
        keep = ctx.enter_context(tc.tile_pool(name="keep", bufs=1))
        xin = ctx.enter_context(tc.tile_pool(name="xin", bufs=5))
        mein = ctx.enter_context(tc.tile_pool(name="mein", bufs=5))
        work = ctx.enter_context(tc.tile_pool(name="work", bufs=3))
        turnp = ctx.enter_context(tc.tile_pool(name="turnp", bufs=5))
        outp = ctx.enter_context(tc.tile_pool(name="outp", bufs=4))
        psum = ctx.enter_context(tc.psum_pool(name="psum", bufs=1))
        ctx.enter_context(tc.manual_schedule())

        ident = keep.tile([P, P], F32, name="ident")
        ident_bf = keep.tile([P, P], BF16, name="ident_bf")
        zeros = keep.tile([P, 1], F32, name="zeros")
        warm = keep.tile([P, 1], F32, name="warm")
        s4 = keep.tile([P, PACK], F32, name="s4")
        bias = keep.tile([P, PACK], BF16, name="bias")
        wi_raw = keep.tile([P, CH], U32, name="wi_raw", align_bytes=64)
        wh_raw = keep.tile([P, CH], U32, name="wh_raw", align_bytes=64)
        wi = keep.tile([P, CH], U32, name="wi", align_bytes=64)
        wh = keep.tile([P, CH], U32, name="wh", align_bytes=64)
        wt = keep.tile([P, N_OUT], U32, name="wt", align_bytes=64)
        ws_raw = keep.tile([P, 4, CH], U8, name="ws_raw", align_bytes=64)
        ws = keep.tile([P, CH], U8, name="ws", align_bytes=64)
        wts = keep.tile([P, N_OUT], U8, name="wts", align_bytes=64)

        x_in, me_in, wide, words, x_bank, me_bank, turned, coded = {}, {}, {}, {}, {}, {}, {}, {}
        sig, gated_coded, res, out_bank = {}, {}, {}, {}

        free_banks = ["bank%d" % i for i in range(BANKS)]

        def take_bank():
            name = free_banks.pop(0)
            return psum.tile([P, BANK], F32, name=name), name

        def load_x(g, i0=0, i1=G):
            t = xin.tile([P, (i1 - i0) * K], U8, name="x%d" % (i1 - i0))
            nc.sync.dma_start(out=t[:].rearrange("p (i k) -> p i k", k=K), in_=x_hbm[:, g * G + i0 : g * G + i1, :])
            x_in[g, i0] = t

        def load_me(g, i0=0, i1=G):
            t = mein.tile([P, (i1 - i0) * K], BF16, name="me%d" % (i1 - i0))
            nc.sync.dma_start(out=t[:].rearrange("p (i k) -> p i k", k=K), in_=me_hbm[:, g * G + i0 : g * G + i1, :])
            for i in range(i0, i1):
                me_in[g, i] = t[:, (i - i0) * K : (i - i0 + 1) * K]

        def load_words(tile, hbm):
            nc.sync.dma_start(out=tile[:].bitcast(I32), in_=hbm[0].rearrange("p n t -> p (n t)").bitcast(I32))

        def permute_words(copy, dst, src):
            copy(out=dst.rearrange("p (t c i) -> p c t i", t=PACK, i=4), in_=src.rearrange("p (c i t) -> p c t i", t=PACK, i=4))

        def plain(g, i):
            return g * G + i < PLAIN_SLABS

        def widen(g, i0=0, i1=G):
            if g not in wide:
                fresh = work.tile([P, G * K], BF16, name="wide")
                wide[g] = fresh
            j0 = max(j for j in range(i0 + 1) if (g, j) in x_in)
            dst, codes = wide[g][:, i0 * K : i1 * K], x_in[g, j0][:, (i0 - j0) * K : (i1 - j0) * K].bitcast(FP8)
            if plain(g, i0):
                nc.scalar.copy(out=dst, in_=codes)
            else:
                nc.scalar.copy(out=dst.rearrange("p (u m e) -> p u m e", u=2, e=2), in_=codes.rearrange("p (m u e) -> p u m e", u=2, e=2))
                note_words(g, i0, i1, dst)

        def note_words(g, i0, i1, values):
            for i in range(i0, i1):
                words[g, i] = values.bitcast(F32).rearrange("p (u i m) -> p i u m", u=2, m=P)[:, i - i0, :, :]

        def turned_tile(g):
            if g not in turned:
                fresh = turnp.tile([P, 2, GT * PACK], BF16, name="turned", align_bytes=64)
                turned[g] = fresh
            return turned[g]

        def turn_words(pt, i0, i1, source):
            bank = pt[:].rearrange("p (i c u r) -> p i u c r", i=2, u=2, r=2)
            for i in range(i0, i1):
                for u in range(2):
                    nc.tensor.transpose(bank[:, i - i0, u, :, :], source(i, u), ident[:])

        def turn_x(g, i0, i1):
            pt, name = take_bank()
            if plain(g, i0):
                bank = pt[:].bitcast(BF16).rearrange("p (i c t r) -> p i t c r", i=2, t=PACK, r=2)
                for i in range(i0, i1):
                    for t in range(PACK):
                        nc.tensor.matmul(
                            bank[:, i - i0, t, :, :], lhsT=wide[g][:, i * K + t : (i + 1) * K : PACK], rhs=ident_bf[:], start=True, stop=True
                        )
            else:
                turn_words(pt, i0, i1, lambda i, u: words[g, i][:, u, :])
            x_bank[g, i0] = (pt, name)

        def scale_x(g, i0, i1):
            pt, name = x_bank[g, i0]
            pairs = (i1 - i0) * P // 2
            dst, src = turned_tile(g)[:, X, i0 * K : i1 * K], pt[:].bitcast(BF16)[:, 0 : (i1 - i0) * K]
            if plain(g, i0):
                nc.vector.tensor_tensor(
                    out=dst.rearrange("p (c r t) -> p c r t", r=2, t=PACK),
                    in0=src.rearrange("p (c t r) -> p c r t", r=2, t=PACK),
                    in1=s4[:].unsqueeze(1).unsqueeze(1).to_broadcast([P, pairs, 2, PACK]),
                    op=MULT,
                )
            else:
                nc.vector.tensor_tensor(
                    out=dst.rearrange("p (c r t) -> p c t r", r=2, t=PACK),
                    in0=src.rearrange("p (c u r e) -> p c u e r", u=2, r=2, e=2),
                    in1=s4[:].unsqueeze(1).unsqueeze(3).to_broadcast([P, pairs, PACK, 2]),
                    op=MULT,
                )
            free_banks.append(name)

        def turn_me(g, i0, stays, copy=nc.scalar.copy):
            pt, name = take_bank()
            turn_words(pt, i0, i0 + 2, lambda i, u: me_in[g, i].bitcast(F32)[:, u::2])
            dst = turned_tile(g)[:, ME, i0 * K : (i0 + 2) * K].bitcast(F32)
            copy(out=dst.rearrange("p (c r u) -> p c r u", r=2, u=2), in_=pt[:].rearrange("p (c u r) -> p c r u", r=2, u=2))
            me_bank[g, i0] = (pt, name)
            if not stays:
                release_me(g, i0)

        def release_me(g, i0):
            free_banks.append(me_bank[g, i0][1])

        def codes_of(g):
            if g not in coded:
                codes = work.tile([P, 2, GT], U32, name="codes", align_bytes=64)
                scales = work.tile([P, 2, GT], U8, name="scales", align_bytes=64)
                coded[g] = (codes, scales)
            return coded[g]

        def quantise_both(g):
            codes, scales = codes_of(g)
            flat = "p a n -> p (a n)"
            nc.vector.quantize_mx(out=codes[:].rearrange(flat).bitcast(FP8X4), scales=scales[:].rearrange(flat), in_=turned[g][:].rearrange(flat))

        def quantise_part(g, part, i0=0, i1=G):
            codes, scales = codes_of(g)
            rows = slice(i0 * P, i1 * P)
            nc.vector.quantize_mx(out=codes[:, part, rows].bitcast(FP8X4), scales=scales[:, part, rows], in_=turned[g][:, part, i0 * K : i1 * K])

        def sigmoids(g, b0, b1, i0=0, i1=G):
            if g not in sig:
                fresh = work.tile([P, PACK, GT], F32, name="sig")
                sig[g] = fresh
            codes, scales = coded[g]
            per, n, rows = PACK // (i1 - i0), (i1 - i0) * P, slice(i0 * P, i1 * P)
            for b in range(b0, b1):
                pm, name = take_bank()
                for j in range(per):
                    cols = slice((b * per + j) * P, (b * per + j + 1) * P)
                    dst = pm[:, j * n : (j + 1) * n]
                    nc.tensor.matmul_mx(
                        out=dst, lhsT=wi[:, cols].bitcast(FP8X4), lhsT_scale=ws[:, cols],
                        rhs=codes[:, X, rows].bitcast(FP8X4), rhs_scale=scales[:, X, rows], start=True, stop=False,
                    )
                    nc.tensor.matmul_mx(
                        out=dst, lhsT=wh[:, cols].bitcast(FP8X4), lhsT_scale=ws[4:, cols],
                        rhs=codes[:, ME, rows].bitcast(FP8X4), rhs_scale=scales[:, ME, rows], start=False, stop=True,
                    )
                for j in range(per):
                    t = b * per + j
                    nc.scalar.activation(out=sig[g][:, t, rows], in_=pm[:, j * n : (j + 1) * n], func=ACT.Sigmoid, bias=bias[:, t : t + 1])
                free_banks.append(name)

        def gated(g, lo, hi):
            if g < last:
                return turned[g + 1][:, X, lo * PACK : hi * PACK]
            if lo < HT:
                return turned[g][:, X, lo * PACK : hi * PACK]
            return turned[g - 1][:, ME, lo * PACK : hi * PACK]

        def gate(engine, g, lo, hi, me_turned, run):
            engine.tensor_tensor(
                out=gated(g, lo, hi).rearrange("p (c i u e) -> p c u e i", i=run, u=2, e=2),
                in0=me_turned,
                in1=sig[g][:, :, lo:hi].rearrange("p (u e) (c i) -> p c u e i", i=run, u=2),
                op=MULT,
            )

        def gate_by_vector(g, lo, hi):
            i0 = lo // HT * 2
            values = me_bank[g, i0][0][:].bitcast(BF16)[:, (lo - i0 * P) * PACK : (hi - i0 * P) * PACK]
            gate(nc.vector, g, lo, hi, values.rearrange("p (c u i e) -> p c u e i", u=2, i=2, e=2), 2)

        def gate_by_gpsimd(g, lo, hi):
            values = turned[g][:, ME, lo * PACK : hi * PACK]
            gate(nc.gpsimd, g, lo, hi, values.rearrange("p (c i u e) -> p c u e i", i=4, u=2, e=2), 4)

        def quantise_gated(g, lo, hi):
            if g not in gated_coded:
                codes = work.tile([P, GT], U32, name="gated_codes", align_bytes=64)
                scales = work.tile([P, GT], U8, name="gated_scales", align_bytes=64)
                gated_coded[g] = (codes, scales)
            codes, scales = gated_coded[g]
            nc.vector.quantize_mx(out=codes[:, lo:hi].bitcast(FP8X4), scales=scales[:, lo:hi], in_=gated(g, lo, hi))

        def read_out(g, i0, i1):
            if g not in res:
                fresh = outp.tile([P, G * N_OUT], F32, name="res")
                res[g] = fresh
            po, name = take_bank()
            codes, scales = gated_coded[g]
            for i in range(i0, i1):
                cols = slice(i * P, (i + 1) * P)
                nc.tensor.matmul_mx(
                    out=po[:, (i - i0) * N_OUT : (i - i0 + 1) * N_OUT], lhsT=codes[:, cols].bitcast(FP8X4), lhsT_scale=scales[:, cols],
                    rhs=wt[:].bitcast(FP8X4), rhs_scale=wts[:], start=True, stop=True,
                )
            out_bank[g, i0] = (po, name)

        def empty_out(copy, g, i0, lo, hi, release=True):
            po, name = out_bank[g, i0]
            copy(out=res[g][:, i0 * N_OUT + lo : i0 * N_OUT + hi], in_=po[:, lo:hi])
            if release:
                free_banks.append(name)

        def store(g, i0, i1):
            rows = res[g][:, i0 * N_OUT : i1 * N_OUT].rearrange("p (i n) -> p i n", n=N_OUT)
            nc.sync.dma_start(out=out_hbm[:, g * G + i0 : g * G + i1, :], in_=rows)

        def leave(copy, g, i0, i1):
            read_out(g, i0, i1)
            empty_out(copy, g, i0, 0, (i1 - i0) * N_OUT)
            store(g, i0, i1)

        nc.gpsimd.memset(zeros[:], 0.0)
        nc.scalar.activation(out=warm[:], in_=zeros[:], func=ACT.Sigmoid)
        nc.vector.memset(ws_raw[:].rearrange("p h n -> p (h n)").bitcast(I32), 0)
        nc.vector.memset(wts[:].bitcast(I32), 0)
        make_identity(nc, ident[:])
        nc.vector.tensor_copy(out=ident_bf[:], in_=ident[:])

        load_x(0, 0, 2)
        nc.sync.dma_start(out=s4[:], in_=x_scale.rearrange("o (p t) -> p (o t)", t=PACK))
        load_me(0, 0, 2)
        load_x(0, 2, 4)
        for row0, hbm in ((0, wi_scales), (4, wh_scales)):
            nc.sync.dma_start(out=ws_raw[row0 : row0 + 4, :, :].bitcast(I32), in_=hbm[0].rearrange("(h r) n -> r h n", r=4).bitcast(I32))
        load_x(1)
        load_words(wi_raw, wi_words)
        load_me(0, 2, 4)
        load_words(wh_raw, wh_words)
        load_x(2)
        load_me(1, 0, 2)
        load_me(1, 2, 4)
        nc.sync.dma_start(out=bias[:], in_=mem_bias.rearrange("(p t) -> p t", t=PACK))
        load_x(3)
        load_me(2)
        load_words(wt, wt_words)
        for h in range(4):
            nc.sync.dma_start(out=wts[32 * h : 32 * h + 4, :].bitcast(I32), in_=wt_scales[0, 4 * h : 4 * h + 4, :].bitcast(I32))
        load_me(3)
        load_x(4)

        for i in range(2):
            widen(0, i, i + 1)
            turn_x(0, i, i + 1)
        widen(0, 2, 4)
        turn_me(0, 0, False)
        widen(1, 0, 2)
        turn_x(0, 2, 4)
        scale_x(0, 0, 1)
        scale_x(0, 1, 2)
        for h in range(1, 4):
            nc.vector.tensor_copy(out=ws_raw[32 * h : 32 * h + 32, 0, :].bitcast(I32), in_=ws_raw[0:32, h, :].bitcast(I32))
        nc.gpsimd.tensor_copy(out=ws[:].rearrange("p (t m) -> p t m", t=PACK), in_=ws_raw[:, 0, :].rearrange("p (m t) -> p t m", t=PACK))
        widen(1, 2, 4)
        scale_x(0, 2, 4)
        permute_words(nc.scalar.copy, wi[:], wi_raw[:])
        turn_x(1, 0, 2)
        turn_me(0, 2, True)
        turn_x(1, 2, 4)
        quantise_part(0, ME, 0, 2)
        quantise_part(0, X)
        permute_words(nc.scalar.copy, wh[:], wh_raw[:])
        spent = turned[0][:, X, 0 : 2 * K]
        nc.gpsimd.tensor_copy(
            out=spent.rearrange("p (u m e) -> p m u e", u=2, e=2), in_=x_in[2, 0][:, 0 : 2 * K].bitcast(FP8).rearrange("p (m u e) -> p m u e", u=2, e=2)
        )
        note_words(2, 0, 2, spent)
        widen(2, 2, 4)
        turn_me(1, 0, True)
        scale_x(1, 0, 2)
        scale_x(1, 2, 4)
        turn_me(1, 2, False, nc.vector.tensor_copy)
        quantise_part(0, ME, 2, 4)
        sigmoids(0, 0, 2, 0, 2)
        turn_x(2, 0, 2)
        turn_x(2, 2, 4)
        widen(3)
        sigmoids(0, 0, 2, 2, 4)
        quantise_part(1, ME)
        quantise_part(1, X)

        for s in range(2, GROUPS):
            mix, done = s - 2, s - 4
            if s + 3 < GROUPS:
                load_x(s + 3)
            if s + 2 < GROUPS:
                load_me(s + 2)
            shared = 0 <= done and s < last
            if mix == 0:
                gate_by_gpsimd(mix, 0, HT)
                gate_by_gpsimd(mix, HT, GT - FIRST_TOKENS)
            else:
                share = SECOND_TOKENS if mix == 1 else STEADY_TOKENS if shared else LATE_TOKENS
                sigmoids(mix, 1, PACK)
                gate_by_gpsimd(mix, share, GT)
                if mix > 1:
                    gate_by_vector(mix, 0, share)
                    release_me(mix, 0)
                turn_x(s, 0, 2)
                turn_x(s, 2, 4)
                if s < last:
                    widen(s + 1)
                if 0 <= done:
                    read_out(done, 0, 2)
                    read_out(done, 2, 4)
                    empty_out(nc.scalar.copy, done, 0, 0, BANK)
                    empty_out(nc.scalar.copy, done, 2, 0, SCALAR_EXTRA if shared else BANK, not shared)
                sigmoids(mix + 1, 0, 1)
            scale_x(s, 0, 2)
            turn_me(s, 2, s == last)
            turn_me(s, 0, True)
            scale_x(s, 2, 4)
            if mix == 0:
                sigmoids(mix + 1, 0, 1)
                gate_by_vector(mix, GT - FIRST_TOKENS, GT)
                release_me(mix, 2)
            if mix == 1:
                gate_by_vector(mix, 0, share)
                release_me(mix, 0)
            if shared:
                empty_out(nc.vector.tensor_copy, done, 2, SCALAR_EXTRA, BANK)
            if 0 <= done:
                store(done, 0, G)
            if s < last:
                quantise_both(s)
            else:
                quantise_part(s, ME)
                quantise_part(s, X)
            quantise_gated(mix, 0, GT)

        sigmoids(last - 1, 1, PACK)
        leave(nc.scalar.copy, last - 3, 0, 2)
        gate_by_gpsimd(last - 1, HT, GT)
        gate_by_vector(last - 1, 0, HT)
        release_me(last - 1, 0)
        leave(nc.vector.tensor_copy, last - 3, 2, 4)
        sigmoids(last, 0, 2, 0, 2)
        leave(nc.vector.tensor_copy, last - 2, 0, 2)
        sigmoids(last, 0, 2, 2, 4)
        leave(nc.scalar.copy, last - 2, 2, 4)
        quantise_gated(last - 1, 0, HT)
        quantise_gated(last - 1, HT, GT)
        gate_by_gpsimd(last, 0, P)
        gate_by_vector(last, P, 2 * P)
        gate_by_vector(last, 2 * P, 3 * P)
        leave(nc.scalar.copy, last - 1, 0, 2)
        leave(nc.scalar.copy, last - 1, 2, 4)
        quantise_gated(last, P, 2 * P)
        quantise_gated(last, 0, P)
        gate_by_vector(last, 3 * P, GT)
        quantise_gated(last, 2 * P, 3 * P)
        quantise_gated(last, 3 * P, GT)
        leave(nc.scalar.copy, last, 1, 2)
        leave(nc.scalar.copy, last, 0, 1)
        leave(nc.vector.tensor_copy, last, 2, 3)
        leave(nc.scalar.copy, last, 3, 4)
